import numpy as np
import ml_dtypes


def mxq(x, axis, fmt="e4m3"):
    dtype, down = {"e4m3": (ml_dtypes.float8_e4m3fn, 7), "e5m2": (ml_dtypes.float8_e5m2, 14)}[fmt]
    v = np.moveaxis(np.asarray(x, np.float32).astype(ml_dtypes.bfloat16).astype(np.float64), axis, -1)
    blocks = v.reshape(v.shape[:-1] + (-1, 32))
    amax = np.abs(blocks).max(-1, keepdims=True)
    byte = np.maximum(np.where(amax > 0, np.frexp(amax)[1] - 1 + 127, 0) - down, 1)
    scale = np.exp2(byte - 127.0)
    codes = (blocks / scale).astype(np.float32).astype(dtype).astype(np.float64)
    return np.moveaxis((codes * scale).reshape(v.shape), -1, axis)


WIDE = False


def mx_kscale(k):
    if not WIDE:
        return np.ones(k)
    levels = np.array([10, -10, 5, -5, 0])
    a = np.random.permutation(np.resize(levels, k // 512 * 4)).reshape(k // 512, 4)
    idx = np.arange(k)
    return np.exp2(a[idx // 512, idx % 128 // 32])


BF16 = ml_dtypes.bfloat16


def bf(x):
    return np.asarray(x, np.float32).astype(BF16)


def f64(x):
    return np.asarray(x).astype(np.float64)


B, N, HD, ED, F = 1, 32, 256, 512, 1024
TD = HD + HD
MD = TD + ED
EPS = 1e-5


def layer_norm(x, g, b):
    mu = x.mean(-1, keepdims=True)
    var = x.var(-1, keepdims=True)
    return (x - mu) * (1.0 / np.sqrt(var + EPS)) * g + b


def setup_inputs():
    t = mx_kscale(F)
    rx = mx_kscale(MD)[:HD]
    r = np.concatenate([rx, rx, np.ones(ED)])
    return {"hid": bf(np.maximum(np.random.standard_normal((B, N, N, F)), 0.0) * t),
            "x_down": bf(np.random.standard_normal((B, N, HD)) * rx),
            "p_ln": bf(np.random.standard_normal((B, N, N, ED))),
            "W2": bf(np.random.standard_normal((F, MD)) / np.sqrt(F) / t[:, None] * r),
            "b2": bf(0.1 * np.random.standard_normal(MD) * r),
            "Wo": bf(np.random.standard_normal((MD, ED)) / np.sqrt(MD) / r[:, None]),
            "bo": bf(0.1 * np.random.standard_normal(ED)),
            "ln_out_g": bf(1.0 + 0.1 * np.random.standard_normal(ED)),
            "ln_out_b": bf(0.1 * np.random.standard_normal(ED))}


def reference(hid, x_down, p_ln, W2, b2, Wo, bo, ln_out_g, ln_out_b):
    xd, pl = f64(x_down), f64(p_ln)
    edge_bias = np.concatenate([np.broadcast_to(xd[:, :, None, :], (B, N, N, HD)),
                                np.broadcast_to(xd[:, None, :, :], (B, N, N, HD))], axis=-1)
    z_in = np.concatenate([edge_bias, pl], axis=-1)
    m = np.maximum((mxq(f64(hid), 3, "e4m3") @ mxq(f64(W2), 0, "e4m3")) + f64(b2), 0.0)
    z = (mxq(m + z_in, 3, "e4m3") @ mxq(f64(Wo), 0, "e4m3")) + f64(bo)
    return pl + layer_norm(z, f64(ln_out_g), f64(ln_out_b))

@@ -1,0 +1,300 @@
+from contextlib import ExitStack
+
+import concourse.mybir as mybir
+from concourse.masks import make_identity
+
+F32 = mybir.dt.float32
+BF16 = mybir.dt.bfloat16
+U32 = mybir.dt.uint32
+U8 = mybir.dt.uint8
+FP8X4 = mybir.dt.float8_e4m3fn_x4
+ALU = mybir.AluOpType
+ACT = mybir.ActivationFunctionType
+
+P = 128
+NODES = 32
+ROWS = NODES * NODES
+F = 1024
+MD = 1024
+ED = 512
+EPS = 1e-5
+HALF = 512
+FLOPS = 2 * ROWS * F * MD + 2 * ROWS * MD * ED
+
+
+def regroup(engine_copy, dst, src):
+    engine_copy(
+        out=dst.rearrange("p (c i) t -> p c t i", i=4),
+        in_=src.rearrange("p t (c i) -> p c t i", i=4),
+    )
+
+
+def tile_edgeupdaterwrapper_v01_pb_kernel(
+    tc, hid, x_down, p_ln, W2, b2, Wo, bo, ln_out_g, ln_out_b, out
+):
+    nc = tc.nc
+    hid2 = hid.rearrange("b i j k -> (b i j) k")
+    pl2 = p_ln.rearrange("b i j f -> (b i j) f")
+    out2 = out.rearrange("b i j f -> (b i j) f")
+    xd2 = x_down.rearrange("b n f -> (b n) f")
+
+    with ExitStack() as ctx:
+        keep = ctx.enter_context(tc.tile_pool(name="keep", bufs=1))
+        work = ctx.enter_context(tc.tile_pool(name="work", bufs=3))
+        tiny = ctx.enter_context(tc.tile_pool(name="tiny", bufs=4))
+        ps_tr = ctx.enter_context(tc.psum_pool(name="ps_tr", bufs=2))
+        ps_s1 = ctx.enter_context(tc.psum_pool(name="ps_s1", bufs=3))
+        ps_s2 = ctx.enter_context(tc.psum_pool(name="ps_s2", bufs=2))
+        ps_pl = ctx.enter_context(tc.psum_pool(name="ps_pl", bufs=1))
+
+        small = keep.tile([P, P], BF16)
+        vecs = keep.tile([P, 3, ED], BF16)
+        ones_b = keep.tile([P, P], BF16)
+        eps_t = keep.tile([P, 1], F32)
+        nc.vector.memset(small[:], 0.0)
+        nc.vector.memset(vecs[:], 0.0)
+        nc.vector.memset(ones_b[:], 1.0)
+        nc.vector.memset(eps_t[:], EPS)
+        ident_f = keep.tile([P, P], F32)
+        ident_b = keep.tile([P, P], BF16)
+        make_identity(nc, ident_f[:])
+        make_identity(nc, ident_b[:])
+
+        nc.scalar.dma_start(out=small[0:32, :], in_=xd2[:, 0:P])
+        nc.scalar.dma_start(out=small[32:64, :], in_=xd2[:, P : 2 * P])
+        nc.scalar.dma_start(out=small[64:72, :], in_=b2.rearrange("(m p) -> m p", p=P))
+        for c, vec in enumerate((bo, ln_out_g, ln_out_b)):
+            nc.scalar.dma_start(out=vecs[0:1, c, :], in_=vec.rearrange("(o f) -> o f", o=1))
+
+        hid_raw = keep.tile([P, 8, F], BF16)
+        w2_raw = keep.tile([P, 2, 4, MD], BF16)
+        wo_raw = keep.tile([P, 2, 4, ED], BF16)
+        pl_raw = keep.tile([P, 8, ED], BF16)
+
+        def load_w2(g):
+            for u in range(2):
+                k0 = 512 * g + 256 * u
+                nc.sync.dma_start(
+                    out=w2_raw[:, g, 2 * u : 2 * u + 2, :],
+                    in_=W2[k0 : k0 + 256, :].rearrange("(q e) n -> q e n", e=2),
+                )
+
+        def load_hid(h):
+            nc.sync.dma_start(
+                out=hid_raw[:, 4 * h : 4 * h + 4, :],
+                in_=hid2[HALF * h : HALF * (h + 1), :].rearrange("(a p) k -> p a k", p=P),
+            )
+
+        def load_pl(h):
+            nc.sync.dma_start(
+                out=pl_raw[:, 4 * h : 4 * h + 4, :],
+                in_=pl2[HALF * h : HALF * (h + 1), :].rearrange("(a p) f -> p a f", p=P),
+            )
+
+        def load_wo(g):
+            nc.sync.dma_start(
+                out=wo_raw[:, g, :, :],
+                in_=Wo[512 * g : 512 * (g + 1), :].rearrange("(t p) n -> p t n", p=P),
+            )
+
+        load_w2(0)
+        load_hid(0)
+        load_w2(1)
+        load_pl(0)
+        load_hid(1)
+        load_wo(0)
+        load_wo(1)
+        load_pl(1)
+
+        w2_gr = keep.tile([P, 2, MD, 4], BF16, align_bytes=64)
+        w2_codes = keep.tile([P, 2, MD], U32, align_bytes=64)
+        w2_sc = keep.tile([P, 2, MD], U8, align_bytes=64)
+        hid_gr = keep.tile([P, 2, ROWS, 2], F32, align_bytes=64)
+        hid_codes = keep.tile([P, 2, ROWS], U32, align_bytes=64)
+        hid_sc = keep.tile([P, 2, ROWS], U8, align_bytes=64)
+        wo_gr = keep.tile([P, 2, ED, 4], BF16, align_bytes=64)
+        wo_codes = keep.tile([P, 2, ED], U32, align_bytes=64)
+        wo_sc = keep.tile([P, 2, ED], U8, align_bytes=64)
+        s_raw = keep.tile([P, 8, ROWS], BF16)
+        s_gr = keep.tile([P, 2, ROWS, 4], BF16, align_bytes=64)
+        s_codes = keep.tile([P, 2, ROWS], U32, align_bytes=64)
+        s_sc = keep.tile([P, 2, ROWS], U8, align_bytes=64)
+        zb = keep.tile([P, 4, ROWS], F32)
+        hid_gr_b = hid_gr[:].bitcast(BF16)
+
+        def quantise(codes, scales, grouped):
+            nc.vector.quantize_mx(
+                out=codes.bitcast(FP8X4),
+                scales=scales,
+                in_=grouped.rearrange("p n t -> p (n t)"),
+            )
+
+        def prep_w2(g):
+            for nb in range(2):
+                cols = slice(512 * nb, 512 * (nb + 1))
+                regroup(nc.vector.tensor_copy, w2_gr[:, g, cols, :], w2_raw[:, g, :, cols])
+            for nb in range(2):
+                cols = slice(512 * nb, 512 * (nb + 1))
+                quantise(w2_codes[:, g, cols], w2_sc[:, g, cols], w2_gr[:, g, cols, :])
+
+        def prep_wo(g):
+            regroup(nc.scalar.copy, wo_gr[:, g, :, :], wo_raw[:, g, :, :])
+
+        def quant_wo(g):
+            quantise(wo_codes[:, g, :], wo_sc[:, g, :], wo_gr[:, g, :, :])
+
+        def prep_hid(h):
+            for g in range(2):
+                for ap in (2 * h, 2 * h + 1):
+                    xt = ps_tr.tile([P, 2, 2, P], F32, tag="tr", name="xt")
+                    for al in range(2):
+                        words = hid_raw[:, 2 * ap + al, :].bitcast(F32)
+                        for u in range(2):
+                            w0 = 256 * g + 128 * u
+                            nc.tensor.transpose(xt[:, al, u, :], words[:, w0 : w0 + P], ident_f[:])
+                    nc.scalar.copy(
+                        out=hid_gr[:, g, 256 * ap : 256 * (ap + 1), :].rearrange(
+                            "p (a r) u -> p a r u", a=2
+                        ),
+                        in_=xt[:].rearrange("p a u r -> p a r u"),
+                    )
+            rows = slice(HALF * h, HALF * (h + 1))
+            for g in range(2):
+                quantise(hid_codes[:, g, rows], hid_sc[:, g, rows], hid_gr_b[:, g, rows, :])
+
+        smT = keep.tile([P, 72], F32)
+        nb2 = keep.tile([P, 8], F32)
+        xb = keep.tile([P, 4, NODES], F32)
+        bo_bc = keep.tile([P, ED], F32)
+        g_bc = keep.tile([P, ED], F32)
+
+        def prep_small():
+            sm_ps = ps_tr.tile([P, P], BF16, tag="tr", name="sm_ps")
+            nc.tensor.transpose(sm_ps[:], small[:], ident_b[:])
+            nc.vector.tensor_copy(out=smT[:], in_=sm_ps[:, 0:72])
+            nc.vector.tensor_scalar_mul(nb2[:], smT[:, 64:72], -1.0)
+            for m in range(4):
+                x0 = 32 * (m % 2)
+                nc.vector.tensor_scalar_add(
+                    out=xb[:, m, :], in0=smT[:, x0 : x0 + 32], scalar1=smT[:, 64 + m : 65 + m]
+                )
+            for c, dst in enumerate((bo_bc, g_bc)):
+                bc_ps = ps_pl.tile([P, ED], F32, tag="pl", name="bc_ps")
+                nc.tensor.matmul(bc_ps[:], lhsT=ones_b[:], rhs=vecs[:, c, :], start=True, stop=True)
+                nc.scalar.copy(out=dst[:], in_=bc_ps[:])
+
+        def prep_pl(h):
+            for tp in range(2):
+                plT = ps_tr.tile([P, 2, HALF], BF16, tag="tr", name="plT")
+                for tl in range(2):
+                    t = 2 * tp + tl
+                    for al in range(4):
+                        nc.tensor.transpose(
+                            plT[:, tl, P * al : P * (al + 1)],
+                            pl_raw[:, 4 * h + al, P * t : P * (t + 1)],
+                            ident_b[:],
+                        )
+                for tl in range(2):
+                    t = 2 * tp + tl
+                    nc.scalar.activation(
+                        out=zb[:, t, HALF * h : HALF * (h + 1)],
+                        in_=plT[:, tl, :],
+                        func=ACT.Identity,
+                        bias=smT[:, 68 + t : 69 + t],
+                        scale=1.0,
+                    )
+
+        def stage1(h, g2):
+            rows = slice(HALF * h, HALF * (h + 1))
+            for t in range(4):
+                m = 4 * g2 + t
+                acc = ps_s1.tile([P, HALF], F32, tag="s1", name="acc")
+                for g in range(2):
+                    nc.tensor.matmul_mx(
+                        out=acc[:],
+                        lhsT=w2_codes[:, g, P * m : P * (m + 1)].bitcast(FP8X4),
+                        lhsT_scale=w2_sc[:, g, P * m : P * (m + 1)],
+                        rhs=hid_codes[:, g, rows].bitcast(FP8X4),
+                        rhs_scale=hid_sc[:, g, rows],
+                        start=(g == 0),
+                        stop=(g == 1),
+                    )
+                if m < 2:
+                    add = xb[:, m, 16 * h : 16 * (h + 1)].unsqueeze(2).to_broadcast([P, 16, NODES])
+                elif m < 4:
+                    add = xb[:, m, :].unsqueeze(1).to_broadcast([P, 16, NODES])
+                else:
+                    add = zb[:, m - 4, rows].rearrange("p (i j) -> p i j", j=NODES)
+                nc.vector.scalar_tensor_tensor(
+                    out=s_raw[:, m, rows].rearrange("p (i j) -> p i j", j=NODES),
+                    in0=acc[:].rearrange("p (i j) -> p i j", j=NODES),
+                    scalar=nb2[:, m : m + 1],
+                    in1=add,
+                    op0=ALU.max,
+                    op1=ALU.add,
+                )
+            regroup(nc.scalar.copy, s_gr[:, g2, rows, :], s_raw[:, 4 * g2 : 4 * g2 + 4, rows])
+            quantise(s_codes[:, g2, rows], s_sc[:, g2, rows], s_gr[:, g2, rows, :])
+
+        def stage2(a):
+            z = ps_s2.tile([P, ED], F32, tag="s2", name="z")
+            for g2 in range(2):
+                nc.tensor.matmul_mx(
+                    out=z[:],
+                    lhsT=s_codes[:, g2, P * a : P * (a + 1)].bitcast(FP8X4),
+                    lhsT_scale=s_sc[:, g2, P * a : P * (a + 1)],
+                    rhs=wo_codes[:, g2, :].bitcast(FP8X4),
+                    rhs_scale=wo_sc[:, g2, :],
+                    start=(g2 == 0),
+                    stop=(g2 == 1),
+                )
+            plb = ps_pl.tile([P, ED], F32, tag="pl", name="plb")
+            nc.tensor.matmul(plb[:], lhsT=ident_b[:], rhs=pl_raw[:, a, :], start=True, stop=False)
+            nc.tensor.matmul(plb[:], lhsT=ones_b[:], rhs=vecs[:, 2, :], start=False, stop=True)
+
+            u = work.tile([P, ED], F32, name="u")
+            su = tiny.tile([P, 1], F32, name="su")
+            nc.vector.scalar_tensor_tensor(
+                out=u[:], in0=z[:], scalar=1.0, in1=bo_bc[:], op0=ALU.mult, op1=ALU.add,
+                accum_out=su[:],
+            )
+            nmu = tiny.tile([P, 1], F32, name="nmu")
+            nc.vector.tensor_scalar_mul(nmu[:], su[:], -1.0 / ED)
+            sq = work.tile([P, ED], BF16, name="sq")
+            ssq = tiny.tile([P, 1], F32, name="ssq")
+            nc.scalar.activation(
+                out=sq[:], in_=u[:], func=ACT.Square, bias=nmu[:], scale=1.0, accum_out=ssq[:]
+            )
+            std = tiny.tile([P, 1], F32, name="std")
+            nc.scalar.activation(out=std[:], in_=ssq[:], func=ACT.Sqrt, bias=eps_t[:], scale=1.0 / ED)
+            rstd = tiny.tile([P, 1], F32, name="rstd")
+            nc.vector.reciprocal(rstd[:], std[:])
+            t1 = work.tile([P, ED], F32, name="t1")
+            nc.vector.scalar_tensor_tensor(
+                out=t1[:], in0=u[:], scalar=nmu[:], in1=g_bc[:], op0=ALU.add, op1=ALU.mult
+            )
+            o = work.tile([P, ED], F32, name="o")
+            nc.vector.scalar_tensor_tensor(
+                out=o[:], in0=t1[:], scalar=rstd[:], in1=plb[:], op0=ALU.mult, op1=ALU.add
+            )
+            nc.sync.dma_start(out=out2[P * a : P * (a + 1), :], in_=o[:])
+
+        prep_w2(0)
+        prep_small()
+        prep_hid(0)
+        prep_w2(1)
+        prep_pl(0)
+        stage1(0, 0)
+        stage1(0, 1)
+        prep_hid(1)
+        prep_wo(0)
+        prep_wo(1)
+        quant_wo(0)
+        quant_wo(1)
+        prep_pl(1)
+        stage1(1, 0)
+        for a in range(4):
+            stage2(a)
+        stage1(1, 1)
+        for a in range(4, 8):
+            stage2(a)

@@ -21,12 +21,40 @@ EPS = 1e-5
 HALF = 512
 FLOPS = 2 * ROWS * F * MD + 2 * ROWS * MD * ED
 
-
-def regroup(engine_copy, dst, src):
-    engine_copy(
-        out=dst.rearrange("p (c i) t -> p c t i", i=4),
-        in_=src.rearrange("p t (c i) -> p c t i", i=4),
-    )
+PSUM_BUFS = {"A": 2, "s1": 4, "pl": 2}
+ORDER = [
+    ("init",), ("SM",), ("W2", 0, 0), ("W2", 0, 1), ("HID", 0), ("HID", 1),
+    ("W2", 1, 0), ("W2", 1, 1), ("HID", 2), ("HID", 3), ("PL", 0), ("PL", 1),
+    ("WO", 0), ("WO", 1), ("Tsm",), ("smT",), ("BC", 0), ("bc", 0),
+    ("BC", 1), ("bc", 1), ("R", 0, 0, "V"), ("R", 0, 1, "V"), ("Qw", 0), ("xb",),
+    ("TH", 0, 0, 0), ("EH", 0, 0, 0, "S"), ("TH", 0, 1, 0), ("EH", 0, 1, 0, "S"), ("TH", 0, 0, 1), ("EH", 0, 0, 1, "S"),
+    ("TH", 0, 1, 1), ("EH", 0, 1, 1, "S"), ("Qh", 0), ("R", 1, 0, "S"), ("R", 1, 1, "V"), ("S1", 0, 0),
+    ("G", 0, 0), ("S1", 0, 1), ("G", 0, 1), ("S1", 0, 2), ("G", 0, 2), ("S1", 0, 3),
+    ("G", 0, 3), ("TH", 1, 0, 0), ("EH", 1, 0, 0, "S"), ("TH", 1, 1, 0), ("EH", 1, 1, 0, "S"), ("TH", 1, 0, 1),
+    ("EH", 1, 0, 1, "S"), ("TH", 1, 1, 1), ("EH", 1, 1, 1, "S"), ("Qw", 1), ("Qh", 1), ("H", 0, 0, "G"),
+    ("TP", 0, 0), ("EP", 0, 0), ("EP", 0, 1), ("TP", 0, 1), ("EP", 0, 2), ("EP", 0, 3),
+    ("RWo", 0, "G"), ("RWo", 1, "G"), ("S1", 0, 4), ("G", 0, 4), ("S1", 0, 5), ("G", 0, 5),
+    ("S1", 0, 6), ("G", 0, 6), ("S1", 0, 7), ("G", 0, 7), ("Qs", 0, 0), ("H", 0, 1, "S"),
+    ("TP", 1, 0), ("EP", 1, 0), ("EP", 1, 1), ("TP", 1, 1), ("EP", 1, 2), ("EP", 1, 3),
+    ("S1", 1, 0), ("G", 1, 0), ("S1", 1, 1), ("G", 1, 1), ("S1", 1, 2), ("G", 1, 2),
+    ("S1", 1, 3), ("G", 1, 3), ("Qs", 0, 1), ("H", 1, 0, "S"), ("S1", 1, 4), ("G", 1, 4),
+    ("S1", 1, 5), ("G", 1, 5), ("S1", 1, 6), ("G", 1, 6), ("S1", 1, 7), ("G", 1, 7),
+    ("Qwo",), ("H", 1, 1, "G"), ("S2", 0), ("J1", 0), ("n", 0), ("JS", 0),
+    ("rs", 0), ("nrS", 0), ("Jy", 0), ("GM", 0), ("S2", 1), ("J1", 1),
+    ("n", 1), ("JS", 1), ("rs", 1), ("nrS", 1), ("Jy", 1), ("GM", 1),
+    ("Qs", 1, 0), ("S2", 2), ("J1", 2), ("n", 2), ("JS", 2), ("rs", 2),
+    ("nrS", 2), ("Jy", 2), ("GM", 2), ("Qs", 1, 1), ("PLB", 0), ("J3g", 0),
+    ("ST", 0), ("S2", 3), ("J1", 3), ("n", 3), ("JS", 3), ("rs", 3),
+    ("nrS", 3), ("Jy", 3), ("GM", 3), ("PLB", 1), ("J3g", 1), ("ST", 1),
+    ("S2", 4), ("J1", 4), ("n", 4), ("JS", 4), ("rs", 4), ("nrS", 4),
+    ("Jy", 4), ("GM", 4), ("PLB", 2), ("J3g", 2), ("ST", 2), ("S2", 5),
+    ("J1", 5), ("n", 5), ("JS", 5), ("rs", 5), ("nrS", 5), ("Jy", 5),
+    ("GM", 5), ("PLB", 3), ("J3g", 3), ("ST", 3), ("S2", 6), ("J1", 6),
+    ("n", 6), ("JS", 6), ("rs", 6), ("nrS", 6), ("Jy", 6), ("GM", 6),
+    ("PLB", 4), ("J3g", 4), ("ST", 4), ("S2", 7), ("J1", 7), ("n", 7),
+    ("JS", 7), ("rs", 7), ("J2", 7), ("PLB", 7), ("J3", 7), ("ST", 7),
+    ("PLB", 5), ("J3g", 5), ("ST", 5), ("PLB", 6), ("J3g", 6), ("ST", 6),
+]
 
 
 def tile_edgeupdaterwrapper_v01_pb_kernel(
@@ -40,261 +68,340 @@ def tile_edgeupdaterwrapper_v01_pb_kernel(
 
     with ExitStack() as ctx:
         keep = ctx.enter_context(tc.tile_pool(name="keep", bufs=1))
-        work = ctx.enter_context(tc.tile_pool(name="work", bufs=3))
-        tiny = ctx.enter_context(tc.tile_pool(name="tiny", bufs=4))
-        ps_tr = ctx.enter_context(tc.psum_pool(name="ps_tr", bufs=2))
-        ps_s1 = ctx.enter_context(tc.psum_pool(name="ps_s1", bufs=3))
-        ps_s2 = ctx.enter_context(tc.psum_pool(name="ps_s2", bufs=2))
-        ps_pl = ctx.enter_context(tc.psum_pool(name="ps_pl", bufs=1))
+        work = ctx.enter_context(tc.tile_pool(name="work", bufs=1))
+        psum = ctx.enter_context(tc.psum_pool(name="psum", bufs=1))
 
         small = keep.tile([P, P], BF16)
         vecs = keep.tile([P, 3, ED], BF16)
         ones_b = keep.tile([P, P], BF16)
         eps_t = keep.tile([P, 1], F32)
-        nc.vector.memset(small[:], 0.0)
-        nc.vector.memset(vecs[:], 0.0)
-        nc.vector.memset(ones_b[:], 1.0)
-        nc.vector.memset(eps_t[:], EPS)
+        warm = keep.tile([P, 1], F32)
         ident_f = keep.tile([P, P], F32)
         ident_b = keep.tile([P, P], BF16)
-        make_identity(nc, ident_f[:])
-        make_identity(nc, ident_b[:])
-
-        nc.scalar.dma_start(out=small[0:32, :], in_=xd2[:, 0:P])
-        nc.scalar.dma_start(out=small[32:64, :], in_=xd2[:, P : 2 * P])
-        nc.scalar.dma_start(out=small[64:72, :], in_=b2.rearrange("(m p) -> m p", p=P))
-        for c, vec in enumerate((bo, ln_out_g, ln_out_b)):
-            nc.scalar.dma_start(out=vecs[0:1, c, :], in_=vec.rearrange("(o f) -> o f", o=1))
-
         hid_raw = keep.tile([P, 8, F], BF16)
-        w2_raw = keep.tile([P, 2, 4, MD], BF16)
+        w2_raw = keep.tile([P, 2, 2, 4, HALF], BF16)
         wo_raw = keep.tile([P, 2, 4, ED], BF16)
         pl_raw = keep.tile([P, 8, ED], BF16)
-
-        def load_w2(g):
-            for u in range(2):
-                k0 = 512 * g + 256 * u
-                nc.sync.dma_start(
-                    out=w2_raw[:, g, 2 * u : 2 * u + 2, :],
-                    in_=W2[k0 : k0 + 256, :].rearrange("(q e) n -> q e n", e=2),
-                )
-
-        def load_hid(h):
-            nc.sync.dma_start(
-                out=hid_raw[:, 4 * h : 4 * h + 4, :],
-                in_=hid2[HALF * h : HALF * (h + 1), :].rearrange("(a p) k -> p a k", p=P),
-            )
-
-        def load_pl(h):
-            nc.sync.dma_start(
-                out=pl_raw[:, 4 * h : 4 * h + 4, :],
-                in_=pl2[HALF * h : HALF * (h + 1), :].rearrange("(a p) f -> p a f", p=P),
-            )
-
-        def load_wo(g):
-            nc.sync.dma_start(
-                out=wo_raw[:, g, :, :],
-                in_=Wo[512 * g : 512 * (g + 1), :].rearrange("(t p) n -> p t n", p=P),
-            )
-
-        load_w2(0)
-        load_hid(0)
-        load_w2(1)
-        load_pl(0)
-        load_hid(1)
-        load_wo(0)
-        load_wo(1)
-        load_pl(1)
-
-        w2_gr = keep.tile([P, 2, MD, 4], BF16, align_bytes=64)
-        w2_codes = keep.tile([P, 2, MD], U32, align_bytes=64)
-        w2_sc = keep.tile([P, 2, MD], U8, align_bytes=64)
-        hid_gr = keep.tile([P, 2, ROWS, 2], F32, align_bytes=64)
-        hid_codes = keep.tile([P, 2, ROWS], U32, align_bytes=64)
-        hid_sc = keep.tile([P, 2, ROWS], U8, align_bytes=64)
+        w2_gr = keep.tile([P, 2, 2, HALF, 4], BF16, align_bytes=64)
+        w2_codes = keep.tile([P, 2, 2, HALF], U32, align_bytes=64)
+        w2_sc = keep.tile([P, 2, 2, HALF], U8, align_bytes=64)
+        hid_gr = keep.tile([P, 2, 2, HALF, 2], F32, align_bytes=64)
+        hid_codes = keep.tile([P, 2, 2, HALF], U32, align_bytes=64)
+        hid_sc = keep.tile([P, 2, 2, HALF], U8, align_bytes=64)
         wo_gr = keep.tile([P, 2, ED, 4], BF16, align_bytes=64)
         wo_codes = keep.tile([P, 2, ED], U32, align_bytes=64)
         wo_sc = keep.tile([P, 2, ED], U8, align_bytes=64)
-        s_raw = keep.tile([P, 8, ROWS], BF16)
-        s_gr = keep.tile([P, 2, ROWS, 4], BF16, align_bytes=64)
-        s_codes = keep.tile([P, 2, ROWS], U32, align_bytes=64)
-        s_sc = keep.tile([P, 2, ROWS], U8, align_bytes=64)
-        zb = keep.tile([P, 4, ROWS], F32)
-        hid_gr_b = hid_gr[:].bitcast(BF16)
-
-        def quantise(codes, scales, grouped):
-            nc.vector.quantize_mx(
-                out=codes.bitcast(FP8X4),
-                scales=scales,
-                in_=grouped.rearrange("p n t -> p (n t)"),
-            )
-
-        def prep_w2(g):
-            for nb in range(2):
-                cols = slice(512 * nb, 512 * (nb + 1))
-                regroup(nc.vector.tensor_copy, w2_gr[:, g, cols, :], w2_raw[:, g, :, cols])
-            for nb in range(2):
-                cols = slice(512 * nb, 512 * (nb + 1))
-                quantise(w2_codes[:, g, cols], w2_sc[:, g, cols], w2_gr[:, g, cols, :])
-
-        def prep_wo(g):
-            regroup(nc.scalar.copy, wo_gr[:, g, :, :], wo_raw[:, g, :, :])
-
-        def quant_wo(g):
-            quantise(wo_codes[:, g, :], wo_sc[:, g, :], wo_gr[:, g, :, :])
-
-        def prep_hid(h):
-            for g in range(2):
-                for ap in (2 * h, 2 * h + 1):
-                    xt = ps_tr.tile([P, 2, 2, P], F32, tag="tr", name="xt")
-                    for al in range(2):
-                        words = hid_raw[:, 2 * ap + al, :].bitcast(F32)
-                        for u in range(2):
-                            w0 = 256 * g + 128 * u
-                            nc.tensor.transpose(xt[:, al, u, :], words[:, w0 : w0 + P], ident_f[:])
-                    nc.scalar.copy(
-                        out=hid_gr[:, g, 256 * ap : 256 * (ap + 1), :].rearrange(
-                            "p (a r) u -> p a r u", a=2
-                        ),
-                        in_=xt[:].rearrange("p a u r -> p a r u"),
-                    )
-            rows = slice(HALF * h, HALF * (h + 1))
-            for g in range(2):
-                quantise(hid_codes[:, g, rows], hid_sc[:, g, rows], hid_gr_b[:, g, rows, :])
-
+        s_raw = keep.tile([P, 2, 2, 4, HALF], BF16)
+        s_gr = keep.tile([P, 2, 2, HALF, 4], BF16, align_bytes=64)
+        s_codes = keep.tile([P, 2, 2, HALF], U32, align_bytes=64)
+        s_sc = keep.tile([P, 2, 2, HALF], U8, align_bytes=64)
+        zb = keep.tile([P, 2, 4, HALF], F32)
         smT = keep.tile([P, 72], F32)
         nb2 = keep.tile([P, 8], F32)
         xb = keep.tile([P, 4, NODES], F32)
         bo_bc = keep.tile([P, ED], F32)
         g_bc = keep.tile([P, ED], F32)
+        hid_gr_b = hid_gr[:].bitcast(BF16)
+        live = {}
 
-        def prep_small():
-            sm_ps = ps_tr.tile([P, P], BF16, tag="tr", name="sm_ps")
-            nc.tensor.transpose(sm_ps[:], small[:], ident_b[:])
-            nc.vector.tensor_copy(out=smT[:], in_=sm_ps[:, 0:72])
+        def bank(key, tag, shape, dtype):
+            t = psum.tile(shape, dtype, tag=tag, bufs=PSUM_BUFS[tag], name="ps_%s" % tag)
+            live[key] = t
+            return t
+
+        def wtile(key, tag, bufs, shape, dtype):
+            t = work.tile(shape, dtype, tag=tag, bufs=bufs, name="w_%s" % tag)
+            live[key] = t
+            return t
+
+        def copy_on(eng, dst, src):
+            if eng == "V":
+                nc.vector.tensor_copy(out=dst, in_=src)
+            elif eng == "S":
+                nc.scalar.copy(out=dst, in_=src)
+            else:
+                nc.gpsimd.tensor_scalar(out=dst, in0=src, scalar1=1.0, scalar2=0.0, op0=ALU.mult, op1=ALU.add)
+
+        def regroup(eng, dst, src):
+            copy_on(
+                eng,
+                dst.rearrange("p (c i) t -> p c t i", i=4),
+                src.rearrange("p t (c i) -> p c t i", i=4),
+            )
+
+        def quantise(codes, scales, grouped):
+            nc.vector.quantize_mx(out=codes.bitcast(FP8X4), scales=scales, in_=grouped)
+
+        def op_init():
+            nc.vector.memset(small[:], 0.0)
+            nc.vector.memset(vecs[:], 0.0)
+            nc.vector.memset(ones_b[:], 1.0)
+            nc.vector.memset(eps_t[:], EPS)
+            make_identity(nc, ident_f[:])
+            make_identity(nc, ident_b[:])
+            nc.scalar.activation(out=warm[:], in_=eps_t[:], func=ACT.Abs_reciprocal_sqrt)
+
+        def op_SM():
+            nc.scalar.dma_start(out=small[0:32, :], in_=xd2[:, 0:P])
+            nc.scalar.dma_start(out=small[32:64, :], in_=xd2[:, P : 2 * P])
+            nc.scalar.dma_start(out=small[64:72, :], in_=b2.rearrange("(m p) -> m p", p=P))
+            for c, vec in enumerate((bo, ln_out_g, ln_out_b)):
+                nc.scalar.dma_start(out=vecs[0:1, c, :], in_=vec.rearrange("(o f) -> o f", o=1))
+
+        def op_W2(nb, g):
+            for u in range(2):
+                k0 = 512 * g + 256 * u
+                nc.sync.dma_start(
+                    out=w2_raw[:, nb, g, 2 * u : 2 * u + 2, :],
+                    in_=W2[k0 : k0 + 256, HALF * nb : HALF * (nb + 1)].rearrange("(q e) n -> q e n", e=2),
+                )
+
+        def op_HID(ap):
+            nc.sync.dma_start(
+                out=hid_raw[:, 2 * ap : 2 * ap + 2, :],
+                in_=hid2[256 * ap : 256 * (ap + 1), :].rearrange("(a p) k -> p a k", p=P),
+            )
+
+        def op_PL(h):
+            nc.sync.dma_start(
+                out=pl_raw[:, 4 * h : 4 * h + 4, :],
+                in_=pl2[HALF * h : HALF * (h + 1), :].rearrange("(a p) f -> p a f", p=P),
+            )
+
+        def op_WO(g):
+            nc.sync.dma_start(
+                out=wo_raw[:, g, :, :],
+                in_=Wo[512 * g : 512 * (g + 1), :].rearrange("(t p) n -> p t n", p=P),
+            )
+
+        def op_Tsm():
+            t = bank("sm", "A", [P, P], BF16)
+            nc.tensor.transpose(t[:], small[:], ident_b[:])
+
+        def op_smT():
+            nc.scalar.copy(out=smT[:], in_=live["sm"][:, 0:72])
+
+        def op_xb():
             nc.vector.tensor_scalar_mul(nb2[:], smT[:, 64:72], -1.0)
             for m in range(4):
                 x0 = 32 * (m % 2)
                 nc.vector.tensor_scalar_add(
                     out=xb[:, m, :], in0=smT[:, x0 : x0 + 32], scalar1=smT[:, 64 + m : 65 + m]
                 )
-            for c, dst in enumerate((bo_bc, g_bc)):
-                bc_ps = ps_pl.tile([P, ED], F32, tag="pl", name="bc_ps")
-                nc.tensor.matmul(bc_ps[:], lhsT=ones_b[:], rhs=vecs[:, c, :], start=True, stop=True)
-                nc.scalar.copy(out=dst[:], in_=bc_ps[:])
 
-        def prep_pl(h):
-            for tp in range(2):
-                plT = ps_tr.tile([P, 2, HALF], BF16, tag="tr", name="plT")
-                for tl in range(2):
-                    t = 2 * tp + tl
-                    for al in range(4):
-                        nc.tensor.transpose(
-                            plT[:, tl, P * al : P * (al + 1)],
-                            pl_raw[:, 4 * h + al, P * t : P * (t + 1)],
-                            ident_b[:],
-                        )
-                for tl in range(2):
-                    t = 2 * tp + tl
-                    nc.scalar.activation(
-                        out=zb[:, t, HALF * h : HALF * (h + 1)],
-                        in_=plT[:, tl, :],
-                        func=ACT.Identity,
-                        bias=smT[:, 68 + t : 69 + t],
-                        scale=1.0,
+        def op_BC(c):
+            t = bank(("bc", c), "pl", [P, ED], F32)
+            nc.tensor.matmul(t[:], lhsT=ones_b[:], rhs=vecs[:, c, :], start=True, stop=True)
+
+        def op_bc(c):
+            nc.scalar.copy(out=(bo_bc, g_bc)[c][:], in_=live[("bc", c)][:])
+
+        def op_R(nb, g, eng):
+            regroup(eng, w2_gr[:, nb, g, :, :], w2_raw[:, nb, g, :, :])
+
+        def op_Qw(nb):
+            quantise(
+                w2_codes[:, nb, :, :].rearrange("p g n -> p (g n)"),
+                w2_sc[:, nb, :, :].rearrange("p g n -> p (g n)"),
+                w2_gr[:, nb, :, :, :].rearrange("p g n t -> p (g n t)"),
+            )
+
+        def op_TH(h, g, l):
+            xt = bank(("th", h, g, l), "A", [P, 2, 2, P], F32)
+            for al in range(2):
+                words = hid_raw[:, 4 * h + 2 * l + al, :].bitcast(F32)
+                for u in range(2):
+                    w0 = 256 * g + 128 * u
+                    nc.tensor.transpose(xt[:, al, u, :], words[:, w0 : w0 + P], ident_f[:])
+
+        def op_EH(h, g, l, eng):
+            copy_on(
+                eng,
+                hid_gr[:, h, g, 256 * l : 256 * (l + 1), :].rearrange("p (a r) u -> p a r u", a=2),
+                live[("th", h, g, l)][:].rearrange("p a u r -> p a r u"),
+            )
+
+        def op_Qh(h):
+            quantise(
+                hid_codes[:, h, :, :].rearrange("p g r -> p (g r)"),
+                hid_sc[:, h, :, :].rearrange("p g r -> p (g r)"),
+                hid_gr_b[:, h, :, :, :].rearrange("p g r t -> p (g r t)"),
+            )
+
+        def op_TP(h, tp):
+            plT = bank(("tp", h, tp), "A", [P, 2, HALF], BF16)
+            for tl in range(2):
+                t = 2 * tp + tl
+                for al in range(4):
+                    nc.tensor.transpose(
+                        plT[:, tl, P * al : P * (al + 1)],
+                        pl_raw[:, 4 * h + al, P * t : P * (t + 1)],
+                        ident_b[:],
                     )
 
-        def stage1(h, g2):
-            rows = slice(HALF * h, HALF * (h + 1))
-            for t in range(4):
-                m = 4 * g2 + t
-                acc = ps_s1.tile([P, HALF], F32, tag="s1", name="acc")
-                for g in range(2):
-                    nc.tensor.matmul_mx(
-                        out=acc[:],
-                        lhsT=w2_codes[:, g, P * m : P * (m + 1)].bitcast(FP8X4),
-                        lhsT_scale=w2_sc[:, g, P * m : P * (m + 1)],
-                        rhs=hid_codes[:, g, rows].bitcast(FP8X4),
-                        rhs_scale=hid_sc[:, g, rows],
-                        start=(g == 0),
-                        stop=(g == 1),
-                    )
-                if m < 2:
-                    add = xb[:, m, 16 * h : 16 * (h + 1)].unsqueeze(2).to_broadcast([P, 16, NODES])
-                elif m < 4:
-                    add = xb[:, m, :].unsqueeze(1).to_broadcast([P, 16, NODES])
-                else:
-                    add = zb[:, m - 4, rows].rearrange("p (i j) -> p i j", j=NODES)
-                nc.vector.scalar_tensor_tensor(
-                    out=s_raw[:, m, rows].rearrange("p (i j) -> p i j", j=NODES),
-                    in0=acc[:].rearrange("p (i j) -> p i j", j=NODES),
-                    scalar=nb2[:, m : m + 1],
-                    in1=add,
-                    op0=ALU.max,
-                    op1=ALU.add,
+        def op_EP(h, t):
+            nc.scalar.activation(
+                out=zb[:, h, t, :],
+                in_=live[("tp", h, t // 2)][:, t % 2, :],
+                func=ACT.Identity,
+                bias=smT[:, 68 + t : 69 + t],
+                scale=1.0,
+            )
+
+        def op_S1(h, m):
+            acc = bank(("s1", h, m), "s1", [P, HALF], F32)
+            cols = slice(P * (m % 4), P * (m % 4 + 1))
+            for g in range(2):
+                nc.tensor.matmul_mx(
+                    out=acc[:],
+                    lhsT=w2_codes[:, m // 4, g, cols].bitcast(FP8X4),
+                    lhsT_scale=w2_sc[:, m // 4, g, cols],
+                    rhs=hid_codes[:, h, g, :].bitcast(FP8X4),
+                    rhs_scale=hid_sc[:, h, g, :],
+                    start=(g == 0),
+                    stop=(g == 1),
                 )
-            regroup(nc.scalar.copy, s_gr[:, g2, rows, :], s_raw[:, 4 * g2 : 4 * g2 + 4, rows])
-            quantise(s_codes[:, g2, rows], s_sc[:, g2, rows], s_gr[:, g2, rows, :])
 
-        def stage2(a):
-            z = ps_s2.tile([P, ED], F32, tag="s2", name="z")
+        def op_G(h, m):
+            if m < 2:
+                add = xb[:, m, 16 * h : 16 * (h + 1)].unsqueeze(2).to_broadcast([P, 16, NODES])
+            elif m < 4:
+                add = xb[:, m, :].unsqueeze(1).to_broadcast([P, 16, NODES])
+            else:
+                add = zb[:, h, m - 4, :].rearrange("p (i j) -> p i j", j=NODES)
+            nc.vector.scalar_tensor_tensor(
+                out=s_raw[:, h, m // 4, m % 4, :].rearrange("p (i j) -> p i j", j=NODES),
+                in0=live[("s1", h, m)][:].rearrange("p (i j) -> p i j", j=NODES),
+                scalar=nb2[:, m : m + 1],
+                in1=add,
+                op0=ALU.max,
+                op1=ALU.add,
+            )
+
+        def op_H(h, g2, eng):
+            regroup(eng, s_gr[:, h, g2, :, :], s_raw[:, h, g2, :, :])
+
+        def op_Qs(h, g2):
+            quantise(
+                s_codes[:, h, g2, :], s_sc[:, h, g2, :], s_gr[:, h, g2, :, :].rearrange("p r t -> p (r t)")
+            )
+
+        def op_RWo(g, eng):
+            regroup(eng, wo_gr[:, g, :, :], wo_raw[:, g, :, :])
+
+        def op_Qwo():
+            quantise(
+                wo_codes[:].rearrange("p g n -> p (g n)"),
+                wo_sc[:].rearrange("p g n -> p (g n)"),
+                wo_gr[:].rearrange("p g n t -> p (g n t)"),
+            )
+
+        def op_S2(a):
+            z = bank(("z", a), "A", [P, ED], F32)
+            h = a // 4
+            rows = slice(P * (a % 4), P * (a % 4 + 1))
             for g2 in range(2):
                 nc.tensor.matmul_mx(
                     out=z[:],
-                    lhsT=s_codes[:, g2, P * a : P * (a + 1)].bitcast(FP8X4),
-                    lhsT_scale=s_sc[:, g2, P * a : P * (a + 1)],
+                    lhsT=s_codes[:, h, g2, rows].bitcast(FP8X4),
+                    lhsT_scale=s_sc[:, h, g2, rows],
                     rhs=wo_codes[:, g2, :].bitcast(FP8X4),
                     rhs_scale=wo_sc[:, g2, :],
                     start=(g2 == 0),
                     stop=(g2 == 1),
                 )
-            plb = ps_pl.tile([P, ED], F32, tag="pl", name="plb")
+
+        def op_PLB(a):
+            plb = bank(("plb", a), "pl", [P, ED], F32)
             nc.tensor.matmul(plb[:], lhsT=ident_b[:], rhs=pl_raw[:, a, :], start=True, stop=False)
             nc.tensor.matmul(plb[:], lhsT=ones_b[:], rhs=vecs[:, 2, :], start=False, stop=True)
 
-            u = work.tile([P, ED], F32, name="u")
-            su = tiny.tile([P, 1], F32, name="su")
+        def op_J1(a):
+            u = wtile(("u", a), "u", 6, [P, ED], F32)
+            su = wtile(("su", a), "su", 8, [P, 1], F32)
             nc.vector.scalar_tensor_tensor(
-                out=u[:], in0=z[:], scalar=1.0, in1=bo_bc[:], op0=ALU.mult, op1=ALU.add,
+                out=u[:], in0=live[("z", a)][:], scalar=1.0, in1=bo_bc[:], op0=ALU.mult, op1=ALU.add,
                 accum_out=su[:],
             )
-            nmu = tiny.tile([P, 1], F32, name="nmu")
-            nc.vector.tensor_scalar_mul(nmu[:], su[:], -1.0 / ED)
-            sq = work.tile([P, ED], BF16, name="sq")
-            ssq = tiny.tile([P, 1], F32, name="ssq")
-            nc.scalar.activation(
-                out=sq[:], in_=u[:], func=ACT.Square, bias=nmu[:], scale=1.0, accum_out=ssq[:]
-            )
-            std = tiny.tile([P, 1], F32, name="std")
-            nc.scalar.activation(out=std[:], in_=ssq[:], func=ACT.Sqrt, bias=eps_t[:], scale=1.0 / ED)
-            rstd = tiny.tile([P, 1], F32, name="rstd")
-            nc.vector.reciprocal(rstd[:], std[:])
-            t1 = work.tile([P, ED], F32, name="t1")
-            nc.vector.scalar_tensor_tensor(
-                out=t1[:], in0=u[:], scalar=nmu[:], in1=g_bc[:], op0=ALU.add, op1=ALU.mult
-            )
-            o = work.tile([P, ED], F32, name="o")
-            nc.vector.scalar_tensor_tensor(
-                out=o[:], in0=t1[:], scalar=rstd[:], in1=plb[:], op0=ALU.mult, op1=ALU.add
-            )
-            nc.sync.dma_start(out=out2[P * a : P * (a + 1), :], in_=o[:])
 
-        prep_w2(0)
-        prep_small()
-        prep_hid(0)
-        prep_w2(1)
-        prep_pl(0)
-        stage1(0, 0)
-        stage1(0, 1)
-        prep_hid(1)
-        prep_wo(0)
-        prep_wo(1)
-        quant_wo(0)
-        quant_wo(1)
-        prep_pl(1)
-        stage1(1, 0)
-        for a in range(4):
-            stage2(a)
-        stage1(1, 1)
-        for a in range(4, 8):
-            stage2(a)
+        def op_n(a):
+            nmu = wtile(("nmu", a), "nmu", 8, [P, 1], F32)
+            nc.scalar.mul(out=nmu[:], in_=live[("su", a)][:], mul=-1.0 / ED)
+
+        def op_JS(a):
+            sq = wtile(("sq", a), "sq", 2, [P, ED], BF16)
+            ssq = wtile(("ssq", a), "ssq", 8, [P, 1], F32)
+            nc.scalar.activation(
+                out=sq[:], in_=live[("u", a)][:], func=ACT.Square, bias=live[("nmu", a)][:], scale=1.0,
+                accum_out=ssq[:],
+            )
+
+        def op_sq(a):
+            std = wtile(("std", a), "std", 8, [P, 1], F32)
+            nc.scalar.activation(
+                out=std[:], in_=live[("ssq", a)][:], func=ACT.Sqrt, bias=eps_t[:], scale=1.0 / ED
+            )
+
+        def op_rs(a):
+            rstd = wtile(("rstd", a), "rstd", 8, [P, 1], F32)
+            nc.scalar.activation(
+                out=rstd[:], in_=live[("ssq", a)][:], func=ACT.Abs_reciprocal_sqrt, bias=eps_t[:], scale=1.0 / ED
+            )
+
+        def op_nrS(a):
+            nmr = wtile(("nmr", a), "nmr", 8, [P, 1], F32)
+            nc.scalar.activation(
+                out=nmr[:], in_=live[("nmu", a)][:], func=ACT.Copy, scale=live[("rstd", a)][:]
+            )
+
+        def op_rc(a):
+            rstd = wtile(("rstd", a), "rstd", 8, [P, 1], F32)
+            nc.vector.reciprocal(rstd[:], live[("std", a)][:])
+
+        def op_J2(a):
+            t1 = wtile(("t1", a), "t1", 4, [P, ED], F32)
+            nc.vector.scalar_tensor_tensor(
+                out=t1[:], in0=live[("u", a)][:], scalar=live[("nmu", a)][:], in1=g_bc[:],
+                op0=ALU.add, op1=ALU.mult,
+            )
+
+        def op_J3(a):
+            t1 = live[("t1", a)]
+            nc.vector.scalar_tensor_tensor(
+                out=t1[:], in0=t1[:], scalar=live[("rstd", a)][:], in1=live[("plb", a)][:],
+                op0=ALU.mult, op1=ALU.add,
+            )
+
+        def op_nr(a):
+            nmr = wtile(("nmr", a), "nmr", 8, [P, 1], F32)
+            nc.vector.tensor_mul(nmr[:], live[("nmu", a)][:], live[("rstd", a)][:])
+
+        def op_Jy(a):
+            u = live[("u", a)]
+            nc.scalar.activation(
+                out=u[:], in_=u[:], func=ACT.Identity, bias=live[("nmr", a)][:], scale=live[("rstd", a)][:]
+            )
+
+        def op_GM(a):
+            u = live[("u", a)]
+            nc.gpsimd.tensor_tensor(out=u[:], in0=u[:], in1=g_bc[:], op=ALU.mult)
+
+        def op_J3g(a):
+            u = live[("u", a)]
+            nc.vector.tensor_tensor(out=u[:], in0=u[:], in1=live[("plb", a)][:], op=ALU.add)
+            live[("t1", a)] = u
+
+        def op_ST(a):
+            nc.sync.dma_start(out=out2[P * a : P * (a + 1), :], in_=live[("t1", a)][:])
+
+        ops = {
+            "init": op_init, "SM": op_SM, "W2": op_W2, "HID": op_HID, "PL": op_PL, "WO": op_WO,
+            "Tsm": op_Tsm, "smT": op_smT, "xb": op_xb, "BC": op_BC, "bc": op_bc, "R": op_R, "Qw": op_Qw,
+            "TH": op_TH, "EH": op_EH, "Qh": op_Qh, "TP": op_TP, "EP": op_EP, "S1": op_S1, "G": op_G,
+            "H": op_H, "Qs": op_Qs, "RWo": op_RWo, "Qwo": op_Qwo, "S2": op_S2, "PLB": op_PLB,
+            "J1": op_J1, "n": op_n, "JS": op_JS, "sq": op_sq, "rc": op_rc, "J2": op_J2, "J3": op_J3,
+            "nr": op_nr, "rs": op_rs, "nrS": op_nrS, "Jy": op_Jy, "GM": op_GM, "J3g": op_J3g, "ST": op_ST,
+        }
+        with tc.manual_schedule():
+            for step in ORDER:
+                ops[step[0]](*step[1:])

@@ -123,6 +123,9 @@ def tile_edgeupdaterwrapper_v01_pb_kernel(
                 nc.gpsimd.tensor_scalar(out=dst, in0=src, scalar1=1.0, scalar2=0.0, op0=ALU.mult, op1=ALU.add)
 
         def regroup(eng, dst, src):
+            if eng == "G":
+                copy_on(eng, dst, src.rearrange("p t n -> p n t"))
+                return
             copy_on(
                 eng,
                 dst.rearrange("p (c i) t -> p c t i", i=4),
@@ -402,6 +405,5 @@ def tile_edgeupdaterwrapper_v01_pb_kernel(
             "J1": op_J1, "n": op_n, "JS": op_JS, "sq": op_sq, "rc": op_rc, "J2": op_J2, "J3": op_J3,
             "nr": op_nr, "rs": op_rs, "nrS": op_nrS, "Jy": op_Jy, "GM": op_GM, "J3g": op_J3g, "ST": op_ST,
         }
-        with tc.manual_schedule():
-            for step in ORDER:
-                ops[step[0]](*step[1:])
+        for step in ORDER:
+            ops[step[0]](*step[1:])

@@ -21,40 +21,12 @@ EPS = 1e-5
 HALF = 512
 FLOPS = 2 * ROWS * F * MD + 2 * ROWS * MD * ED
 
-PSUM_BUFS = {"A": 2, "s1": 4, "pl": 2}
-ORDER = [
-    ("init",), ("SM",), ("W2", 0, 0), ("W2", 0, 1), ("HID", 0), ("HID", 1),
-    ("W2", 1, 0), ("W2", 1, 1), ("HID", 2), ("HID", 3), ("PL", 0), ("PL", 1),
-    ("WO", 0), ("WO", 1), ("Tsm",), ("smT",), ("BC", 0), ("bc", 0),
-    ("BC", 1), ("bc", 1), ("R", 0, 0, "V"), ("R", 0, 1, "V"), ("Qw", 0), ("xb",),
-    ("TH", 0, 0, 0), ("EH", 0, 0, 0, "S"), ("TH", 0, 1, 0), ("EH", 0, 1, 0, "S"), ("TH", 0, 0, 1), ("EH", 0, 0, 1, "S"),
-    ("TH", 0, 1, 1), ("EH", 0, 1, 1, "S"), ("Qh", 0), ("R", 1, 0, "S"), ("R", 1, 1, "V"), ("S1", 0, 0),
-    ("G", 0, 0), ("S1", 0, 1), ("G", 0, 1), ("S1", 0, 2), ("G", 0, 2), ("S1", 0, 3),
-    ("G", 0, 3), ("TH", 1, 0, 0), ("EH", 1, 0, 0, "S"), ("TH", 1, 1, 0), ("EH", 1, 1, 0, "S"), ("TH", 1, 0, 1),
-    ("EH", 1, 0, 1, "S"), ("TH", 1, 1, 1), ("EH", 1, 1, 1, "S"), ("Qw", 1), ("Qh", 1), ("H", 0, 0, "G"),
-    ("TP", 0, 0), ("EP", 0, 0), ("EP", 0, 1), ("TP", 0, 1), ("EP", 0, 2), ("EP", 0, 3),
-    ("RWo", 0, "G"), ("RWo", 1, "G"), ("S1", 0, 4), ("G", 0, 4), ("S1", 0, 5), ("G", 0, 5),
-    ("S1", 0, 6), ("G", 0, 6), ("S1", 0, 7), ("G", 0, 7), ("Qs", 0, 0), ("H", 0, 1, "S"),
-    ("TP", 1, 0), ("EP", 1, 0), ("EP", 1, 1), ("TP", 1, 1), ("EP", 1, 2), ("EP", 1, 3),
-    ("S1", 1, 0), ("G", 1, 0), ("S1", 1, 1), ("G", 1, 1), ("S1", 1, 2), ("G", 1, 2),
-    ("S1", 1, 3), ("G", 1, 3), ("Qs", 0, 1), ("H", 1, 0, "S"), ("S1", 1, 4), ("G", 1, 4),
-    ("S1", 1, 5), ("G", 1, 5), ("S1", 1, 6), ("G", 1, 6), ("S1", 1, 7), ("G", 1, 7),
-    ("Qwo",), ("H", 1, 1, "G"), ("S2", 0), ("J1", 0), ("n", 0), ("JS", 0),
-    ("rs", 0), ("nrS", 0), ("Jy", 0), ("GM", 0), ("S2", 1), ("J1", 1),
-    ("n", 1), ("JS", 1), ("rs", 1), ("nrS", 1), ("Jy", 1), ("GM", 1),
-    ("Qs", 1, 0), ("S2", 2), ("J1", 2), ("n", 2), ("JS", 2), ("rs", 2),
-    ("nrS", 2), ("Jy", 2), ("GM", 2), ("Qs", 1, 1), ("PLB", 0), ("J3g", 0),
-    ("ST", 0), ("S2", 3), ("J1", 3), ("n", 3), ("JS", 3), ("rs", 3),
-    ("nrS", 3), ("Jy", 3), ("GM", 3), ("PLB", 1), ("J3g", 1), ("ST", 1),
-    ("S2", 4), ("J1", 4), ("n", 4), ("JS", 4), ("rs", 4), ("nrS", 4),
-    ("Jy", 4), ("GM", 4), ("PLB", 2), ("J3g", 2), ("ST", 2), ("S2", 5),
-    ("J1", 5), ("n", 5), ("JS", 5), ("rs", 5), ("nrS", 5), ("Jy", 5),
-    ("GM", 5), ("PLB", 3), ("J3g", 3), ("ST", 3), ("S2", 6), ("J1", 6),
-    ("n", 6), ("JS", 6), ("rs", 6), ("nrS", 6), ("Jy", 6), ("GM", 6),
-    ("PLB", 4), ("J3g", 4), ("ST", 4), ("S2", 7), ("J1", 7), ("n", 7),
-    ("JS", 7), ("rs", 7), ("J2", 7), ("PLB", 7), ("J3", 7), ("ST", 7),
-    ("PLB", 5), ("J3g", 5), ("ST", 5), ("PLB", 6), ("J3g", 6), ("ST", 6),
-]
+BLOCKS = ((0,256),(256,512),(768,256))
+R_ENGINE = ("V","V","V","V")
+WO_ENGINE = ("V","V")
+H_ENGINE = (("S","S"),("S","S"),("S","S"))
+EH_ENGINE = "S"
+LOADS = (("W2", 0), ("HID", 0), ("W2", 1), ("PL", 0), ("WO", 0), ("HID", 1), ("HID", 2), ("PL", 1), ("HID", 3))
 
 
 def tile_edgeupdaterwrapper_v01_pb_kernel(
@@ -85,47 +57,24 @@ def tile_edgeupdaterwrapper_v01_pb_kernel(
         w2_gr = keep.tile([P, 2, 2, HALF, 4], BF16, align_bytes=64)
         w2_codes = keep.tile([P, 2, 2, HALF], U32, align_bytes=64)
         w2_sc = keep.tile([P, 2, 2, HALF], U8, align_bytes=64)
-        hid_gr = keep.tile([P, 2, 2, HALF, 2], F32, align_bytes=64)
-        hid_codes = keep.tile([P, 2, 2, HALF], U32, align_bytes=64)
-        hid_sc = keep.tile([P, 2, 2, HALF], U8, align_bytes=64)
         wo_gr = keep.tile([P, 2, ED, 4], BF16, align_bytes=64)
         wo_codes = keep.tile([P, 2, ED], U32, align_bytes=64)
         wo_sc = keep.tile([P, 2, ED], U8, align_bytes=64)
-        s_raw = keep.tile([P, 2, 2, 4, HALF], BF16)
-        s_gr = keep.tile([P, 2, 2, HALF, 4], BF16, align_bytes=64)
-        s_codes = keep.tile([P, 2, 2, HALF], U32, align_bytes=64)
-        s_sc = keep.tile([P, 2, 2, HALF], U8, align_bytes=64)
-        zb = keep.tile([P, 2, 4, HALF], F32)
+        s_raw = keep.tile([P, 8, ROWS], BF16)
+        zb = keep.tile([P, 4, ROWS], F32)
         smT = keep.tile([P, 72], F32)
         nb2 = keep.tile([P, 8], F32)
         xb = keep.tile([P, 4, NODES], F32)
         bo_bc = keep.tile([P, ED], F32)
         g_bc = keep.tile([P, ED], F32)
-        hid_gr_b = hid_gr[:].bitcast(BF16)
-        live = {}
-
-        def bank(key, tag, shape, dtype):
-            t = psum.tile(shape, dtype, tag=tag, bufs=PSUM_BUFS[tag], name="ps_%s" % tag)
-            live[key] = t
-            return t
-
-        def wtile(key, tag, bufs, shape, dtype):
-            t = work.tile(shape, dtype, tag=tag, bufs=bufs, name="w_%s" % tag)
-            live[key] = t
-            return t
 
         def copy_on(eng, dst, src):
             if eng == "V":
                 nc.vector.tensor_copy(out=dst, in_=src)
-            elif eng == "S":
-                nc.scalar.copy(out=dst, in_=src)
             else:
-                nc.gpsimd.tensor_scalar(out=dst, in0=src, scalar1=1.0, scalar2=0.0, op0=ALU.mult, op1=ALU.add)
+                nc.scalar.copy(out=dst, in_=src)
 
         def regroup(eng, dst, src):
-            if eng == "G":
-                copy_on(eng, dst, src.rearrange("p t n -> p n t"))
-                return
             copy_on(
                 eng,
                 dst.rearrange("p (c i) t -> p c t i", i=4),
@@ -135,275 +84,236 @@ def tile_edgeupdaterwrapper_v01_pb_kernel(
         def quantise(codes, scales, grouped):
             nc.vector.quantize_mx(out=codes.bitcast(FP8X4), scales=scales, in_=grouped)
 
-        def op_init():
-            nc.vector.memset(small[:], 0.0)
-            nc.vector.memset(vecs[:], 0.0)
-            nc.vector.memset(ones_b[:], 1.0)
-            nc.vector.memset(eps_t[:], EPS)
-            make_identity(nc, ident_f[:])
-            make_identity(nc, ident_b[:])
-            nc.scalar.activation(out=warm[:], in_=eps_t[:], func=ACT.Abs_reciprocal_sqrt)
+        nc.vector.memset(small[:], 0.0)
+        nc.vector.memset(vecs[:], 0.0)
+        nc.vector.memset(ones_b[:], 1.0)
+        nc.vector.memset(eps_t[:], EPS)
+        make_identity(nc, ident_f[:])
+        make_identity(nc, ident_b[:])
+        nc.scalar.dma_start(out=small[0:32, :], in_=xd2[:, 0:P])
+        nc.scalar.dma_start(out=small[32:64, :], in_=xd2[:, P : 2 * P])
+        nc.scalar.dma_start(out=small[64:72, :], in_=b2.rearrange("(m p) -> m p", p=P))
+        for c, vec in enumerate((bo, ln_out_g, ln_out_b)):
+            nc.scalar.dma_start(out=vecs[0:1, c, :], in_=vec.rearrange("(o f) -> o f", o=1))
+        nc.scalar.activation(out=warm[:], in_=eps_t[:], func=ACT.Abs_reciprocal_sqrt)
 
-        def op_SM():
-            nc.scalar.dma_start(out=small[0:32, :], in_=xd2[:, 0:P])
-            nc.scalar.dma_start(out=small[32:64, :], in_=xd2[:, P : 2 * P])
-            nc.scalar.dma_start(out=small[64:72, :], in_=b2.rearrange("(m p) -> m p", p=P))
-            for c, vec in enumerate((bo, ln_out_g, ln_out_b)):
-                nc.scalar.dma_start(out=vecs[0:1, c, :], in_=vec.rearrange("(o f) -> o f", o=1))
-
-        def op_W2(nb, g):
-            for u in range(2):
-                k0 = 512 * g + 256 * u
+        for kind, idx in LOADS:
+            if kind == "W2":
+                for g in range(2):
+                    for u in range(2):
+                        k0 = 512 * g + 256 * u
+                        nc.sync.dma_start(
+                            out=w2_raw[:, idx, g, 2 * u : 2 * u + 2, :],
+                            in_=W2[k0 : k0 + 256, HALF * idx : HALF * (idx + 1)].rearrange(
+                                "(q e) n -> q e n", e=2
+                            ),
+                        )
+            elif kind == "HID":
                 nc.sync.dma_start(
-                    out=w2_raw[:, nb, g, 2 * u : 2 * u + 2, :],
-                    in_=W2[k0 : k0 + 256, HALF * nb : HALF * (nb + 1)].rearrange("(q e) n -> q e n", e=2),
+                    out=hid_raw[:, 2 * idx : 2 * idx + 2, :],
+                    in_=hid2[256 * idx : 256 * (idx + 1), :].rearrange("(a p) k -> p a k", p=P),
                 )
-
-        def op_HID(ap):
-            nc.sync.dma_start(
-                out=hid_raw[:, 2 * ap : 2 * ap + 2, :],
-                in_=hid2[256 * ap : 256 * (ap + 1), :].rearrange("(a p) k -> p a k", p=P),
-            )
-
-        def op_PL(h):
-            nc.sync.dma_start(
-                out=pl_raw[:, 4 * h : 4 * h + 4, :],
-                in_=pl2[HALF * h : HALF * (h + 1), :].rearrange("(a p) f -> p a f", p=P),
-            )
-
-        def op_WO(g):
-            nc.sync.dma_start(
-                out=wo_raw[:, g, :, :],
-                in_=Wo[512 * g : 512 * (g + 1), :].rearrange("(t p) n -> p t n", p=P),
-            )
-
-        def op_Tsm():
-            t = bank("sm", "A", [P, P], BF16)
-            nc.tensor.transpose(t[:], small[:], ident_b[:])
-
-        def op_smT():
-            nc.scalar.copy(out=smT[:], in_=live["sm"][:, 0:72])
-
-        def op_xb():
-            nc.vector.tensor_scalar_mul(nb2[:], smT[:, 64:72], -1.0)
-            for m in range(4):
-                x0 = 32 * (m % 2)
-                nc.vector.tensor_scalar_add(
-                    out=xb[:, m, :], in0=smT[:, x0 : x0 + 32], scalar1=smT[:, 64 + m : 65 + m]
+            elif kind == "PL":
+                nc.sync.dma_start(
+                    out=pl_raw[:, 4 * idx : 4 * idx + 4, :],
+                    in_=pl2[HALF * idx : HALF * (idx + 1), :].rearrange("(a p) f -> p a f", p=P),
                 )
+            else:
+                for g in range(2):
+                    nc.sync.dma_start(
+                        out=wo_raw[:, g, :, :],
+                        in_=Wo[512 * g : 512 * (g + 1), :].rearrange("(t p) n -> p t n", p=P),
+                    )
 
-        def op_BC(c):
-            t = bank(("bc", c), "pl", [P, ED], F32)
-            nc.tensor.matmul(t[:], lhsT=ones_b[:], rhs=vecs[:, c, :], start=True, stop=True)
-
-        def op_bc(c):
-            nc.scalar.copy(out=(bo_bc, g_bc)[c][:], in_=live[("bc", c)][:])
-
-        def op_R(nb, g, eng):
-            regroup(eng, w2_gr[:, nb, g, :, :], w2_raw[:, nb, g, :, :])
-
-        def op_Qw(nb):
+        def prep_w2(nb):
+            for g in range(2):
+                regroup(R_ENGINE[2 * nb + g], w2_gr[:, nb, g, :, :], w2_raw[:, nb, g, :, :])
             quantise(
                 w2_codes[:, nb, :, :].rearrange("p g n -> p (g n)"),
                 w2_sc[:, nb, :, :].rearrange("p g n -> p (g n)"),
                 w2_gr[:, nb, :, :, :].rearrange("p g n t -> p (g n t)"),
             )
 
-        def op_TH(h, g, l):
-            xt = bank(("th", h, g, l), "A", [P, 2, 2, P], F32)
-            for al in range(2):
-                words = hid_raw[:, 4 * h + 2 * l + al, :].bitcast(F32)
-                for u in range(2):
-                    w0 = 256 * g + 128 * u
-                    nc.tensor.transpose(xt[:, al, u, :], words[:, w0 : w0 + P], ident_f[:])
-
-        def op_EH(h, g, l, eng):
-            copy_on(
-                eng,
-                hid_gr[:, h, g, 256 * l : 256 * (l + 1), :].rearrange("p (a r) u -> p a r u", a=2),
-                live[("th", h, g, l)][:].rearrange("p a u r -> p a r u"),
-            )
-
-        def op_Qh(h):
-            quantise(
-                hid_codes[:, h, :, :].rearrange("p g r -> p (g r)"),
-                hid_sc[:, h, :, :].rearrange("p g r -> p (g r)"),
-                hid_gr_b[:, h, :, :, :].rearrange("p g r t -> p (g r t)"),
-            )
-
-        def op_TP(h, tp):
-            plT = bank(("tp", h, tp), "A", [P, 2, HALF], BF16)
-            for tl in range(2):
-                t = 2 * tp + tl
-                for al in range(4):
-                    nc.tensor.transpose(
-                        plT[:, tl, P * al : P * (al + 1)],
-                        pl_raw[:, 4 * h + al, P * t : P * (t + 1)],
-                        ident_b[:],
-                    )
-
-        def op_EP(h, t):
-            nc.scalar.activation(
-                out=zb[:, h, t, :],
-                in_=live[("tp", h, t // 2)][:, t % 2, :],
-                func=ACT.Identity,
-                bias=smT[:, 68 + t : 69 + t],
-                scale=1.0,
-            )
-
-        def op_S1(h, m):
-            acc = bank(("s1", h, m), "s1", [P, HALF], F32)
-            cols = slice(P * (m % 4), P * (m % 4 + 1))
-            for g in range(2):
-                nc.tensor.matmul_mx(
-                    out=acc[:],
-                    lhsT=w2_codes[:, m // 4, g, cols].bitcast(FP8X4),
-                    lhsT_scale=w2_sc[:, m // 4, g, cols],
-                    rhs=hid_codes[:, h, g, :].bitcast(FP8X4),
-                    rhs_scale=hid_sc[:, h, g, :],
-                    start=(g == 0),
-                    stop=(g == 1),
+        def prep_small():
+            sm_ps = psum.tile([P, P], BF16, tag="A", bufs=3, name="sm_ps")
+            nc.tensor.transpose(sm_ps[:], small[:], ident_b[:])
+            nc.scalar.copy(out=smT[:], in_=sm_ps[:, 0:72])
+            nc.vector.tensor_scalar_mul(nb2[:], smT[:, 64:72], -1.0)
+            for m in range(4):
+                x0 = 32 * (m % 2)
+                nc.vector.tensor_scalar_add(
+                    out=xb[:, m, :], in0=smT[:, x0 : x0 + 32], scalar1=smT[:, 64 + m : 65 + m]
                 )
+            for c, dst in enumerate((bo_bc, g_bc)):
+                bc_ps = psum.tile([P, ED], F32, tag="pl", bufs=2, name="bc_ps")
+                nc.tensor.matmul(bc_ps[:], lhsT=ones_b[:], rhs=vecs[:, c, :], start=True, stop=True)
+                nc.scalar.copy(out=dst[:], in_=bc_ps[:])
 
-        def op_G(h, m):
-            if m < 2:
-                add = xb[:, m, 16 * h : 16 * (h + 1)].unsqueeze(2).to_broadcast([P, 16, NODES])
-            elif m < 4:
-                add = xb[:, m, :].unsqueeze(1).to_broadcast([P, 16, NODES])
-            else:
-                add = zb[:, h, m - 4, :].rearrange("p (i j) -> p i j", j=NODES)
-            nc.vector.scalar_tensor_tensor(
-                out=s_raw[:, h, m // 4, m % 4, :].rearrange("p (i j) -> p i j", j=NODES),
-                in0=live[("s1", h, m)][:].rearrange("p (i j) -> p i j", j=NODES),
-                scalar=nb2[:, m : m + 1],
-                in1=add,
-                op0=ALU.max,
-                op1=ALU.add,
-            )
-
-        def op_H(h, g2, eng):
-            regroup(eng, s_gr[:, h, g2, :, :], s_raw[:, h, g2, :, :])
-
-        def op_Qs(h, g2):
-            quantise(
-                s_codes[:, h, g2, :], s_sc[:, h, g2, :], s_gr[:, h, g2, :, :].rearrange("p r t -> p (r t)")
-            )
-
-        def op_RWo(g, eng):
-            regroup(eng, wo_gr[:, g, :, :], wo_raw[:, g, :, :])
-
-        def op_Qwo():
+        def prep_wo():
+            for g in range(2):
+                regroup(WO_ENGINE[g], wo_gr[:, g, :, :], wo_raw[:, g, :, :])
             quantise(
                 wo_codes[:].rearrange("p g n -> p (g n)"),
                 wo_sc[:].rearrange("p g n -> p (g n)"),
                 wo_gr[:].rearrange("p g n t -> p (g n t)"),
             )
 
-        def op_S2(a):
-            z = bank(("z", a), "A", [P, ED], F32)
-            h = a // 4
-            rows = slice(P * (a % 4), P * (a % 4 + 1))
+        def prep_pl(h):
+            for tp in range(2):
+                plT = psum.tile([P, 2, HALF], BF16, tag="A", bufs=3, name="plT")
+                for tl in range(2):
+                    t = 2 * tp + tl
+                    for al in range(4):
+                        nc.tensor.transpose(
+                            plT[:, tl, P * al : P * (al + 1)],
+                            pl_raw[:, 4 * h + al, P * t : P * (t + 1)],
+                            ident_b[:],
+                        )
+                for tl in range(2):
+                    t = 2 * tp + tl
+                    nc.scalar.activation(
+                        out=zb[:, t, HALF * h : HALF * (h + 1)],
+                        in_=plT[:, tl, :],
+                        func=ACT.Identity,
+                        bias=smT[:, 68 + t : 69 + t],
+                        scale=1.0,
+                    )
+
+        hid_codes = {}
+        hid_sc = {}
+        s_codes = {}
+        s_sc = {}
+        s_grs = {}
+
+        def prep_hid(b):
+            r0, n = BLOCKS[b]
+            gr = keep.tile([P, 2, n, 2], F32, align_bytes=64, name="hid_gr%d" % b)
+            hid_codes[b] = keep.tile([P, 2, n], U32, align_bytes=64, name="hid_codes%d" % b)
+            hid_sc[b] = keep.tile([P, 2, n], U8, align_bytes=64, name="hid_sc%d" % b)
+            for l in range(n // 256):
+                for g in range(2):
+                    xt = psum.tile([P, 2, 2, P], F32, tag="A", bufs=3, name="xt")
+                    for al in range(2):
+                        words = hid_raw[:, r0 // P + 2 * l + al, :].bitcast(F32)
+                        for u in range(2):
+                            w0 = 256 * g + 128 * u
+                            nc.tensor.transpose(xt[:, al, u, :], words[:, w0 : w0 + P], ident_f[:])
+                    copy_on(
+                        EH_ENGINE,
+                        gr[:, g, 256 * l : 256 * (l + 1), :].rearrange("p (a r) u -> p a r u", a=2),
+                        xt[:].rearrange("p a u r -> p a r u"),
+                    )
+            quantise(
+                hid_codes[b][:].rearrange("p g r -> p (g r)"),
+                hid_sc[b][:].rearrange("p g r -> p (g r)"),
+                gr[:].bitcast(BF16).rearrange("p g r t -> p (g r t)"),
+            )
+
+        def stage1(b, g2):
+            r0, n = BLOCKS[b]
+            rows = slice(r0, r0 + n)
+            i0 = r0 // NODES
+            ni = n // NODES
+            if g2 == 0:
+                s_grs[b] = keep.tile([P, 2, n, 4], BF16, align_bytes=64, name="s_gr%d" % b)
+                s_codes[b] = keep.tile([P, 2, n], U32, align_bytes=64, name="s_codes%d" % b)
+                s_sc[b] = keep.tile([P, 2, n], U8, align_bytes=64, name="s_sc%d" % b)
+            for t in range(4):
+                m = 4 * g2 + t
+                acc = psum.tile([P, n], F32, tag="s1", bufs=3, name="acc")
+                cols = slice(P * t, P * (t + 1))
+                for g in range(2):
+                    nc.tensor.matmul_mx(
+                        out=acc[:],
+                        lhsT=w2_codes[:, g2, g, cols].bitcast(FP8X4),
+                        lhsT_scale=w2_sc[:, g2, g, cols],
+                        rhs=hid_codes[b][:, g, :].bitcast(FP8X4),
+                        rhs_scale=hid_sc[b][:, g, :],
+                        start=(g == 0),
+                        stop=(g == 1),
+                    )
+                if m < 2:
+                    add = xb[:, m, i0 : i0 + ni].unsqueeze(2).to_broadcast([P, ni, NODES])
+                elif m < 4:
+                    add = xb[:, m, :].unsqueeze(1).to_broadcast([P, ni, NODES])
+                else:
+                    add = zb[:, m - 4, rows].rearrange("p (i j) -> p i j", j=NODES)
+                nc.vector.scalar_tensor_tensor(
+                    out=s_raw[:, m, rows].rearrange("p (i j) -> p i j", j=NODES),
+                    in0=acc[:].rearrange("p (i j) -> p i j", j=NODES),
+                    scalar=nb2[:, m : m + 1],
+                    in1=add,
+                    op0=ALU.max,
+                    op1=ALU.add,
+                )
+            regroup(H_ENGINE[b][g2], s_grs[b][:, g2, :, :], s_raw[:, 4 * g2 : 4 * g2 + 4, rows])
+
+        def quant_s(b):
+            quantise(
+                s_codes[b][:].rearrange("p g r -> p (g r)"),
+                s_sc[b][:].rearrange("p g r -> p (g r)"),
+                s_grs[b][:].rearrange("p g r t -> p (g r t)"),
+            )
+
+        def stage2(b, al):
+            r0, n = BLOCKS[b]
+            a = r0 // P + al
+            rows = slice(P * al, P * (al + 1))
+            z = psum.tile([P, ED], F32, tag="A", bufs=3, name="z")
             for g2 in range(2):
                 nc.tensor.matmul_mx(
                     out=z[:],
-                    lhsT=s_codes[:, h, g2, rows].bitcast(FP8X4),
-                    lhsT_scale=s_sc[:, h, g2, rows],
+                    lhsT=s_codes[b][:, g2, rows].bitcast(FP8X4),
+                    lhsT_scale=s_sc[b][:, g2, rows],
                     rhs=wo_codes[:, g2, :].bitcast(FP8X4),
                     rhs_scale=wo_sc[:, g2, :],
                     start=(g2 == 0),
                     stop=(g2 == 1),
                 )
-
-        def op_PLB(a):
-            plb = bank(("plb", a), "pl", [P, ED], F32)
+            plb = psum.tile([P, ED], F32, tag="pl", bufs=2, name="plb")
             nc.tensor.matmul(plb[:], lhsT=ident_b[:], rhs=pl_raw[:, a, :], start=True, stop=False)
             nc.tensor.matmul(plb[:], lhsT=ones_b[:], rhs=vecs[:, 2, :], start=False, stop=True)
-
-        def op_J1(a):
-            u = wtile(("u", a), "u", 6, [P, ED], F32)
-            su = wtile(("su", a), "su", 8, [P, 1], F32)
+            u = work.tile([P, ED], F32, tag="u", bufs=4, name="u")
+            su = work.tile([P, 1], F32, tag="su", bufs=4, name="su")
             nc.vector.scalar_tensor_tensor(
-                out=u[:], in0=live[("z", a)][:], scalar=1.0, in1=bo_bc[:], op0=ALU.mult, op1=ALU.add,
-                accum_out=su[:],
+                out=u[:], in0=z[:], scalar=1.0, in1=bo_bc[:], op0=ALU.mult, op1=ALU.add, accum_out=su[:]
             )
-
-        def op_n(a):
-            nmu = wtile(("nmu", a), "nmu", 8, [P, 1], F32)
-            nc.scalar.mul(out=nmu[:], in_=live[("su", a)][:], mul=-1.0 / ED)
-
-        def op_JS(a):
-            sq = wtile(("sq", a), "sq", 2, [P, ED], BF16)
-            ssq = wtile(("ssq", a), "ssq", 8, [P, 1], F32)
+            nmu = work.tile([P, 1], F32, tag="nmu", bufs=4, name="nmu")
+            nc.scalar.mul(out=nmu[:], in_=su[:], mul=-1.0 / ED)
+            sq = work.tile([P, ED], BF16, tag="sq", bufs=2, name="sq")
+            ssq = work.tile([P, 1], F32, tag="ssq", bufs=4, name="ssq")
             nc.scalar.activation(
-                out=sq[:], in_=live[("u", a)][:], func=ACT.Square, bias=live[("nmu", a)][:], scale=1.0,
-                accum_out=ssq[:],
+                out=sq[:], in_=u[:], func=ACT.Square, bias=nmu[:], scale=1.0, accum_out=ssq[:]
             )
-
-        def op_sq(a):
-            std = wtile(("std", a), "std", 8, [P, 1], F32)
+            rstd = work.tile([P, 1], F32, tag="rstd", bufs=4, name="rstd")
             nc.scalar.activation(
-                out=std[:], in_=live[("ssq", a)][:], func=ACT.Sqrt, bias=eps_t[:], scale=1.0 / ED
+                out=rstd[:], in_=ssq[:], func=ACT.Abs_reciprocal_sqrt, bias=eps_t[:], scale=1.0 / ED
             )
-
-        def op_rs(a):
-            rstd = wtile(("rstd", a), "rstd", 8, [P, 1], F32)
-            nc.scalar.activation(
-                out=rstd[:], in_=live[("ssq", a)][:], func=ACT.Abs_reciprocal_sqrt, bias=eps_t[:], scale=1.0 / ED
-            )
-
-        def op_nrS(a):
-            nmr = wtile(("nmr", a), "nmr", 8, [P, 1], F32)
-            nc.scalar.activation(
-                out=nmr[:], in_=live[("nmu", a)][:], func=ACT.Copy, scale=live[("rstd", a)][:]
-            )
-
-        def op_rc(a):
-            rstd = wtile(("rstd", a), "rstd", 8, [P, 1], F32)
-            nc.vector.reciprocal(rstd[:], live[("std", a)][:])
-
-        def op_J2(a):
-            t1 = wtile(("t1", a), "t1", 4, [P, ED], F32)
+            t1 = work.tile([P, ED], F32, tag="t1", bufs=4, name="t1")
             nc.vector.scalar_tensor_tensor(
-                out=t1[:], in0=live[("u", a)][:], scalar=live[("nmu", a)][:], in1=g_bc[:],
-                op0=ALU.add, op1=ALU.mult,
+                out=t1[:], in0=u[:], scalar=nmu[:], in1=g_bc[:], op0=ALU.add, op1=ALU.mult
             )
-
-        def op_J3(a):
-            t1 = live[("t1", a)]
             nc.vector.scalar_tensor_tensor(
-                out=t1[:], in0=t1[:], scalar=live[("rstd", a)][:], in1=live[("plb", a)][:],
-                op0=ALU.mult, op1=ALU.add,
+                out=t1[:], in0=t1[:], scalar=rstd[:], in1=plb[:], op0=ALU.mult, op1=ALU.add
             )
+            nc.sync.dma_start(out=out2[P * a : P * (a + 1), :], in_=t1[:])
 
-        def op_nr(a):
-            nmr = wtile(("nmr", a), "nmr", 8, [P, 1], F32)
-            nc.vector.tensor_mul(nmr[:], live[("nmu", a)][:], live[("rstd", a)][:])
-
-        def op_Jy(a):
-            u = live[("u", a)]
-            nc.scalar.activation(
-                out=u[:], in_=u[:], func=ACT.Identity, bias=live[("nmr", a)][:], scale=live[("rstd", a)][:]
-            )
-
-        def op_GM(a):
-            u = live[("u", a)]
-            nc.gpsimd.tensor_tensor(out=u[:], in0=u[:], in1=g_bc[:], op=ALU.mult)
-
-        def op_J3g(a):
-            u = live[("u", a)]
-            nc.vector.tensor_tensor(out=u[:], in0=u[:], in1=live[("plb", a)][:], op=ALU.add)
-            live[("t1", a)] = u
-
-        def op_ST(a):
-            nc.sync.dma_start(out=out2[P * a : P * (a + 1), :], in_=live[("t1", a)][:])
-
-        ops = {
-            "init": op_init, "SM": op_SM, "W2": op_W2, "HID": op_HID, "PL": op_PL, "WO": op_WO,
-            "Tsm": op_Tsm, "smT": op_smT, "xb": op_xb, "BC": op_BC, "bc": op_bc, "R": op_R, "Qw": op_Qw,
-            "TH": op_TH, "EH": op_EH, "Qh": op_Qh, "TP": op_TP, "EP": op_EP, "S1": op_S1, "G": op_G,
-            "H": op_H, "Qs": op_Qs, "RWo": op_RWo, "Qwo": op_Qwo, "S2": op_S2, "PLB": op_PLB,
-            "J1": op_J1, "n": op_n, "JS": op_JS, "sq": op_sq, "rc": op_rc, "J2": op_J2, "J3": op_J3,
-            "nr": op_nr, "rs": op_rs, "nrS": op_nrS, "Jy": op_Jy, "GM": op_GM, "J3g": op_J3g, "ST": op_ST,
-        }
-        for step in ORDER:
-            ops[step[0]](*step[1:])
+        prep_w2(0)
+        prep_small()
+        prep_hid(0)
+        stage1(0, 0)
+        prep_w2(1)
+        prep_pl(0)
+        stage1(0, 1)
+        quant_s(0)
+        prep_wo()
+        for b in range(len(BLOCKS)):
+            if b + 1 < len(BLOCKS):
+                prep_hid(b + 1)
+                if BLOCKS[b + 1][0] + BLOCKS[b + 1][1] > HALF and BLOCKS[b + 1][0] <= HALF:
+                    prep_pl(1)
+                stage1(b + 1, 0)
+                stage1(b + 1, 1)
+                quant_s(b + 1)
+            for al in range(BLOCKS[b][1] // P):
+                stage2(b, al)

@@ -26,7 +26,7 @@ R_ENGINE = ("V","V","V","V")
 WO_ENGINE = ("V","V")
 H_ENGINE = (("S","S"),("S","S"),("S","S"))
 EH_ENGINE = "S"
-LOADS = (("W2", 0), ("HID", 0), ("W2", 1), ("PL", 0), ("WO", 0), ("HID", 1), ("HID", 2), ("PL", 1), ("HID", 3))
+LOADS = (("W2", 0), ("HID", 0), ("XD", 0), ("W2", 1), ("PL", 0), ("VEC", 0), ("WO", 0), ("HID", 1), ("HID", 2), ("PL", 1), ("HID", 3))
 
 
 def tile_edgeupdaterwrapper_v01_pb_kernel(
@@ -90,11 +90,6 @@ def tile_edgeupdaterwrapper_v01_pb_kernel(
         nc.vector.memset(eps_t[:], EPS)
         make_identity(nc, ident_f[:])
         make_identity(nc, ident_b[:])
-        nc.scalar.dma_start(out=small[0:32, :], in_=xd2[:, 0:P])
-        nc.scalar.dma_start(out=small[32:64, :], in_=xd2[:, P : 2 * P])
-        nc.scalar.dma_start(out=small[64:72, :], in_=b2.rearrange("(m p) -> m p", p=P))
-        for c, vec in enumerate((bo, ln_out_g, ln_out_b)):
-            nc.scalar.dma_start(out=vecs[0:1, c, :], in_=vec.rearrange("(o f) -> o f", o=1))
         nc.scalar.activation(out=warm[:], in_=eps_t[:], func=ACT.Abs_reciprocal_sqrt)
 
         for kind, idx in LOADS:
@@ -108,6 +103,13 @@ def tile_edgeupdaterwrapper_v01_pb_kernel(
                                 "(q e) n -> q e n", e=2
                             ),
                         )
+            elif kind == "XD":
+                nc.sync.dma_start(out=small[0:32, :], in_=xd2[:, 0:P])
+                nc.sync.dma_start(out=small[32:64, :], in_=xd2[:, P : 2 * P])
+                nc.sync.dma_start(out=small[64:72, :], in_=b2.rearrange("(m p) -> m p", p=P))
+            elif kind == "VEC":
+                for c, vec in enumerate((bo, ln_out_g, ln_out_b)):
+                    nc.sync.dma_start(out=vecs[0:1, c, :], in_=vec.rearrange("(o f) -> o f", o=1))
             elif kind == "HID":
                 nc.sync.dma_start(
                     out=hid_raw[:, 2 * idx : 2 * idx + 2, :],

@@ -12,310 +12,336 @@ ALU = mybir.AluOpType
 ACT = mybir.ActivationFunctionType
 
 P = 128
+PACK = 4
+K_PASS = P * PACK
 NODES = 32
 ROWS = NODES * NODES
 F = 1024
 MD = 1024
 ED = 512
+PASSES = 2
+HID_LOAD = 256
+PLN_LOAD = 512
 EPS = 1e-5
-HALF = 512
 FLOPS = 2 * ROWS * F * MD + 2 * ROWS * MD * ED
 
-BLOCKS = ((0,256),(256,512),(768,256))
-R_ENGINE = ("V","V","V","V")
-WO_ENGINE = ("V","V")
-H_ENGINE = (("S","S"),("S","S"),("S","S"))
-EH_ENGINE = "S"
-LOADS = (("W2", 0), ("HID", 0), ("XD", 0), ("W2", 1), ("PL", 0), ("VEC", 0), ("WO", 0), ("HID", 1), ("HID", 2), ("PL", 1), ("HID", 3))
+BLOCKS = ((0, 512), (512, 512))
+
+BANKS_T, BANKS_S, BANKS_B = 3, 3, 2
+LN_DEPTH = 4
 
 
 def tile_edgeupdaterwrapper_v01_pb_kernel(
     tc, hid, x_down, p_ln, W2, b2, Wo, bo, ln_out_g, ln_out_b, out
 ):
     nc = tc.nc
-    hid2 = hid.rearrange("b i j k -> (b i j) k")
-    pl2 = p_ln.rearrange("b i j f -> (b i j) f")
-    out2 = out.rearrange("b i j f -> (b i j) f")
-    xd2 = x_down.rearrange("b n f -> (b n) f")
+    hid_rows = hid.rearrange("b i j k -> (b i j) k")
+    pln_rows = p_ln.rearrange("b i j f -> (b i j) f")
+    out_rows = out.rearrange("b i j f -> (b i j) f")
+    xd_rows = x_down.rearrange("b n f -> (b n) f")
 
     with ExitStack() as ctx:
         keep = ctx.enter_context(tc.tile_pool(name="keep", bufs=1))
         work = ctx.enter_context(tc.tile_pool(name="work", bufs=1))
         psum = ctx.enter_context(tc.psum_pool(name="psum", bufs=1))
 
-        small = keep.tile([P, P], BF16)
-        vecs = keep.tile([P, 3, ED], BF16)
-        ones_b = keep.tile([P, P], BF16)
-        eps_t = keep.tile([P, 1], F32)
-        warm = keep.tile([P, 1], F32)
-        ident_f = keep.tile([P, P], F32)
-        ident_b = keep.tile([P, P], BF16)
-        hid_raw = keep.tile([P, 8, F], BF16)
-        w2_raw = keep.tile([P, 2, 2, 4, HALF], BF16)
-        wo_raw = keep.tile([P, 2, 4, ED], BF16)
-        pl_raw = keep.tile([P, 8, ED], BF16)
-        w2_gr = keep.tile([P, 2, 2, HALF, 4], BF16, align_bytes=64)
-        w2_codes = keep.tile([P, 2, 2, HALF], U32, align_bytes=64)
-        w2_sc = keep.tile([P, 2, 2, HALF], U8, align_bytes=64)
-        wo_gr = keep.tile([P, 2, ED, 4], BF16, align_bytes=64)
-        wo_codes = keep.tile([P, 2, ED], U32, align_bytes=64)
-        wo_sc = keep.tile([P, 2, ED], U8, align_bytes=64)
-        s_raw = keep.tile([P, 8, ROWS], BF16)
-        zb = keep.tile([P, 4, ROWS], F32)
-        smT = keep.tile([P, 72], F32)
-        nb2 = keep.tile([P, 8], F32)
-        xb = keep.tile([P, 4, NODES], F32)
-        bo_bc = keep.tile([P, ED], F32)
-        g_bc = keep.tile([P, ED], F32)
+        hid_raw = keep.tile([P, ROWS // P, F], BF16)
+        w2_raw = keep.tile([P, 2, PASSES, PACK, K_PASS], BF16)
+        wo_raw = keep.tile([P, PASSES, PACK, ED], BF16)
+        pln_raw = keep.tile([P, ROWS // P, ED], BF16)
+        node_raw = keep.tile([P, P], BF16)
+        vec_raw = keep.tile([P, 3, ED], BF16)
+        w2_grouped = keep.tile([P, 2, PASSES, K_PASS, PACK], BF16, align_bytes=64)
+        w2_words = keep.tile([P, 2, PASSES, K_PASS], U32, align_bytes=64)
+        w2_scales = keep.tile([P, 2, PASSES, K_PASS], U8, align_bytes=64)
+        wo_grouped = keep.tile([P, PASSES, ED, PACK], BF16, align_bytes=64)
+        wo_words = keep.tile([P, PASSES, ED], U32, align_bytes=64)
+        wo_scales = keep.tile([P, PASSES, ED], U8, align_bytes=64)
+        s_planes = keep.tile([P, MD // P, ROWS], BF16)
+        edge_add = keep.tile([P, PACK, ROWS], F32)
+        node_add = keep.tile([P, PACK, NODES], F32)
+        node_t = keep.tile([P, 72], F32)
+        neg_b2 = keep.tile([P, MD // P], F32)
+        ones = keep.tile([P, P], BF16)
+        ident_f32 = keep.tile([P, P], F32)
+        ident_bf16 = keep.tile([P, P], BF16)
+        eps = keep.tile([P, 1], F32)
+        table_warm = keep.tile([P, 1], F32)
+        bo_all = keep.tile([P, ED], F32)
+        gain_all = keep.tile([P, ED], F32)
 
-        def copy_on(eng, dst, src):
-            if eng == "V":
-                nc.vector.tensor_copy(out=dst, in_=src)
-            else:
-                nc.scalar.copy(out=dst, in_=src)
-
-        def regroup(eng, dst, src):
-            copy_on(
-                eng,
-                dst.rearrange("p (c i) t -> p c t i", i=4),
-                src.rearrange("p t (c i) -> p c t i", i=4),
+        def interleave(copy, dst, src):
+            copy(
+                out=dst.rearrange("p (c i) t -> p c t i", i=4),
+                in_=src.rearrange("p t (c i) -> p c t i", i=4),
             )
 
-        def quantise(codes, scales, grouped):
-            nc.vector.quantize_mx(out=codes.bitcast(FP8X4), scales=scales, in_=grouped)
+        def quantise(words, scales, grouped):
+            nc.vector.quantize_mx(out=words.bitcast(FP8X4), scales=scales, in_=grouped)
 
-        nc.vector.memset(small[:], 0.0)
-        nc.vector.memset(vecs[:], 0.0)
-        nc.vector.memset(ones_b[:], 1.0)
-        nc.vector.memset(eps_t[:], EPS)
-        make_identity(nc, ident_f[:])
-        make_identity(nc, ident_b[:])
-        nc.scalar.activation(out=warm[:], in_=eps_t[:], func=ACT.Abs_reciprocal_sqrt)
+        nc.vector.memset(node_raw[:], 0.0)
+        nc.vector.memset(vec_raw[:], 0.0)
+        nc.vector.memset(ones[:], 1.0)
+        nc.vector.memset(eps[:], EPS)
+        make_identity(nc, ident_f32[:])
+        make_identity(nc, ident_bf16[:])
+        nc.scalar.activation(out=table_warm[:], in_=eps[:], func=ACT.Abs_reciprocal_sqrt)
 
-        for kind, idx in LOADS:
-            if kind == "W2":
-                for g in range(2):
-                    for u in range(2):
-                        k0 = 512 * g + 256 * u
-                        nc.sync.dma_start(
-                            out=w2_raw[:, idx, g, 2 * u : 2 * u + 2, :],
-                            in_=W2[k0 : k0 + 256, HALF * idx : HALF * (idx + 1)].rearrange(
-                                "(q e) n -> q e n", e=2
-                            ),
-                        )
-            elif kind == "XD":
-                nc.sync.dma_start(out=small[0:32, :], in_=xd2[:, 0:P])
-                nc.sync.dma_start(out=small[32:64, :], in_=xd2[:, P : 2 * P])
-                nc.sync.dma_start(out=small[64:72, :], in_=b2.rearrange("(m p) -> m p", p=P))
-            elif kind == "VEC":
-                for c, vec in enumerate((bo, ln_out_g, ln_out_b)):
-                    nc.sync.dma_start(out=vecs[0:1, c, :], in_=vec.rearrange("(o f) -> o f", o=1))
-            elif kind == "HID":
-                nc.sync.dma_start(
-                    out=hid_raw[:, 2 * idx : 2 * idx + 2, :],
-                    in_=hid2[256 * idx : 256 * (idx + 1), :].rearrange("(a p) k -> p a k", p=P),
-                )
-            elif kind == "PL":
-                nc.sync.dma_start(
-                    out=pl_raw[:, 4 * idx : 4 * idx + 4, :],
-                    in_=pl2[HALF * idx : HALF * (idx + 1), :].rearrange("(a p) f -> p a f", p=P),
-                )
-            else:
-                for g in range(2):
+        def load_w2(half):
+            for g in range(PASSES):
+                for u in range(2):
+                    k0 = K_PASS * g + 256 * u
                     nc.sync.dma_start(
-                        out=wo_raw[:, g, :, :],
-                        in_=Wo[512 * g : 512 * (g + 1), :].rearrange("(t p) n -> p t n", p=P),
+                        out=w2_raw[:, half, g, 2 * u : 2 * u + 2, :],
+                        in_=W2[k0 : k0 + 256, K_PASS * half : K_PASS * (half + 1)].rearrange(
+                            "(q e) n -> q e n", e=2
+                        ),
                     )
 
-        def prep_w2(nb):
-            for g in range(2):
-                regroup(R_ENGINE[2 * nb + g], w2_gr[:, nb, g, :, :], w2_raw[:, nb, g, :, :])
-            quantise(
-                w2_codes[:, nb, :, :].rearrange("p g n -> p (g n)"),
-                w2_sc[:, nb, :, :].rearrange("p g n -> p (g n)"),
-                w2_gr[:, nb, :, :, :].rearrange("p g n t -> p (g n t)"),
+        def load_hid(part):
+            tiles = HID_LOAD // P
+            nc.sync.dma_start(
+                out=hid_raw[:, tiles * part : tiles * (part + 1), :],
+                in_=hid_rows[HID_LOAD * part : HID_LOAD * (part + 1), :].rearrange(
+                    "(a p) k -> p a k", p=P
+                ),
             )
 
-        def prep_small():
-            sm_ps = psum.tile([P, P], BF16, tag="A", bufs=3, name="sm_ps")
-            nc.tensor.transpose(sm_ps[:], small[:], ident_b[:])
-            nc.scalar.copy(out=smT[:], in_=sm_ps[:, 0:72])
-            nc.vector.tensor_scalar_mul(nb2[:], smT[:, 64:72], -1.0)
-            for m in range(4):
-                x0 = 32 * (m % 2)
-                nc.vector.tensor_scalar_add(
-                    out=xb[:, m, :], in0=smT[:, x0 : x0 + 32], scalar1=smT[:, 64 + m : 65 + m]
+        def load_node_inputs():
+            nc.sync.dma_start(out=node_raw[0:32, :], in_=xd_rows[:, 0:P])
+            nc.sync.dma_start(out=node_raw[32:64, :], in_=xd_rows[:, P : 2 * P])
+            nc.sync.dma_start(out=node_raw[64:72, :], in_=b2.rearrange("(m p) -> m p", p=P))
+
+        def load_p_ln(part):
+            tiles = PLN_LOAD // P
+            nc.sync.dma_start(
+                out=pln_raw[:, tiles * part : tiles * (part + 1), :],
+                in_=pln_rows[PLN_LOAD * part : PLN_LOAD * (part + 1), :].rearrange(
+                    "(a p) f -> p a f", p=P
+                ),
+            )
+
+        def load_row_vectors():
+            for c, vec in enumerate((bo, ln_out_g, ln_out_b)):
+                nc.sync.dma_start(out=vec_raw[0:1, c, :], in_=vec.rearrange("(o f) -> o f", o=1))
+
+        def load_wo():
+            for g in range(PASSES):
+                nc.sync.dma_start(
+                    out=wo_raw[:, g, :, :],
+                    in_=Wo[K_PASS * g : K_PASS * (g + 1), :].rearrange("(t p) n -> p t n", p=P),
                 )
-            for c, dst in enumerate((bo_bc, g_bc)):
-                bc_ps = psum.tile([P, ED], F32, tag="pl", bufs=2, name="bc_ps")
-                nc.tensor.matmul(bc_ps[:], lhsT=ones_b[:], rhs=vecs[:, c, :], start=True, stop=True)
-                nc.scalar.copy(out=dst[:], in_=bc_ps[:])
 
-        def prep_wo():
-            for g in range(2):
-                regroup(WO_ENGINE[g], wo_gr[:, g, :, :], wo_raw[:, g, :, :])
+        load_w2(0)
+        load_hid(0)
+        load_hid(1)
+        load_node_inputs()
+        load_w2(1)
+        load_p_ln(0)
+        load_row_vectors()
+        load_wo()
+        load_hid(2)
+        load_hid(3)
+        load_p_ln(1)
+
+        def prepare_w2(half):
+            for g in range(PASSES):
+                interleave(nc.vector.tensor_copy, w2_grouped[:, half, g, :, :], w2_raw[:, half, g, :, :])
             quantise(
-                wo_codes[:].rearrange("p g n -> p (g n)"),
-                wo_sc[:].rearrange("p g n -> p (g n)"),
-                wo_gr[:].rearrange("p g n t -> p (g n t)"),
+                w2_words[:, half, :, :].rearrange("p g n -> p (g n)"),
+                w2_scales[:, half, :, :].rearrange("p g n -> p (g n)"),
+                w2_grouped[:, half, :, :, :].rearrange("p g n t -> p (g n t)"),
             )
 
-        def prep_pl(h):
-            for tp in range(2):
-                plT = psum.tile([P, 2, HALF], BF16, tag="A", bufs=3, name="plT")
-                for tl in range(2):
-                    t = 2 * tp + tl
-                    for al in range(4):
+        def prepare_wo():
+            for g in range(PASSES):
+                interleave(nc.vector.tensor_copy, wo_grouped[:, g, :, :], wo_raw[:, g, :, :])
+            quantise(
+                wo_words[:].rearrange("p g n -> p (g n)"),
+                wo_scales[:].rearrange("p g n -> p (g n)"),
+                wo_grouped[:].rearrange("p g n t -> p (g n t)"),
+            )
+
+        def prepare_small_inputs():
+            node_ps = psum.tile([P, P], BF16, tag="t", bufs=BANKS_T, name="node_ps")
+            nc.tensor.transpose(node_ps[:], node_raw[:], ident_bf16[:])
+            nc.scalar.copy(out=node_t[:], in_=node_ps[:, 0:72])
+            nc.vector.tensor_scalar_mul(neg_b2[:], node_t[:, 64:72], -1.0)
+            for m in range(PACK):
+                x0 = NODES * (m % 2)
+                nc.vector.tensor_scalar_add(
+                    out=node_add[:, m, :],
+                    in0=node_t[:, x0 : x0 + NODES],
+                    scalar1=node_t[:, 64 + m : 65 + m],
+                )
+            for c, dst in enumerate((bo_all, gain_all)):
+                spread = psum.tile([P, ED], F32, tag="b", bufs=BANKS_B, name="spread")
+                nc.tensor.matmul(spread[:], lhsT=ones[:], rhs=vec_raw[:, c, :], start=True, stop=True)
+                nc.scalar.copy(out=dst[:], in_=spread[:])
+
+        def prepare_edge_add(part):
+            tiles = PLN_LOAD // P
+            for pair in range(2):
+                pln_t = psum.tile([P, 2, PLN_LOAD], BF16, tag="t", bufs=BANKS_T, name="pln_t")
+                for c in range(2):
+                    t = 2 * pair + c
+                    for a in range(tiles):
                         nc.tensor.transpose(
-                            plT[:, tl, P * al : P * (al + 1)],
-                            pl_raw[:, 4 * h + al, P * t : P * (t + 1)],
-                            ident_b[:],
+                            pln_t[:, c, P * a : P * (a + 1)],
+                            pln_raw[:, tiles * part + a, P * t : P * (t + 1)],
+                            ident_bf16[:],
                         )
-                for tl in range(2):
-                    t = 2 * tp + tl
+                for c in range(2):
+                    t = 2 * pair + c
                     nc.scalar.activation(
-                        out=zb[:, t, HALF * h : HALF * (h + 1)],
-                        in_=plT[:, tl, :],
+                        out=edge_add[:, t, PLN_LOAD * part : PLN_LOAD * (part + 1)],
+                        in_=pln_t[:, c, :],
                         func=ACT.Identity,
-                        bias=smT[:, 68 + t : 69 + t],
+                        bias=node_t[:, 68 + t : 69 + t],
                         scale=1.0,
                     )
 
-        hid_codes = {}
-        hid_sc = {}
-        s_codes = {}
-        s_sc = {}
-        s_grs = {}
+        hid_words, hid_scales = {}, {}
+        s_grouped, s_words, s_scales = {}, {}, {}
 
-        def prep_hid(b):
-            r0, n = BLOCKS[b]
-            gr = keep.tile([P, 2, n, 2], F32, align_bytes=64, name="hid_gr%d" % b)
-            hid_codes[b] = keep.tile([P, 2, n], U32, align_bytes=64, name="hid_codes%d" % b)
-            hid_sc[b] = keep.tile([P, 2, n], U8, align_bytes=64, name="hid_sc%d" % b)
-            for l in range(n // 256):
-                for g in range(2):
-                    xt = psum.tile([P, 2, 2, P], F32, tag="A", bufs=3, name="xt")
-                    for al in range(2):
-                        words = hid_raw[:, r0 // P + 2 * l + al, :].bitcast(F32)
+        def prepare_hid(b):
+            first, n = BLOCKS[b]
+            grouped = keep.tile([P, PASSES, n, 2], F32, align_bytes=64, name="hid_grouped%d" % b)
+            hid_words[b] = keep.tile([P, PASSES, n], U32, align_bytes=64, name="hid_words%d" % b)
+            hid_scales[b] = keep.tile([P, PASSES, n], U8, align_bytes=64, name="hid_scales%d" % b)
+            for part in range(n // 256):
+                for g in range(PASSES):
+                    hid_t = psum.tile([P, 2, 2, P], F32, tag="t", bufs=BANKS_T, name="hid_t")
+                    for a in range(2):
+                        pairs_of_k = hid_raw[:, first // P + 2 * part + a, :].bitcast(F32)
                         for u in range(2):
-                            w0 = 256 * g + 128 * u
-                            nc.tensor.transpose(xt[:, al, u, :], words[:, w0 : w0 + P], ident_f[:])
-                    copy_on(
-                        EH_ENGINE,
-                        gr[:, g, 256 * l : 256 * (l + 1), :].rearrange("p (a r) u -> p a r u", a=2),
-                        xt[:].rearrange("p a u r -> p a r u"),
+                            w0 = 256 * g + P * u
+                            nc.tensor.transpose(
+                                hid_t[:, a, u, :], pairs_of_k[:, w0 : w0 + P], ident_f32[:]
+                            )
+                    nc.scalar.copy(
+                        out=grouped[:, g, 256 * part : 256 * (part + 1), :].rearrange(
+                            "p (a r) u -> p a r u", a=2
+                        ),
+                        in_=hid_t[:].rearrange("p a u r -> p a r u"),
                     )
             quantise(
-                hid_codes[b][:].rearrange("p g r -> p (g r)"),
-                hid_sc[b][:].rearrange("p g r -> p (g r)"),
-                gr[:].bitcast(BF16).rearrange("p g r t -> p (g r t)"),
+                hid_words[b][:].rearrange("p g r -> p (g r)"),
+                hid_scales[b][:].rearrange("p g r -> p (g r)"),
+                grouped[:].bitcast(BF16).rearrange("p g r t -> p (g r t)"),
             )
 
-        def stage1(b, g2):
-            r0, n = BLOCKS[b]
-            rows = slice(r0, r0 + n)
-            i0 = r0 // NODES
-            ni = n // NODES
-            if g2 == 0:
-                s_grs[b] = keep.tile([P, 2, n, 4], BF16, align_bytes=64, name="s_gr%d" % b)
-                s_codes[b] = keep.tile([P, 2, n], U32, align_bytes=64, name="s_codes%d" % b)
-                s_sc[b] = keep.tile([P, 2, n], U8, align_bytes=64, name="s_sc%d" % b)
-            for t in range(4):
-                m = 4 * g2 + t
-                acc = psum.tile([P, n], F32, tag="s1", bufs=3, name="acc")
+        def first_stage(b, half):
+            first, n = BLOCKS[b]
+            rows = slice(first, first + n)
+            i0, ni = first // NODES, n // NODES
+            if half == 0:
+                s_grouped[b] = keep.tile([P, PASSES, n, PACK], BF16, align_bytes=64, name="s_grouped%d" % b)
+                s_words[b] = keep.tile([P, PASSES, n], U32, align_bytes=64, name="s_words%d" % b)
+                s_scales[b] = keep.tile([P, PASSES, n], U8, align_bytes=64, name="s_scales%d" % b)
+            for t in range(PACK):
+                m = PACK * half + t
+                x = psum.tile([P, n], F32, tag="s", bufs=BANKS_S, name="x")
                 cols = slice(P * t, P * (t + 1))
-                for g in range(2):
+                for g in range(PASSES):
                     nc.tensor.matmul_mx(
-                        out=acc[:],
-                        lhsT=w2_codes[:, g2, g, cols].bitcast(FP8X4),
-                        lhsT_scale=w2_sc[:, g2, g, cols],
-                        rhs=hid_codes[b][:, g, :].bitcast(FP8X4),
-                        rhs_scale=hid_sc[b][:, g, :],
+                        out=x[:],
+                        lhsT=w2_words[:, half, g, cols].bitcast(FP8X4),
+                        lhsT_scale=w2_scales[:, half, g, cols],
+                        rhs=hid_words[b][:, g, :].bitcast(FP8X4),
+                        rhs_scale=hid_scales[b][:, g, :],
                         start=(g == 0),
-                        stop=(g == 1),
+                        stop=(g == PASSES - 1),
                     )
                 if m < 2:
-                    add = xb[:, m, i0 : i0 + ni].unsqueeze(2).to_broadcast([P, ni, NODES])
+                    add = node_add[:, m, i0 : i0 + ni].unsqueeze(2).to_broadcast([P, ni, NODES])
                 elif m < 4:
-                    add = xb[:, m, :].unsqueeze(1).to_broadcast([P, ni, NODES])
+                    add = node_add[:, m, :].unsqueeze(1).to_broadcast([P, ni, NODES])
                 else:
-                    add = zb[:, m - 4, rows].rearrange("p (i j) -> p i j", j=NODES)
+                    add = edge_add[:, m - 4, rows].rearrange("p (i j) -> p i j", j=NODES)
                 nc.vector.scalar_tensor_tensor(
-                    out=s_raw[:, m, rows].rearrange("p (i j) -> p i j", j=NODES),
-                    in0=acc[:].rearrange("p (i j) -> p i j", j=NODES),
-                    scalar=nb2[:, m : m + 1],
+                    out=s_planes[:, m, rows].rearrange("p (i j) -> p i j", j=NODES),
+                    in0=x[:].rearrange("p (i j) -> p i j", j=NODES),
+                    scalar=neg_b2[:, m : m + 1],
                     in1=add,
                     op0=ALU.max,
                     op1=ALU.add,
                 )
-            regroup(H_ENGINE[b][g2], s_grs[b][:, g2, :, :], s_raw[:, 4 * g2 : 4 * g2 + 4, rows])
-
-        def quant_s(b):
-            quantise(
-                s_codes[b][:].rearrange("p g r -> p (g r)"),
-                s_sc[b][:].rearrange("p g r -> p (g r)"),
-                s_grs[b][:].rearrange("p g r t -> p (g r t)"),
+            interleave(
+                nc.scalar.copy, s_grouped[b][:, half, :, :], s_planes[:, PACK * half : PACK * (half + 1), rows]
             )
 
-        def stage2(b, al):
-            r0, n = BLOCKS[b]
-            a = r0 // P + al
-            rows = slice(P * al, P * (al + 1))
-            z = psum.tile([P, ED], F32, tag="A", bufs=3, name="z")
-            for g2 in range(2):
+        def quantise_s(b):
+            quantise(
+                s_words[b][:].rearrange("p g r -> p (g r)"),
+                s_scales[b][:].rearrange("p g r -> p (g r)"),
+                s_grouped[b][:].rearrange("p g r t -> p (g r t)"),
+            )
+
+        def second_stage(b, a):
+            first = BLOCKS[b][0]
+            tile_index = first // P + a
+            rows = slice(P * a, P * (a + 1))
+            z = psum.tile([P, ED], F32, tag="t", bufs=BANKS_T, name="z")
+            for g in range(PASSES):
                 nc.tensor.matmul_mx(
                     out=z[:],
-                    lhsT=s_codes[b][:, g2, rows].bitcast(FP8X4),
-                    lhsT_scale=s_sc[b][:, g2, rows],
-                    rhs=wo_codes[:, g2, :].bitcast(FP8X4),
-                    rhs_scale=wo_sc[:, g2, :],
-                    start=(g2 == 0),
-                    stop=(g2 == 1),
+                    lhsT=s_words[b][:, g, rows].bitcast(FP8X4),
+                    lhsT_scale=s_scales[b][:, g, rows],
+                    rhs=wo_words[:, g, :].bitcast(FP8X4),
+                    rhs_scale=wo_scales[:, g, :],
+                    start=(g == 0),
+                    stop=(g == PASSES - 1),
                 )
-            plb = psum.tile([P, ED], F32, tag="pl", bufs=2, name="plb")
-            nc.tensor.matmul(plb[:], lhsT=ident_b[:], rhs=pl_raw[:, a, :], start=True, stop=False)
-            nc.tensor.matmul(plb[:], lhsT=ones_b[:], rhs=vecs[:, 2, :], start=False, stop=True)
-            u = work.tile([P, ED], F32, tag="u", bufs=4, name="u")
-            su = work.tile([P, 1], F32, tag="su", bufs=4, name="su")
-            nc.vector.scalar_tensor_tensor(
-                out=u[:], in0=z[:], scalar=1.0, in1=bo_bc[:], op0=ALU.mult, op1=ALU.add, accum_out=su[:]
+            shift = psum.tile([P, ED], F32, tag="b", bufs=BANKS_B, name="shift")
+            nc.tensor.matmul(
+                shift[:], lhsT=ident_bf16[:], rhs=pln_raw[:, tile_index, :], start=True, stop=False
             )
-            nmu = work.tile([P, 1], F32, tag="nmu", bufs=4, name="nmu")
-            nc.scalar.mul(out=nmu[:], in_=su[:], mul=-1.0 / ED)
-            sq = work.tile([P, ED], BF16, tag="sq", bufs=2, name="sq")
-            ssq = work.tile([P, 1], F32, tag="ssq", bufs=4, name="ssq")
+            nc.tensor.matmul(shift[:], lhsT=ones[:], rhs=vec_raw[:, 2, :], start=False, stop=True)
+            u = work.tile([P, ED], F32, tag="u", bufs=LN_DEPTH, name="u")
+            u_sum = work.tile([P, 1], F32, tag="u_sum", bufs=LN_DEPTH, name="u_sum")
+            nc.vector.scalar_tensor_tensor(
+                out=u[:], in0=z[:], scalar=1.0, in1=bo_all[:], op0=ALU.mult, op1=ALU.add,
+                accum_out=u_sum[:],
+            )
+            neg_mean = work.tile([P, 1], F32, tag="neg_mean", bufs=LN_DEPTH, name="neg_mean")
+            nc.scalar.mul(out=neg_mean[:], in_=u_sum[:], mul=-1.0 / ED)
+            squares = work.tile([P, ED], BF16, tag="squares", bufs=2, name="squares")
+            sq_sum = work.tile([P, 1], F32, tag="sq_sum", bufs=LN_DEPTH, name="sq_sum")
             nc.scalar.activation(
-                out=sq[:], in_=u[:], func=ACT.Square, bias=nmu[:], scale=1.0, accum_out=ssq[:]
+                out=squares[:], in_=u[:], func=ACT.Square, bias=neg_mean[:], scale=1.0,
+                accum_out=sq_sum[:],
             )
-            rstd = work.tile([P, 1], F32, tag="rstd", bufs=4, name="rstd")
+            rstd = work.tile([P, 1], F32, tag="rstd", bufs=LN_DEPTH, name="rstd")
             nc.scalar.activation(
-                out=rstd[:], in_=ssq[:], func=ACT.Abs_reciprocal_sqrt, bias=eps_t[:], scale=1.0 / ED
+                out=rstd[:], in_=sq_sum[:], func=ACT.Abs_reciprocal_sqrt, bias=eps[:], scale=1.0 / ED
             )
-            t1 = work.tile([P, ED], F32, tag="t1", bufs=4, name="t1")
+            res = work.tile([P, ED], F32, tag="res", bufs=LN_DEPTH, name="res")
             nc.vector.scalar_tensor_tensor(
-                out=t1[:], in0=u[:], scalar=nmu[:], in1=g_bc[:], op0=ALU.add, op1=ALU.mult
+                out=res[:], in0=u[:], scalar=neg_mean[:], in1=gain_all[:], op0=ALU.add, op1=ALU.mult
             )
             nc.vector.scalar_tensor_tensor(
-                out=t1[:], in0=t1[:], scalar=rstd[:], in1=plb[:], op0=ALU.mult, op1=ALU.add
+                out=res[:], in0=res[:], scalar=rstd[:], in1=shift[:], op0=ALU.mult, op1=ALU.add
             )
-            nc.sync.dma_start(out=out2[P * a : P * (a + 1), :], in_=t1[:])
+            nc.sync.dma_start(out=out_rows[P * tile_index : P * (tile_index + 1), :], in_=res[:])
 
-        prep_w2(0)
-        prep_small()
-        prep_hid(0)
-        stage1(0, 0)
-        prep_w2(1)
-        prep_pl(0)
-        stage1(0, 1)
-        quant_s(0)
-        prep_wo()
+        prepare_w2(0)
+        prepare_small_inputs()
+        prepare_hid(0)
+        first_stage(0, 0)
+        prepare_w2(1)
+        prepare_edge_add(0)
+        first_stage(0, 1)
+        quantise_s(0)
+        prepare_wo()
         for b in range(len(BLOCKS)):
             if b + 1 < len(BLOCKS):
-                prep_hid(b + 1)
-                if BLOCKS[b + 1][0] + BLOCKS[b + 1][1] > HALF and BLOCKS[b + 1][0] <= HALF:
-                    prep_pl(1)
-                stage1(b + 1, 0)
-                stage1(b + 1, 1)
-                quant_s(b + 1)
-            for al in range(BLOCKS[b][1] // P):
-                stage2(b, al)
+                first, n = BLOCKS[b + 1]
+                prepare_hid(b + 1)
+                if first <= PLN_LOAD < first + n:
+                    prepare_edge_add(1)
+                first_stage(b + 1, 0)
+                first_stage(b + 1, 1)
+                quantise_s(b + 1)
+            for a in range(BLOCKS[b][1] // P):
+                second_stage(b, a)

@@ -27,7 +27,7 @@ FLOPS = 2 * ROWS * F * MD + 2 * ROWS * MD * ED
 
 BLOCKS = ((0, 512), (512, 512))
 
-BANKS_T, BANKS_S, BANKS_B = 3, 3, 2
+BANKS_T, BANKS_S, BANKS_B = 2, 4, 2
 LN_DEPTH = 4
 
 
@@ -57,11 +57,10 @@ def tile_edgeupdaterwrapper_v01_pb_kernel(
         wo_grouped = keep.tile([P, PASSES, ED, PACK], BF16, align_bytes=64)
         wo_words = keep.tile([P, PASSES, ED], U32, align_bytes=64)
         wo_scales = keep.tile([P, PASSES, ED], U8, align_bytes=64)
-        s_planes = keep.tile([P, MD // P, ROWS], BF16)
-        edge_add = keep.tile([P, PACK, ROWS], F32)
+        s_planes = keep.tile([P, PACK, ROWS], BF16)
         node_add = keep.tile([P, PACK, NODES], F32)
         node_t = keep.tile([P, 72], F32)
-        neg_b2 = keep.tile([P, MD // P], F32)
+        neg_b2 = keep.tile([P, PACK], F32)
         ones = keep.tile([P, P], BF16)
         ident_f32 = keep.tile([P, P], F32)
         ident_bf16 = keep.tile([P, P], BF16)
@@ -87,16 +86,15 @@ def tile_edgeupdaterwrapper_v01_pb_kernel(
         make_identity(nc, ident_bf16[:])
         nc.scalar.activation(out=table_warm[:], in_=eps[:], func=ACT.Abs_reciprocal_sqrt)
 
-        def load_w2(half):
-            for g in range(PASSES):
-                for u in range(2):
-                    k0 = K_PASS * g + 256 * u
-                    nc.sync.dma_start(
-                        out=w2_raw[:, half, g, 2 * u : 2 * u + 2, :],
-                        in_=W2[k0 : k0 + 256, K_PASS * half : K_PASS * (half + 1)].rearrange(
-                            "(q e) n -> q e n", e=2
-                        ),
-                    )
+        def load_w2(half, g):
+            for u in range(2):
+                k0 = K_PASS * g + 256 * u
+                nc.sync.dma_start(
+                    out=w2_raw[:, half, g, 2 * u : 2 * u + 2, :],
+                    in_=W2[k0 : k0 + 256, K_PASS * half : K_PASS * (half + 1)].rearrange(
+                        "(q e) n -> q e n", e=2
+                    ),
+                )
 
         def load_hid(part):
             tiles = HID_LOAD // P
@@ -132,25 +130,26 @@ def tile_edgeupdaterwrapper_v01_pb_kernel(
                     in_=Wo[K_PASS * g : K_PASS * (g + 1), :].rearrange("(t p) n -> p t n", p=P),
                 )
 
-        load_w2(0)
+        load_w2(1, 0)
         load_hid(0)
+        load_w2(1, 1)
         load_hid(1)
         load_node_inputs()
-        load_w2(1)
         load_p_ln(0)
+        load_w2(0, 0)
+        load_w2(0, 1)
         load_row_vectors()
-        load_wo()
         load_hid(2)
         load_hid(3)
+        load_wo()
         load_p_ln(1)
 
-        def prepare_w2(half):
-            for g in range(PASSES):
-                interleave(nc.vector.tensor_copy, w2_grouped[:, half, g, :, :], w2_raw[:, half, g, :, :])
+        def prepare_w2(half, g):
+            interleave(nc.vector.tensor_copy, w2_grouped[:, half, g, :, :], w2_raw[:, half, g, :, :])
             quantise(
-                w2_words[:, half, :, :].rearrange("p g n -> p (g n)"),
-                w2_scales[:, half, :, :].rearrange("p g n -> p (g n)"),
-                w2_grouped[:, half, :, :, :].rearrange("p g n t -> p (g n t)"),
+                w2_words[:, half, g, :],
+                w2_scales[:, half, g, :],
+                w2_grouped[:, half, g, :, :].rearrange("p n t -> p (n t)"),
             )
 
         def prepare_wo():
@@ -166,7 +165,7 @@ def tile_edgeupdaterwrapper_v01_pb_kernel(
             node_ps = psum.tile([P, P], BF16, tag="t", bufs=BANKS_T, name="node_ps")
             nc.tensor.transpose(node_ps[:], node_raw[:], ident_bf16[:])
             nc.scalar.copy(out=node_t[:], in_=node_ps[:, 0:72])
-            nc.vector.tensor_scalar_mul(neg_b2[:], node_t[:, 64:72], -1.0)
+            nc.vector.tensor_scalar_mul(neg_b2[:], node_t[:, 64:68], -1.0)
             for m in range(PACK):
                 x0 = NODES * (m % 2)
                 nc.vector.tensor_scalar_add(
@@ -174,35 +173,34 @@ def tile_edgeupdaterwrapper_v01_pb_kernel(
                     in0=node_t[:, x0 : x0 + NODES],
                     scalar1=node_t[:, 64 + m : 65 + m],
                 )
+        def prepare_row_vectors():
             for c, dst in enumerate((bo_all, gain_all)):
-                spread = psum.tile([P, ED], F32, tag="b", bufs=BANKS_B, name="spread")
+                spread = psum.tile([P, ED], F32, tag="t", bufs=BANKS_T, name="spread")
                 nc.tensor.matmul(spread[:], lhsT=ones[:], rhs=vec_raw[:, c, :], start=True, stop=True)
                 nc.scalar.copy(out=dst[:], in_=spread[:])
 
-        def prepare_edge_add(part):
-            tiles = PLN_LOAD // P
-            for pair in range(2):
-                pln_t = psum.tile([P, 2, PLN_LOAD], BF16, tag="t", bufs=BANKS_T, name="pln_t")
-                for c in range(2):
-                    t = 2 * pair + c
-                    for a in range(tiles):
+        def prepare_edge(b):
+            first, n = BLOCKS[b]
+            edge_t[b] = []
+            for part in range(n // 256):
+                pln_t = psum.tile([P, PACK, 256], BF16, tag="b", bufs=BANKS_B, name="pln_t")
+                for t in range(PACK):
+                    for a in range(2):
                         nc.tensor.transpose(
-                            pln_t[:, c, P * a : P * (a + 1)],
-                            pln_raw[:, tiles * part + a, P * t : P * (t + 1)],
+                            pln_t[:, t, P * a : P * (a + 1)],
+                            pln_raw[:, first // P + 2 * part + a, P * t : P * (t + 1)],
                             ident_bf16[:],
                         )
-                for c in range(2):
-                    t = 2 * pair + c
-                    nc.scalar.activation(
-                        out=edge_add[:, t, PLN_LOAD * part : PLN_LOAD * (part + 1)],
-                        in_=pln_t[:, c, :],
-                        func=ACT.Identity,
-                        bias=node_t[:, 68 + t : 69 + t],
-                        scale=1.0,
-                    )
+                edge_t[b].append(pln_t)
 
-        hid_words, hid_scales = {}, {}
-        s_grouped, s_words, s_scales = {}, {}, {}
+        hid_grouped, hid_words, hid_scales = {}, {}, {}
+        edge_t = {}
+        relu, s_grouped, s_words, s_scales = {}, {}, {}, {}
+        for b, (first, n) in enumerate(BLOCKS):
+            relu[b] = keep.tile([P, n // 4, PACK, 4], F32, name="relu%d" % b)
+            s_grouped[b] = keep.tile([P, PASSES, n, PACK], BF16, align_bytes=64, name="s_grouped%d" % b)
+            s_words[b] = keep.tile([P, PASSES, n], U32, align_bytes=64, name="s_words%d" % b)
+            s_scales[b] = keep.tile([P, PASSES, n], U8, align_bytes=64, name="s_scales%d" % b)
 
         def prepare_hid(b):
             first, n = BLOCKS[b]
@@ -225,62 +223,85 @@ def tile_edgeupdaterwrapper_v01_pb_kernel(
                         ),
                         in_=hid_t[:].rearrange("p a u r -> p a r u"),
                     )
-            quantise(
-                hid_words[b][:].rearrange("p g r -> p (g r)"),
-                hid_scales[b][:].rearrange("p g r -> p (g r)"),
-                grouped[:].bitcast(BF16).rearrange("p g r t -> p (g r t)"),
-            )
+            hid_grouped[b] = grouped
 
-        def first_stage(b, half):
+        def quantise_hid(b):
+            for g in range(PASSES):
+                quantise(
+                    hid_words[b][:, g, :],
+                    hid_scales[b][:, g, :],
+                    hid_grouped[b][:, g, :, :].bitcast(BF16).rearrange("p r t -> p (r t)"),
+                )
+
+        def first_matmul(b, m):
+            n = BLOCKS[b][1]
+            half, t = divmod(m, PACK)
+            x = psum.tile([P, n], F32, tag="s", bufs=BANKS_S, name="x")
+            cols = slice(P * t, P * (t + 1))
+            for g in range(PASSES):
+                nc.tensor.matmul_mx(
+                    out=x[:],
+                    lhsT=w2_words[:, half, g, cols].bitcast(FP8X4),
+                    lhsT_scale=w2_scales[:, half, g, cols],
+                    rhs=hid_words[b][:, g, :].bitcast(FP8X4),
+                    rhs_scale=hid_scales[b][:, g, :],
+                    start=(g == 0),
+                    stop=(g == PASSES - 1),
+                )
+            return x
+
+        def node_chunk(b, m):
             first, n = BLOCKS[b]
             rows = slice(first, first + n)
             i0, ni = first // NODES, n // NODES
-            if half == 0:
-                s_grouped[b] = keep.tile([P, PASSES, n, PACK], BF16, align_bytes=64, name="s_grouped%d" % b)
-                s_words[b] = keep.tile([P, PASSES, n], U32, align_bytes=64, name="s_words%d" % b)
-                s_scales[b] = keep.tile([P, PASSES, n], U8, align_bytes=64, name="s_scales%d" % b)
-            for t in range(PACK):
-                m = PACK * half + t
-                x = psum.tile([P, n], F32, tag="s", bufs=BANKS_S, name="x")
-                cols = slice(P * t, P * (t + 1))
-                for g in range(PASSES):
-                    nc.tensor.matmul_mx(
-                        out=x[:],
-                        lhsT=w2_words[:, half, g, cols].bitcast(FP8X4),
-                        lhsT_scale=w2_scales[:, half, g, cols],
-                        rhs=hid_words[b][:, g, :].bitcast(FP8X4),
-                        rhs_scale=hid_scales[b][:, g, :],
-                        start=(g == 0),
-                        stop=(g == PASSES - 1),
-                    )
-                if m < 2:
-                    add = node_add[:, m, i0 : i0 + ni].unsqueeze(2).to_broadcast([P, ni, NODES])
-                elif m < 4:
-                    add = node_add[:, m, :].unsqueeze(1).to_broadcast([P, ni, NODES])
-                else:
-                    add = edge_add[:, m - 4, rows].rearrange("p (i j) -> p i j", j=NODES)
-                nc.vector.scalar_tensor_tensor(
-                    out=s_planes[:, m, rows].rearrange("p (i j) -> p i j", j=NODES),
-                    in0=x[:].rearrange("p (i j) -> p i j", j=NODES),
-                    scalar=neg_b2[:, m : m + 1],
-                    in1=add,
-                    op0=ALU.max,
-                    op1=ALU.add,
-                )
-            interleave(
-                nc.scalar.copy, s_grouped[b][:, half, :, :], s_planes[:, PACK * half : PACK * (half + 1), rows]
+            x = first_matmul(b, m)
+            if m < 2:
+                add = node_add[:, m, i0 : i0 + ni].unsqueeze(2).to_broadcast([P, ni, NODES])
+            else:
+                add = node_add[:, m, :].unsqueeze(1).to_broadcast([P, ni, NODES])
+            nc.vector.scalar_tensor_tensor(
+                out=s_planes[:, m, rows].rearrange("p (i j) -> p i j", j=NODES),
+                in0=x[:].rearrange("p (i j) -> p i j", j=NODES),
+                scalar=neg_b2[:, m : m + 1],
+                in1=add,
+                op0=ALU.max,
+                op1=ALU.add,
             )
 
-        def quantise_s(b):
+        def interleave_nodes(b):
+            first, n = BLOCKS[b]
+            interleave(nc.scalar.copy, s_grouped[b][:, 0, :, :], s_planes[:, :, first : first + n])
+
+        def edge_chunk(b, m):
+            t = m - PACK
+            x = first_matmul(b, m)
+            nc.scalar.activation(
+                out=relu[b][:, :, t, :],
+                in_=x[:].rearrange("p (c i) -> p c i", i=4),
+                func=ACT.Relu,
+                bias=node_t[:, 64 + m : 65 + m],
+                scale=1.0,
+            )
+
+        def add_edges(b):
+            for part in range(BLOCKS[b][1] // 256):
+                nc.vector.tensor_tensor(
+                    out=s_grouped[b][:, 1, 256 * part : 256 * (part + 1), :].rearrange(
+                        "p (c i) t -> p c i t", i=4
+                    ),
+                    in0=edge_t[b][part][:].rearrange("p t (c i) -> p c i t", i=4),
+                    in1=relu[b][:, 64 * part : 64 * (part + 1), :, :].rearrange("p c t i -> p c i t"),
+                    op=ALU.add,
+                )
+
+        def quantise_s(b, half):
             quantise(
-                s_words[b][:].rearrange("p g r -> p (g r)"),
-                s_scales[b][:].rearrange("p g r -> p (g r)"),
-                s_grouped[b][:].rearrange("p g r t -> p (g r t)"),
+                s_words[b][:, half, :],
+                s_scales[b][:, half, :],
+                s_grouped[b][:, half, :, :].rearrange("p r t -> p (r t)"),
             )
 
         def second_stage(b, a):
-            first = BLOCKS[b][0]
-            tile_index = first // P + a
             rows = slice(P * a, P * (a + 1))
             z = psum.tile([P, ED], F32, tag="t", bufs=BANKS_T, name="z")
             for g in range(PASSES):
@@ -293,11 +314,6 @@ def tile_edgeupdaterwrapper_v01_pb_kernel(
                     start=(g == 0),
                     stop=(g == PASSES - 1),
                 )
-            shift = psum.tile([P, ED], F32, tag="b", bufs=BANKS_B, name="shift")
-            nc.tensor.matmul(
-                shift[:], lhsT=ident_bf16[:], rhs=pln_raw[:, tile_index, :], start=True, stop=False
-            )
-            nc.tensor.matmul(shift[:], lhsT=ones[:], rhs=vec_raw[:, 2, :], start=False, stop=True)
             u = work.tile([P, ED], F32, tag="u", bufs=LN_DEPTH, name="u")
             u_sum = work.tile([P, 1], F32, tag="u_sum", bufs=LN_DEPTH, name="u_sum")
             nc.vector.scalar_tensor_tensor(
@@ -306,42 +322,74 @@ def tile_edgeupdaterwrapper_v01_pb_kernel(
             )
             neg_mean = work.tile([P, 1], F32, tag="neg_mean", bufs=LN_DEPTH, name="neg_mean")
             nc.scalar.mul(out=neg_mean[:], in_=u_sum[:], mul=-1.0 / ED)
+            centred = work.tile([P, ED], F32, tag="centred", bufs=LN_DEPTH, name="centred")
+            nc.scalar.activation(
+                out=centred[:], in_=u[:], func=ACT.Identity, bias=neg_mean[:], scale=1.0
+            )
+            scaled = work.tile([P, ED], F32, tag="scaled", bufs=LN_DEPTH, name="scaled")
+            nc.gpsimd.tensor_tensor(out=scaled[:], in0=centred[:], in1=gain_all[:], op=ALU.mult)
             squares = work.tile([P, ED], BF16, tag="squares", bufs=2, name="squares")
             sq_sum = work.tile([P, 1], F32, tag="sq_sum", bufs=LN_DEPTH, name="sq_sum")
             nc.scalar.activation(
-                out=squares[:], in_=u[:], func=ACT.Square, bias=neg_mean[:], scale=1.0,
-                accum_out=sq_sum[:],
+                out=squares[:], in_=centred[:], func=ACT.Square, accum_out=sq_sum[:]
             )
             rstd = work.tile([P, 1], F32, tag="rstd", bufs=LN_DEPTH, name="rstd")
             nc.scalar.activation(
                 out=rstd[:], in_=sq_sum[:], func=ACT.Abs_reciprocal_sqrt, bias=eps[:], scale=1.0 / ED
             )
+            return scaled, rstd
+
+        def finish(b, a, scaled, rstd, tag, bufs):
+            tile_index = BLOCKS[b][0] // P + a
+            shift = psum.tile([P, ED], F32, tag=tag, bufs=bufs, name="shift")
+            nc.tensor.matmul(
+                shift[:], lhsT=ident_bf16[:], rhs=pln_raw[:, tile_index, :], start=True, stop=False
+            )
+            nc.tensor.matmul(shift[:], lhsT=ones[:], rhs=vec_raw[:, 2, :], start=False, stop=True)
             res = work.tile([P, ED], F32, tag="res", bufs=LN_DEPTH, name="res")
             nc.vector.scalar_tensor_tensor(
-                out=res[:], in0=u[:], scalar=neg_mean[:], in1=gain_all[:], op0=ALU.add, op1=ALU.mult
-            )
-            nc.vector.scalar_tensor_tensor(
-                out=res[:], in0=res[:], scalar=rstd[:], in1=shift[:], op0=ALU.mult, op1=ALU.add
+                out=res[:], in0=scaled[:], scalar=rstd[:], in1=shift[:], op0=ALU.mult, op1=ALU.add
             )
             nc.sync.dma_start(out=out_rows[P * tile_index : P * (tile_index + 1), :], in_=res[:])
 
-        prepare_w2(0)
-        prepare_small_inputs()
-        prepare_hid(0)
-        first_stage(0, 0)
-        prepare_w2(1)
-        prepare_edge_add(0)
-        first_stage(0, 1)
-        quantise_s(0)
-        prepare_wo()
-        for b in range(len(BLOCKS)):
-            if b + 1 < len(BLOCKS):
-                first, n = BLOCKS[b + 1]
-                prepare_hid(b + 1)
-                if first <= PLN_LOAD < first + n:
-                    prepare_edge_add(1)
-                first_stage(b + 1, 0)
-                first_stage(b + 1, 1)
-                quantise_s(b + 1)
-            for a in range(BLOCKS[b][1] // P):
-                second_stage(b, a)
+        with tc.manual_schedule(engines={mybir.EngineType.PE}):
+            prepare_w2(1, 0)
+            prepare_hid(0)
+            prepare_w2(1, 1)
+            quantise_hid(0)
+            prepare_small_inputs()
+            prepare_edge(0)
+            for m in range(4, 8):
+                edge_chunk(0, m)
+            prepare_w2(0, 0)
+            prepare_w2(0, 1)
+            prepare_row_vectors()
+            for m in range(4):
+                node_chunk(0, m)
+            add_edges(0)
+            quantise_s(0, 1)
+            prepare_hid(1)
+            interleave_nodes(0)
+            quantise_s(0, 0)
+            quantise_hid(1)
+            prepare_wo()
+            prepare_edge(1)
+            for m in range(4, 8):
+                edge_chunk(1, m)
+            add_edges(1)
+            quantise_s(1, 1)
+            parts = {}
+            for a in range(2):
+                parts[a] = second_stage(0, a)
+            for m in range(4):
+                node_chunk(1, m)
+            interleave_nodes(1)
+            quantise_s(1, 0)
+            for a in range(2, 4):
+                parts[a] = second_stage(0, a)
+            for a in range(4):
+                finish(0, a, *parts[a], "b", BANKS_B)
+            for a in range(4):
+                parts[a] = second_stage(1, a)
+            for a in range(4):
+                finish(1, a, *parts[a], "s", BANKS_S)

@@ -20,7 +20,6 @@ F = 1024
 MD = 1024
 ED = 512
 PASSES = 2
-HID_LOAD = 256
 PLN_LOAD = 512
 EPS = 1e-5
 FLOPS = 2 * ROWS * F * MD + 2 * ROWS * MD * ED
@@ -96,19 +95,13 @@ def tile_edgeupdaterwrapper_v01_pb_kernel(
                     ),
                 )
 
-        def load_hid(part):
-            tiles = HID_LOAD // P
-            nc.sync.dma_start(
-                out=hid_raw[:, tiles * part : tiles * (part + 1), :],
-                in_=hid_rows[HID_LOAD * part : HID_LOAD * (part + 1), :].rearrange(
-                    "(a p) k -> p a k", p=P
-                ),
-            )
+        def load_hid(a):
+            nc.sync.dma_start(out=hid_raw[:, a, :], in_=hid_rows[P * a : P * (a + 1), :])
 
         def load_node_inputs():
-            nc.sync.dma_start(out=node_raw[0:32, :], in_=xd_rows[:, 0:P])
-            nc.sync.dma_start(out=node_raw[32:64, :], in_=xd_rows[:, P : 2 * P])
-            nc.sync.dma_start(out=node_raw[64:72, :], in_=b2.rearrange("(m p) -> m p", p=P))
+            nc.scalar.dma_start(out=node_raw[0:32, :], in_=xd_rows[:, 0:P])
+            nc.scalar.dma_start(out=node_raw[32:64, :], in_=xd_rows[:, P : 2 * P])
+            nc.scalar.dma_start(out=node_raw[64:72, :], in_=b2.rearrange("(m p) -> m p", p=P))
 
         def load_p_ln(part):
             tiles = PLN_LOAD // P
@@ -121,63 +114,68 @@ def tile_edgeupdaterwrapper_v01_pb_kernel(
 
         def load_row_vectors():
             for c, vec in enumerate((bo, ln_out_g, ln_out_b)):
-                nc.sync.dma_start(out=vec_raw[0:1, c, :], in_=vec.rearrange("(o f) -> o f", o=1))
+                nc.scalar.dma_start(out=vec_raw[0:1, c, :], in_=vec.rearrange("(o f) -> o f", o=1))
 
-        def load_wo():
-            for g in range(PASSES):
-                nc.sync.dma_start(
-                    out=wo_raw[:, g, :, :],
-                    in_=Wo[K_PASS * g : K_PASS * (g + 1), :].rearrange("(t p) n -> p t n", p=P),
-                )
+        def load_wo(g):
+            nc.sync.dma_start(
+                out=wo_raw[:, g, :, :],
+                in_=Wo[K_PASS * g : K_PASS * (g + 1), :].rearrange("(t p) n -> p t n", p=P),
+            )
 
-        load_w2(1, 0)
-        load_hid(0)
-        load_w2(1, 1)
-        load_hid(1)
         load_node_inputs()
+        load_row_vectors()
+        load_hid(0)
+        load_w2(1, 0)
+        load_hid(1)
+        load_hid(2)
+        load_w2(1, 1)
+        load_hid(3)
         load_p_ln(0)
         load_w2(0, 0)
         load_w2(0, 1)
-        load_row_vectors()
-        load_hid(2)
-        load_hid(3)
-        load_wo()
+        load_hid(4)
+        load_hid(5)
+        load_hid(6)
+        load_hid(7)
+        load_wo(0)
         load_p_ln(1)
+        load_wo(1)
 
-        def prepare_w2(half, g):
+        def group_w2(half, g):
             interleave(nc.vector.tensor_copy, w2_grouped[:, half, g, :, :], w2_raw[:, half, g, :, :])
+
+        def quantise_w2(half, g):
             quantise(
                 w2_words[:, half, g, :],
                 w2_scales[:, half, g, :],
                 w2_grouped[:, half, g, :, :].rearrange("p n t -> p (n t)"),
             )
 
-        def prepare_wo():
-            for g in range(PASSES):
-                interleave(nc.vector.tensor_copy, wo_grouped[:, g, :, :], wo_raw[:, g, :, :])
+        def group_wo(g):
+            interleave(nc.scalar.copy, wo_grouped[:, g, :, :], wo_raw[:, g, :, :])
+
+        def quantise_wo(g):
             quantise(
-                wo_words[:].rearrange("p g n -> p (g n)"),
-                wo_scales[:].rearrange("p g n -> p (g n)"),
-                wo_grouped[:].rearrange("p g n t -> p (g n t)"),
+                wo_words[:, g, :], wo_scales[:, g, :], wo_grouped[:, g, :, :].rearrange("p n t -> p (n t)")
             )
 
         def prepare_small_inputs():
             node_ps = psum.tile([P, P], BF16, tag="t", bufs=BANKS_T, name="node_ps")
             nc.tensor.transpose(node_ps[:], node_raw[:], ident_bf16[:])
             nc.scalar.copy(out=node_t[:], in_=node_ps[:, 0:72])
-            nc.vector.tensor_scalar_mul(neg_b2[:], node_t[:, 64:68], -1.0)
+            nc.gpsimd.tensor_scalar_mul(neg_b2[:], node_t[:, 64:68], -1.0)
             for m in range(PACK):
                 x0 = NODES * (m % 2)
-                nc.vector.tensor_scalar_add(
+                nc.gpsimd.tensor_scalar_add(
                     out=node_add[:, m, :],
                     in0=node_t[:, x0 : x0 + NODES],
                     scalar1=node_t[:, 64 + m : 65 + m],
                 )
         def prepare_row_vectors():
-            for c, dst in enumerate((bo_all, gain_all)):
+            for c, dst, factor in ((0, bo_all, -1.0 / ED), (1, gain_all, 1.0)):
                 spread = psum.tile([P, ED], F32, tag="t", bufs=BANKS_T, name="spread")
                 nc.tensor.matmul(spread[:], lhsT=ones[:], rhs=vec_raw[:, c, :], start=True, stop=True)
-                nc.scalar.copy(out=dst[:], in_=spread[:])
+                nc.scalar.mul(out=dst[:], in_=spread[:], mul=factor)
 
         def prepare_edge(b):
             first, n = BLOCKS[b]
@@ -202,36 +200,29 @@ def tile_edgeupdaterwrapper_v01_pb_kernel(
             s_words[b] = keep.tile([P, PASSES, n], U32, align_bytes=64, name="s_words%d" % b)
             s_scales[b] = keep.tile([P, PASSES, n], U8, align_bytes=64, name="s_scales%d" % b)
 
-        def prepare_hid(b):
-            first, n = BLOCKS[b]
-            grouped = keep.tile([P, PASSES, n, 2], F32, align_bytes=64, name="hid_grouped%d" % b)
+        for b, (first, n) in enumerate(BLOCKS):
+            hid_grouped[b] = keep.tile([P, PASSES, n, 2], F32, align_bytes=64, name="hid_grouped%d" % b)
             hid_words[b] = keep.tile([P, PASSES, n], U32, align_bytes=64, name="hid_words%d" % b)
             hid_scales[b] = keep.tile([P, PASSES, n], U8, align_bytes=64, name="hid_scales%d" % b)
-            for part in range(n // 256):
-                for g in range(PASSES):
-                    hid_t = psum.tile([P, 2, 2, P], F32, tag="t", bufs=BANKS_T, name="hid_t")
-                    for a in range(2):
-                        pairs_of_k = hid_raw[:, first // P + 2 * part + a, :].bitcast(F32)
-                        for u in range(2):
-                            w0 = 256 * g + P * u
-                            nc.tensor.transpose(
-                                hid_t[:, a, u, :], pairs_of_k[:, w0 : w0 + P], ident_f32[:]
-                            )
-                    nc.scalar.copy(
-                        out=grouped[:, g, 256 * part : 256 * (part + 1), :].rearrange(
-                            "p (a r) u -> p a r u", a=2
-                        ),
-                        in_=hid_t[:].rearrange("p a u r -> p a r u"),
-                    )
-            hid_grouped[b] = grouped
 
-        def quantise_hid(b):
+        def prepare_hid(b, a):
+            hid_t = psum.tile([P, PASSES, 2, P], F32, tag="t", bufs=BANKS_T, name="hid_t")
+            pairs_of_k = hid_raw[:, BLOCKS[b][0] // P + a, :].bitcast(F32)
             for g in range(PASSES):
-                quantise(
-                    hid_words[b][:, g, :],
-                    hid_scales[b][:, g, :],
-                    hid_grouped[b][:, g, :, :].bitcast(BF16).rearrange("p r t -> p (r t)"),
-                )
+                for u in range(2):
+                    w0 = 256 * g + P * u
+                    nc.tensor.transpose(hid_t[:, g, u, :], pairs_of_k[:, w0 : w0 + P], ident_f32[:])
+            nc.scalar.copy(
+                out=hid_grouped[b][:, :, P * a : P * (a + 1), :],
+                in_=hid_t[:].rearrange("p g u r -> p g r u"),
+            )
+
+        def quantise_hid(b, g):
+            quantise(
+                hid_words[b][:, g, :],
+                hid_scales[b][:, g, :],
+                hid_grouped[b][:, g, :, :].bitcast(BF16).rearrange("p r t -> p (r t)"),
+            )
 
         def first_matmul(b, m):
             n = BLOCKS[b][1]
@@ -301,12 +292,15 @@ def tile_edgeupdaterwrapper_v01_pb_kernel(
                 s_grouped[b][:, half, :, :].rearrange("p r t -> p (r t)"),
             )
 
-        def second_stage(b, a):
+        z, u, neg_mean, scaled, sq_sum, rstd, shift = {}, {}, {}, {}, {}, {}, {}
+
+        def second_matmul(k):
+            b, a = divmod(k, 4)
             rows = slice(P * a, P * (a + 1))
-            z = psum.tile([P, ED], F32, tag="t", bufs=BANKS_T, name="z")
+            z[k] = psum.tile([P, ED], F32, tag="t", bufs=BANKS_T, name="z")
             for g in range(PASSES):
                 nc.tensor.matmul_mx(
-                    out=z[:],
+                    out=z[k][:],
                     lhsT=s_words[b][:, g, rows].bitcast(FP8X4),
                     lhsT_scale=s_scales[b][:, g, rows],
                     rhs=wo_words[:, g, :].bitcast(FP8X4),
@@ -314,82 +308,118 @@ def tile_edgeupdaterwrapper_v01_pb_kernel(
                     start=(g == 0),
                     stop=(g == PASSES - 1),
                 )
-            u = work.tile([P, ED], F32, tag="u", bufs=LN_DEPTH, name="u")
-            u_sum = work.tile([P, 1], F32, tag="u_sum", bufs=LN_DEPTH, name="u_sum")
+
+        def add_bo(k):
+            u[k] = work.tile([P, ED], F32, tag="u", bufs=LN_DEPTH, name="u")
+            neg_mean[k] = work.tile([P, 1], F32, tag="neg_mean", bufs=LN_DEPTH, name="neg_mean")
             nc.vector.scalar_tensor_tensor(
-                out=u[:], in0=z[:], scalar=1.0, in1=bo_all[:], op0=ALU.mult, op1=ALU.add,
-                accum_out=u_sum[:],
+                out=u[k][:], in0=z[k][:], scalar=-1.0 / ED, in1=bo_all[:], op0=ALU.mult, op1=ALU.add,
+                accum_out=neg_mean[k][:],
             )
-            neg_mean = work.tile([P, 1], F32, tag="neg_mean", bufs=LN_DEPTH, name="neg_mean")
-            nc.scalar.mul(out=neg_mean[:], in_=u_sum[:], mul=-1.0 / ED)
+
+        def centre(k):
             centred = work.tile([P, ED], F32, tag="centred", bufs=LN_DEPTH, name="centred")
             nc.scalar.activation(
-                out=centred[:], in_=u[:], func=ACT.Identity, bias=neg_mean[:], scale=1.0
+                out=centred[:], in_=u[k][:], func=ACT.Identity, bias=neg_mean[k][:], scale=-float(ED)
             )
-            scaled = work.tile([P, ED], F32, tag="scaled", bufs=LN_DEPTH, name="scaled")
-            nc.gpsimd.tensor_tensor(out=scaled[:], in0=centred[:], in1=gain_all[:], op=ALU.mult)
-            squares = work.tile([P, ED], BF16, tag="squares", bufs=2, name="squares")
-            sq_sum = work.tile([P, 1], F32, tag="sq_sum", bufs=LN_DEPTH, name="sq_sum")
-            nc.scalar.activation(
-                out=squares[:], in_=centred[:], func=ACT.Square, accum_out=sq_sum[:]
-            )
-            rstd = work.tile([P, 1], F32, tag="rstd", bufs=LN_DEPTH, name="rstd")
-            nc.scalar.activation(
-                out=rstd[:], in_=sq_sum[:], func=ACT.Abs_reciprocal_sqrt, bias=eps[:], scale=1.0 / ED
-            )
-            return scaled, rstd
+            scaled[k] = work.tile([P, ED], F32, tag="scaled", bufs=LN_DEPTH, name="scaled")
+            nc.gpsimd.tensor_tensor(out=scaled[k][:], in0=centred[:], in1=gain_all[:], op=ALU.mult)
 
-        def finish(b, a, scaled, rstd, tag, bufs):
-            tile_index = BLOCKS[b][0] // P + a
-            shift = psum.tile([P, ED], F32, tag=tag, bufs=bufs, name="shift")
-            nc.tensor.matmul(
-                shift[:], lhsT=ident_bf16[:], rhs=pln_raw[:, tile_index, :], start=True, stop=False
+        def deviation(k):
+            sq_sum[k] = work.tile([P, 2], F32, tag="sq_sum", bufs=2, name="sq_sum")
+            for i in range(2):
+                squares = work.tile([P, ED], BF16, tag="squares", bufs=2, name="squares")
+                nc.scalar.activation(
+                    out=squares[:], in_=u[k + i][:], func=ACT.Square, bias=neg_mean[k + i][:],
+                    scale=-float(ED), accum_out=sq_sum[k][:, i : i + 1],
+                )
+            both = work.tile([P, 2], F32, tag="rstd", bufs=2, name="both")
+            nc.scalar.activation(
+                out=both[:], in_=sq_sum[k][:], func=ACT.Abs_reciprocal_sqrt, bias=eps[:], scale=1.0 / ED
             )
-            nc.tensor.matmul(shift[:], lhsT=ones[:], rhs=vec_raw[:, 2, :], start=False, stop=True)
+            for i in range(2):
+                rstd[k + i] = both[:, i : i + 1]
+
+        def add_shift(k):
+            shift[k] = psum.tile([P, ED], F32, tag="s", bufs=BANKS_S, name="shift")
+            nc.tensor.matmul(
+                shift[k][:], lhsT=ident_bf16[:], rhs=pln_raw[:, k, :], start=True, stop=False
+            )
+            nc.tensor.matmul(shift[k][:], lhsT=ones[:], rhs=vec_raw[:, 2, :], start=False, stop=True)
+
+        def finish(k):
             res = work.tile([P, ED], F32, tag="res", bufs=LN_DEPTH, name="res")
             nc.vector.scalar_tensor_tensor(
-                out=res[:], in0=scaled[:], scalar=rstd[:], in1=shift[:], op0=ALU.mult, op1=ALU.add
+                out=res[:], in0=scaled[k][:], scalar=rstd[k], in1=shift[k][:], op0=ALU.mult, op1=ALU.add
             )
-            nc.sync.dma_start(out=out_rows[P * tile_index : P * (tile_index + 1), :], in_=res[:])
+            nc.sync.dma_start(out=out_rows[P * k : P * (k + 1), :], in_=res[:])
 
-        with tc.manual_schedule(engines={mybir.EngineType.PE}):
-            prepare_w2(1, 0)
-            prepare_hid(0)
-            prepare_w2(1, 1)
-            quantise_hid(0)
+        with tc.manual_schedule():
+            prepare_hid(0, 0)
+            group_w2(1, 0)
+            prepare_hid(0, 1)
+            prepare_hid(0, 2)
+            group_w2(1, 1)
+            quantise_w2(1, 0)
+            prepare_hid(0, 3)
+            quantise_w2(1, 1)
             prepare_small_inputs()
+            prepare_row_vectors()
+            for g in range(PASSES):
+                quantise_hid(0, g)
             prepare_edge(0)
+            group_w2(0, 0)
             for m in range(4, 8):
                 edge_chunk(0, m)
-            prepare_w2(0, 0)
-            prepare_w2(0, 1)
-            prepare_row_vectors()
+            group_w2(0, 1)
+            quantise_w2(0, 0)
+            quantise_w2(0, 1)
+            for a in range(4):
+                prepare_hid(1, a)
+            add_edges(0)
+            for g in range(PASSES):
+                quantise_hid(1, g)
             for m in range(4):
                 node_chunk(0, m)
-            add_edges(0)
             quantise_s(0, 1)
-            prepare_hid(1)
-            interleave_nodes(0)
-            quantise_s(0, 0)
-            quantise_hid(1)
-            prepare_wo()
+            group_wo(0)
             prepare_edge(1)
             for m in range(4, 8):
                 edge_chunk(1, m)
+            interleave_nodes(0)
+            quantise_wo(0)
             add_edges(1)
-            quantise_s(1, 1)
-            parts = {}
-            for a in range(2):
-                parts[a] = second_stage(0, a)
-            for m in range(4):
+            group_wo(1)
+            for m in range(2):
                 node_chunk(1, m)
+            quantise_s(0, 0)
+            quantise_wo(1)
+            for m in range(2, 4):
+                node_chunk(1, m)
+            quantise_s(1, 1)
+            for k in range(2):
+                second_matmul(k)
+            for k in range(2):
+                add_bo(k)
             interleave_nodes(1)
+            for k in range(2, 4):
+                second_matmul(k)
+            for k in range(2):
+                centre(k)
+            add_bo(2)
             quantise_s(1, 0)
-            for a in range(2, 4):
-                parts[a] = second_stage(0, a)
-            for a in range(4):
-                finish(0, a, *parts[a], "b", BANKS_B)
-            for a in range(4):
-                parts[a] = second_stage(1, a)
-            for a in range(4):
-                finish(1, a, *parts[a], "s", BANKS_S)
+            add_bo(3)
+            deviation(0)
+            for k in range(0, 8, 2):
+                for i in range(k + 2, min(k + 4, 8)):
+                    centre(i)
+                for i in range(k, k + 2):
+                    add_shift(i)
+                for i in range(k + 4, min(k + 6, 8)):
+                    second_matmul(i)
+                for i in range(k, k + 2):
+                    finish(i)
+                for i in range(k + 4, min(k + 6, 8)):
+                    add_bo(i)
+                if k + 2 < 8:
+                    deviation(k + 2)

@@ -56,7 +56,6 @@ def tile_edgeupdaterwrapper_v01_pb_kernel(
         wo_grouped = keep.tile([P, PASSES, ED, PACK], BF16, align_bytes=64)
         wo_words = keep.tile([P, PASSES, ED], U32, align_bytes=64)
         wo_scales = keep.tile([P, PASSES, ED], U8, align_bytes=64)
-        s_planes = keep.tile([P, PACK, ROWS], BF16)
         node_add = keep.tile([P, PACK, NODES], F32)
         node_t = keep.tile([P, 72], F32)
         neg_b2 = keep.tile([P, PACK], F32)
@@ -99,9 +98,9 @@ def tile_edgeupdaterwrapper_v01_pb_kernel(
             nc.sync.dma_start(out=hid_raw[:, a, :], in_=hid_rows[P * a : P * (a + 1), :])
 
         def load_node_inputs():
-            nc.scalar.dma_start(out=node_raw[0:32, :], in_=xd_rows[:, 0:P])
-            nc.scalar.dma_start(out=node_raw[32:64, :], in_=xd_rows[:, P : 2 * P])
-            nc.scalar.dma_start(out=node_raw[64:72, :], in_=b2.rearrange("(m p) -> m p", p=P))
+            nc.sync.dma_start(out=node_raw[0:32, :], in_=xd_rows[:, 0:P])
+            nc.sync.dma_start(out=node_raw[32:64, :], in_=xd_rows[:, P : 2 * P])
+            nc.sync.dma_start(out=node_raw[64:72, :], in_=b2.rearrange("(m p) -> m p", p=P))
 
         def load_p_ln(part):
             tiles = PLN_LOAD // P
@@ -114,7 +113,7 @@ def tile_edgeupdaterwrapper_v01_pb_kernel(
 
         def load_row_vectors():
             for c, vec in enumerate((bo, ln_out_g, ln_out_b)):
-                nc.scalar.dma_start(out=vec_raw[0:1, c, :], in_=vec.rearrange("(o f) -> o f", o=1))
+                nc.sync.dma_start(out=vec_raw[0:1, c, :], in_=vec.rearrange("(o f) -> o f", o=1))
 
         def load_wo(g):
             nc.sync.dma_start(
@@ -122,14 +121,14 @@ def tile_edgeupdaterwrapper_v01_pb_kernel(
                 in_=Wo[K_PASS * g : K_PASS * (g + 1), :].rearrange("(t p) n -> p t n", p=P),
             )
 
-        load_node_inputs()
-        load_row_vectors()
         load_hid(0)
         load_w2(1, 0)
         load_hid(1)
         load_hid(2)
         load_w2(1, 1)
         load_hid(3)
+        load_node_inputs()
+        load_row_vectors()
         load_p_ln(0)
         load_w2(0, 0)
         load_w2(0, 1)
@@ -193,8 +192,9 @@ def tile_edgeupdaterwrapper_v01_pb_kernel(
 
         hid_grouped, hid_words, hid_scales = {}, {}, {}
         edge_t = {}
-        relu, s_grouped, s_words, s_scales = {}, {}, {}, {}
+        s_planes, relu, s_grouped, s_words, s_scales = {}, {}, {}, {}, {}
         for b, (first, n) in enumerate(BLOCKS):
+            s_planes[b] = keep.tile([P, PACK, n], BF16, name="s_planes%d" % b)
             relu[b] = keep.tile([P, n // 4, PACK, 4], F32, name="relu%d" % b)
             s_grouped[b] = keep.tile([P, PASSES, n, PACK], BF16, align_bytes=64, name="s_grouped%d" % b)
             s_words[b] = keep.tile([P, PASSES, n], U32, align_bytes=64, name="s_words%d" % b)
@@ -243,7 +243,6 @@ def tile_edgeupdaterwrapper_v01_pb_kernel(
 
         def node_chunk(b, m):
             first, n = BLOCKS[b]
-            rows = slice(first, first + n)
             i0, ni = first // NODES, n // NODES
             x = first_matmul(b, m)
             if m < 2:
@@ -251,7 +250,7 @@ def tile_edgeupdaterwrapper_v01_pb_kernel(
             else:
                 add = node_add[:, m, :].unsqueeze(1).to_broadcast([P, ni, NODES])
             nc.vector.scalar_tensor_tensor(
-                out=s_planes[:, m, rows].rearrange("p (i j) -> p i j", j=NODES),
+                out=s_planes[b][:, m, :].rearrange("p (i j) -> p i j", j=NODES),
                 in0=x[:].rearrange("p (i j) -> p i j", j=NODES),
                 scalar=neg_b2[:, m : m + 1],
                 in1=add,
@@ -260,8 +259,7 @@ def tile_edgeupdaterwrapper_v01_pb_kernel(
             )
 
         def interleave_nodes(b):
-            first, n = BLOCKS[b]
-            interleave(nc.scalar.copy, s_grouped[b][:, 0, :, :], s_planes[:, :, first : first + n])
+            interleave(nc.scalar.copy, s_grouped[b][:, 0, :, :], s_planes[b][:])
 
         def edge_chunk(b, m):
             t = m - PACK
@@ -292,7 +290,7 @@ def tile_edgeupdaterwrapper_v01_pb_kernel(
                 s_grouped[b][:, half, :, :].rearrange("p r t -> p (r t)"),
             )
 
-        z, u, neg_mean, scaled, sq_sum, rstd, shift = {}, {}, {}, {}, {}, {}, {}
+        z, u, neg_mean, scaled, rstd, shift = {}, {}, {}, {}, {}, {}
 
         def second_matmul(k):
             b, a = divmod(k, 4)
@@ -326,19 +324,16 @@ def tile_edgeupdaterwrapper_v01_pb_kernel(
             nc.gpsimd.tensor_tensor(out=scaled[k][:], in0=centred[:], in1=gain_all[:], op=ALU.mult)
 
         def deviation(k):
-            sq_sum[k] = work.tile([P, 2], F32, tag="sq_sum", bufs=2, name="sq_sum")
-            for i in range(2):
-                squares = work.tile([P, ED], BF16, tag="squares", bufs=2, name="squares")
-                nc.scalar.activation(
-                    out=squares[:], in_=u[k + i][:], func=ACT.Square, bias=neg_mean[k + i][:],
-                    scale=-float(ED), accum_out=sq_sum[k][:, i : i + 1],
-                )
-            both = work.tile([P, 2], F32, tag="rstd", bufs=2, name="both")
+            squares = work.tile([P, ED], BF16, tag="squares", bufs=2, name="squares")
+            sq_sum = work.tile([P, 1], F32, tag="sq_sum", bufs=LN_DEPTH, name="sq_sum")
             nc.scalar.activation(
-                out=both[:], in_=sq_sum[k][:], func=ACT.Abs_reciprocal_sqrt, bias=eps[:], scale=1.0 / ED
+                out=squares[:], in_=u[k][:], func=ACT.Square, bias=neg_mean[k][:], scale=-float(ED),
+                accum_out=sq_sum[:],
             )
-            for i in range(2):
-                rstd[k + i] = both[:, i : i + 1]
+            rstd[k] = work.tile([P, 1], F32, tag="rstd", bufs=LN_DEPTH, name="rstd")
+            nc.scalar.activation(
+                out=rstd[k][:], in_=sq_sum[:], func=ACT.Abs_reciprocal_sqrt, bias=eps[:], scale=1.0 / ED
+            )
 
         def add_shift(k):
             shift[k] = psum.tile([P, ED], F32, tag="s", bufs=BANKS_S, name="shift")
@@ -350,7 +345,7 @@ def tile_edgeupdaterwrapper_v01_pb_kernel(
         def finish(k):
             res = work.tile([P, ED], F32, tag="res", bufs=LN_DEPTH, name="res")
             nc.vector.scalar_tensor_tensor(
-                out=res[:], in0=scaled[k][:], scalar=rstd[k], in1=shift[k][:], op0=ALU.mult, op1=ALU.add
+                out=res[:], in0=scaled[k][:], scalar=rstd[k][:], in1=shift[k][:], op0=ALU.mult, op1=ALU.add
             )
             nc.sync.dma_start(out=out_rows[P * k : P * (k + 1), :], in_=res[:])
 
@@ -381,45 +376,44 @@ def tile_edgeupdaterwrapper_v01_pb_kernel(
                 quantise_hid(1, g)
             for m in range(4):
                 node_chunk(0, m)
-            quantise_s(0, 1)
             group_wo(0)
-            prepare_edge(1)
-            for m in range(4, 8):
-                edge_chunk(1, m)
-            interleave_nodes(0)
-            quantise_wo(0)
-            add_edges(1)
             group_wo(1)
-            for m in range(2):
-                node_chunk(1, m)
+            quantise_s(0, 1)
+            interleave_nodes(0)
+            prepare_edge(1)
+            for m in range(8):
+                if m < 4:
+                    node_chunk(1, m)
+                else:
+                    edge_chunk(1, m)
+            quantise_wo(0)
             quantise_s(0, 0)
             quantise_wo(1)
-            for m in range(2, 4):
-                node_chunk(1, m)
-            quantise_s(1, 1)
             for k in range(2):
                 second_matmul(k)
+            interleave_nodes(1)
             for k in range(2):
                 add_bo(k)
-            interleave_nodes(1)
+            for k in range(2):
+                centre(k)
+            add_edges(1)
             for k in range(2, 4):
                 second_matmul(k)
             for k in range(2):
-                centre(k)
+                deviation(k)
             add_bo(2)
             quantise_s(1, 0)
+            quantise_s(1, 1)
             add_bo(3)
-            deviation(0)
-            for k in range(0, 8, 2):
-                for i in range(k + 2, min(k + 4, 8)):
-                    centre(i)
-                for i in range(k, k + 2):
-                    add_shift(i)
-                for i in range(k + 4, min(k + 6, 8)):
-                    second_matmul(i)
-                for i in range(k, k + 2):
-                    finish(i)
-                for i in range(k + 4, min(k + 6, 8)):
-                    add_bo(i)
+            for k in range(4):
+                add_shift(k)
+            for k in range(8):
                 if k + 2 < 8:
+                    centre(k + 2)
                     deviation(k + 2)
+                if k + 4 < 8:
+                    second_matmul(k + 4)
+                finish(k)
+                if k + 4 < 8:
+                    add_shift(k + 4)
+                    add_bo(k + 4)

@@ -121,11 +121,11 @@ def tile_edgeupdaterwrapper_v01_pb_kernel(
                 in_=Wo[K_PASS * g : K_PASS * (g + 1), :].rearrange("(t p) n -> p t n", p=P),
             )
 
-        load_hid(0)
         load_w2(1, 0)
+        load_hid(0)
         load_hid(1)
-        load_hid(2)
         load_w2(1, 1)
+        load_hid(2)
         load_hid(3)
         load_node_inputs()
         load_row_vectors()
@@ -150,8 +150,8 @@ def tile_edgeupdaterwrapper_v01_pb_kernel(
                 w2_grouped[:, half, g, :, :].rearrange("p n t -> p (n t)"),
             )
 
-        def group_wo(g):
-            interleave(nc.scalar.copy, wo_grouped[:, g, :, :], wo_raw[:, g, :, :])
+        def group_wo(copy, g):
+            interleave(copy, wo_grouped[:, g, :, :], wo_raw[:, g, :, :])
 
         def quantise_wo(g):
             quantise(
@@ -176,22 +176,20 @@ def tile_edgeupdaterwrapper_v01_pb_kernel(
                 nc.tensor.matmul(spread[:], lhsT=ones[:], rhs=vec_raw[:, c, :], start=True, stop=True)
                 nc.scalar.mul(out=dst[:], in_=spread[:], mul=factor)
 
-        def prepare_edge(b):
-            first, n = BLOCKS[b]
-            edge_t[b] = []
-            for part in range(n // 256):
-                pln_t = psum.tile([P, PACK, 256], BF16, tag="b", bufs=BANKS_B, name="pln_t")
-                for t in range(PACK):
-                    for a in range(2):
-                        nc.tensor.transpose(
-                            pln_t[:, t, P * a : P * (a + 1)],
-                            pln_raw[:, first // P + 2 * part + a, P * t : P * (t + 1)],
-                            ident_bf16[:],
-                        )
-                edge_t[b].append(pln_t)
+        def prepare_edge(b, part):
+            pln_t = psum.tile([P, PACK, 256], BF16, tag="b", bufs=BANKS_B, name="pln_t")
+            for t in range(PACK):
+                for a in range(2):
+                    nc.tensor.transpose(
+                        pln_t[:, t, P * a : P * (a + 1)],
+                        pln_raw[:, BLOCKS[b][0] // P + 2 * part + a, P * t : P * (t + 1)],
+                        ident_bf16[:],
+                    )
+            edge_t[b, part] = pln_t
 
         hid_grouped, hid_words, hid_scales = {}, {}, {}
         edge_t = {}
+        node_relus = keep.tile([P, PACK, BLOCKS[0][1]], F32)
         s_planes, relu, s_grouped, s_words, s_scales = {}, {}, {}, {}, {}
         for b, (first, n) in enumerate(BLOCKS):
             s_planes[b] = keep.tile([P, PACK, n], BF16, name="s_planes%d" % b)
@@ -258,6 +256,31 @@ def tile_edgeupdaterwrapper_v01_pb_kernel(
                 op1=ALU.add,
             )
 
+        def node_relu(m):
+            x = first_matmul(0, m)
+            nc.scalar.activation(
+                out=node_relus[:, m, :],
+                in_=x[:],
+                func=ACT.Relu,
+                bias=node_t[:, 64 + m : 65 + m],
+                scale=1.0,
+            )
+
+        def add_nodes(by_i):
+            ni = BLOCKS[0][1] // NODES
+            x_down_t = node_t[:, 0 : 2 * NODES].rearrange("p (t n) -> p n t", t=2)
+            t0 = 0 if by_i else 2
+            if by_i:
+                add = x_down_t[:, 0:ni, :].unsqueeze(2).to_broadcast([P, ni, NODES, 2])
+            else:
+                add = x_down_t.unsqueeze(1).to_broadcast([P, ni, NODES, 2])
+            nc.gpsimd.tensor_tensor(
+                out=s_grouped[0][:, 0, :, t0 : t0 + 2].rearrange("p (i j) t -> p i j t", j=NODES),
+                in0=node_relus[:, t0 : t0 + 2, :].rearrange("p t (i j) -> p i j t", j=NODES),
+                in1=add,
+                op=ALU.add,
+            )
+
         def interleave_nodes(b):
             interleave(nc.scalar.copy, s_grouped[b][:, 0, :, :], s_planes[b][:])
 
@@ -278,7 +301,7 @@ def tile_edgeupdaterwrapper_v01_pb_kernel(
                     out=s_grouped[b][:, 1, 256 * part : 256 * (part + 1), :].rearrange(
                         "p (c i) t -> p c i t", i=4
                     ),
-                    in0=edge_t[b][part][:].rearrange("p t (c i) -> p c i t", i=4),
+                    in0=edge_t[b, part][:].rearrange("p t (c i) -> p c i t", i=4),
                     in1=relu[b][:, 64 * part : 64 * (part + 1), :, :].rearrange("p c t i -> p c i t"),
                     op=ALU.add,
                 )
@@ -291,6 +314,10 @@ def tile_edgeupdaterwrapper_v01_pb_kernel(
             )
 
         z, u, neg_mean, scaled, rstd, shift = {}, {}, {}, {}, {}, {}
+
+        def pieces(k):
+            width = ED // 2 if k == ROWS // P - 1 else ED
+            return [slice(f, f + width) for f in range(0, ED, width)]
 
         def second_matmul(k):
             b, a = divmod(k, 4)
@@ -321,7 +348,10 @@ def tile_edgeupdaterwrapper_v01_pb_kernel(
                 out=centred[:], in_=u[k][:], func=ACT.Identity, bias=neg_mean[k][:], scale=-float(ED)
             )
             scaled[k] = work.tile([P, ED], F32, tag="scaled", bufs=LN_DEPTH, name="scaled")
-            nc.gpsimd.tensor_tensor(out=scaled[k][:], in0=centred[:], in1=gain_all[:], op=ALU.mult)
+            for cols in pieces(k):
+                nc.gpsimd.tensor_tensor(
+                    out=scaled[k][:, cols], in0=centred[:, cols], in1=gain_all[:, cols], op=ALU.mult
+                )
 
         def deviation(k):
             squares = work.tile([P, ED], BF16, tag="squares", bufs=2, name="squares")
@@ -344,28 +374,31 @@ def tile_edgeupdaterwrapper_v01_pb_kernel(
 
         def finish(k):
             res = work.tile([P, ED], F32, tag="res", bufs=LN_DEPTH, name="res")
-            nc.vector.scalar_tensor_tensor(
-                out=res[:], in0=scaled[k][:], scalar=rstd[k][:], in1=shift[k][:], op0=ALU.mult, op1=ALU.add
-            )
-            nc.sync.dma_start(out=out_rows[P * k : P * (k + 1), :], in_=res[:])
+            for cols in pieces(k):
+                nc.vector.scalar_tensor_tensor(
+                    out=res[:, cols], in0=scaled[k][:, cols], scalar=rstd[k][:], in1=shift[k][:, cols],
+                    op0=ALU.mult, op1=ALU.add,
+                )
+                nc.sync.dma_start(out=out_rows[P * k : P * (k + 1), cols], in_=res[:, cols])
 
         with tc.manual_schedule():
-            prepare_hid(0, 0)
             group_w2(1, 0)
-            prepare_hid(0, 1)
-            prepare_hid(0, 2)
-            group_w2(1, 1)
             quantise_w2(1, 0)
-            prepare_hid(0, 3)
+            prepare_hid(0, 0)
+            prepare_hid(0, 1)
+            group_w2(1, 1)
+            prepare_hid(0, 2)
             quantise_w2(1, 1)
+            prepare_hid(0, 3)
             prepare_small_inputs()
             prepare_row_vectors()
             for g in range(PASSES):
                 quantise_hid(0, g)
-            prepare_edge(0)
+            prepare_edge(0, 0)
             group_w2(0, 0)
             for m in range(4, 8):
                 edge_chunk(0, m)
+            prepare_edge(0, 1)
             group_w2(0, 1)
             quantise_w2(0, 0)
             quantise_w2(0, 1)
@@ -375,12 +408,14 @@ def tile_edgeupdaterwrapper_v01_pb_kernel(
             for g in range(PASSES):
                 quantise_hid(1, g)
             for m in range(4):
-                node_chunk(0, m)
-            group_wo(0)
-            group_wo(1)
+                node_relu(m)
+            add_nodes(True)
+            add_nodes(False)
+            group_wo(nc.vector.tensor_copy, 0)
             quantise_s(0, 1)
-            interleave_nodes(0)
-            prepare_edge(1)
+            group_wo(nc.scalar.copy, 1)
+            for part in range(2):
+                prepare_edge(1, part)
             for m in range(8):
                 if m < 4:
                     node_chunk(1, m)

@@ -150,8 +150,8 @@ def tile_edgeupdaterwrapper_v01_pb_kernel(
                 w2_grouped[:, half, g, :, :].rearrange("p n t -> p (n t)"),
             )
 
-        def group_wo(copy, g):
-            interleave(copy, wo_grouped[:, g, :, :], wo_raw[:, g, :, :])
+        def group_wo(g):
+            interleave(nc.scalar.copy, wo_grouped[:, g, :, :], wo_raw[:, g, :, :])
 
         def quantise_wo(g):
             quantise(
@@ -189,7 +189,6 @@ def tile_edgeupdaterwrapper_v01_pb_kernel(
 
         hid_grouped, hid_words, hid_scales = {}, {}, {}
         edge_t = {}
-        node_relus = keep.tile([P, PACK, BLOCKS[0][1]], F32)
         s_planes, relu, s_grouped, s_words, s_scales = {}, {}, {}, {}, {}
         for b, (first, n) in enumerate(BLOCKS):
             s_planes[b] = keep.tile([P, PACK, n], BF16, name="s_planes%d" % b)
@@ -254,31 +253,6 @@ def tile_edgeupdaterwrapper_v01_pb_kernel(
                 in1=add,
                 op0=ALU.max,
                 op1=ALU.add,
-            )
-
-        def node_relu(m):
-            x = first_matmul(0, m)
-            nc.scalar.activation(
-                out=node_relus[:, m, :],
-                in_=x[:],
-                func=ACT.Relu,
-                bias=node_t[:, 64 + m : 65 + m],
-                scale=1.0,
-            )
-
-        def add_nodes(by_i):
-            ni = BLOCKS[0][1] // NODES
-            x_down_t = node_t[:, 0 : 2 * NODES].rearrange("p (t n) -> p n t", t=2)
-            t0 = 0 if by_i else 2
-            if by_i:
-                add = x_down_t[:, 0:ni, :].unsqueeze(2).to_broadcast([P, ni, NODES, 2])
-            else:
-                add = x_down_t.unsqueeze(1).to_broadcast([P, ni, NODES, 2])
-            nc.gpsimd.tensor_tensor(
-                out=s_grouped[0][:, 0, :, t0 : t0 + 2].rearrange("p (i j) t -> p i j t", j=NODES),
-                in0=node_relus[:, t0 : t0 + 2, :].rearrange("p t (i j) -> p i j t", j=NODES),
-                in1=add,
-                op=ALU.add,
             )
 
         def interleave_nodes(b):
@@ -408,12 +382,11 @@ def tile_edgeupdaterwrapper_v01_pb_kernel(
             for g in range(PASSES):
                 quantise_hid(1, g)
             for m in range(4):
-                node_relu(m)
-            add_nodes(True)
-            add_nodes(False)
-            group_wo(nc.vector.tensor_copy, 0)
+                node_chunk(0, m)
+            group_wo(0)
+            group_wo(1)
             quantise_s(0, 1)
-            group_wo(nc.scalar.copy, 1)
+            interleave_nodes(0)
             for part in range(2):
                 prepare_edge(1, part)
             for m in range(8):

@@ -123,11 +123,11 @@ def tile_edgeupdaterwrapper_v01_pb_kernel(
 
         load_w2(1, 0)
         load_hid(0)
+        load_node_inputs()
         load_hid(1)
         load_w2(1, 1)
         load_hid(2)
         load_hid(3)
-        load_node_inputs()
         load_row_vectors()
         load_p_ln(0)
         load_w2(0, 0)

@@ -28,6 +28,7 @@ BLOCKS = ((0, 512), (512, 512))
 
 BANKS_T, BANKS_S, BANKS_B = 2, 4, 2
 LN_DEPTH = 4
+ON_VECTOR = 3
 
 
 def tile_edgeupdaterwrapper_v01_pb_kernel(
@@ -287,7 +288,7 @@ def tile_edgeupdaterwrapper_v01_pb_kernel(
                 s_grouped[b][:, half, :, :].rearrange("p r t -> p (r t)"),
             )
 
-        z, u, neg_mean, scaled, rstd, shift = {}, {}, {}, {}, {}, {}
+        z, u, neg_mean, mean_part, scaled, rstd, shift = {}, {}, {}, {}, {}, {}, {}
 
         def pieces(k):
             width = ED // 2 if k == ROWS // P - 1 else ED
@@ -296,7 +297,8 @@ def tile_edgeupdaterwrapper_v01_pb_kernel(
         def second_matmul(k):
             b, a = divmod(k, 4)
             rows = slice(P * a, P * (a + 1))
-            z[k] = psum.tile([P, ED], F32, tag="t", bufs=BANKS_T, name="z")
+            tag, bufs = ("t", BANKS_T) if k < 6 else ("b", BANKS_B)
+            z[k] = psum.tile([P, ED], F32, tag=tag, bufs=bufs, name="z")
             for g in range(PASSES):
                 nc.tensor.matmul_mx(
                     out=z[k][:],
@@ -317,6 +319,10 @@ def tile_edgeupdaterwrapper_v01_pb_kernel(
             )
 
         def centre(k):
+            if k == ON_VECTOR:
+                mean_part[k] = work.tile([P, 1], F32, tag="mean_part", bufs=1, name="mean_part")
+                nc.scalar.mul(out=mean_part[k][:], in_=neg_mean[k][:], mul=1.0 / ED)
+                return
             centred = work.tile([P, ED], F32, tag="centred", bufs=LN_DEPTH, name="centred")
             nc.scalar.activation(
                 out=centred[:], in_=u[k][:], func=ACT.Identity, bias=neg_mean[k][:], scale=-float(ED)
@@ -337,6 +343,15 @@ def tile_edgeupdaterwrapper_v01_pb_kernel(
             rstd[k] = work.tile([P, 1], F32, tag="rstd", bufs=LN_DEPTH, name="rstd")
             nc.scalar.activation(
                 out=rstd[k][:], in_=sq_sum[:], func=ACT.Abs_reciprocal_sqrt, bias=eps[:], scale=1.0 / ED
+            )
+            if k == ON_VECTOR:
+                nc.scalar.mul(out=rstd[k][:], in_=rstd[k][:], mul=-float(ED))
+
+        def gain(k):
+            scaled[k] = work.tile([P, ED], F32, tag="scaled", bufs=LN_DEPTH, name="scaled")
+            nc.vector.scalar_tensor_tensor(
+                out=scaled[k][:], in0=u[k][:], scalar=mean_part[k][:], in1=gain_all[:],
+                op0=ALU.subtract, op1=ALU.mult,
             )
 
         def add_shift(k):
@@ -399,19 +414,19 @@ def tile_edgeupdaterwrapper_v01_pb_kernel(
             quantise_wo(1)
             for k in range(2):
                 second_matmul(k)
-            interleave_nodes(1)
             for k in range(2):
                 add_bo(k)
             for k in range(2):
                 centre(k)
+            interleave_nodes(1)
             add_edges(1)
             for k in range(2, 4):
                 second_matmul(k)
             for k in range(2):
                 deviation(k)
             add_bo(2)
-            quantise_s(1, 0)
             quantise_s(1, 1)
+            quantise_s(1, 0)
             add_bo(3)
             for k in range(4):
                 add_shift(k)
@@ -419,8 +434,11 @@ def tile_edgeupdaterwrapper_v01_pb_kernel(
                 if k + 2 < 8:
                     centre(k + 2)
                     deviation(k + 2)
-                if k + 4 < 8:
-                    second_matmul(k + 4)
+                if k == 0:
+                    for i in range(4, 8):
+                        second_matmul(i)
+                if k == ON_VECTOR:
+                    gain(k)
                 finish(k)
                 if k + 4 < 8:
                     add_shift(k + 4)

@@ -256,8 +256,8 @@ def tile_edgeupdaterwrapper_v01_pb_kernel(
                 op1=ALU.add,
             )
 
-        def interleave_nodes(b):
-            interleave(nc.scalar.copy, s_grouped[b][:, 0, :, :], s_planes[b][:])
+        def interleave_nodes(copy, b):
+            interleave(copy, s_grouped[b][:, 0, :, :], s_planes[b][:])
 
         def edge_chunk(b, m):
             t = m - PACK
@@ -401,7 +401,7 @@ def tile_edgeupdaterwrapper_v01_pb_kernel(
             group_wo(0)
             group_wo(1)
             quantise_s(0, 1)
-            interleave_nodes(0)
+            interleave_nodes(nc.scalar.copy, 0)
             for part in range(2):
                 prepare_edge(1, part)
             for m in range(8):
@@ -414,11 +414,11 @@ def tile_edgeupdaterwrapper_v01_pb_kernel(
             quantise_wo(1)
             for k in range(2):
                 second_matmul(k)
+            interleave_nodes(nc.vector.tensor_copy, 1)
             for k in range(2):
                 add_bo(k)
             for k in range(2):
                 centre(k)
-            interleave_nodes(1)
             add_edges(1)
             for k in range(2, 4):
                 second_matmul(k)

@@ -28,7 +28,6 @@ BLOCKS = ((0, 512), (512, 512))
 
 BANKS_T, BANKS_S, BANKS_B = 2, 4, 2
 LN_DEPTH = 4
-ON_VECTOR = 3
 
 
 def tile_edgeupdaterwrapper_v01_pb_kernel(
@@ -215,6 +214,10 @@ def tile_edgeupdaterwrapper_v01_pb_kernel(
                 in_=hid_t[:].rearrange("p g u r -> p g r u"),
             )
 
+        def keep_clock():
+            idle = psum.tile([P, P], F32, tag="s", bufs=BANKS_S, name="idle")
+            nc.tensor.matmul(idle[:], lhsT=ident_f32[:], rhs=ident_f32[:], start=True, stop=True)
+
         def quantise_hid(b, g):
             quantise(
                 hid_words[b][:, g, :],
@@ -288,7 +291,7 @@ def tile_edgeupdaterwrapper_v01_pb_kernel(
                 s_grouped[b][:, half, :, :].rearrange("p r t -> p (r t)"),
             )
 
-        z, u, neg_mean, mean_part, scaled, rstd, shift = {}, {}, {}, {}, {}, {}, {}
+        z, u, neg_mean, scaled, rstd, shift = {}, {}, {}, {}, {}, {}
 
         def pieces(k):
             width = ED // 2 if k == ROWS // P - 1 else ED
@@ -319,10 +322,6 @@ def tile_edgeupdaterwrapper_v01_pb_kernel(
             )
 
         def centre(k):
-            if k == ON_VECTOR:
-                mean_part[k] = work.tile([P, 1], F32, tag="mean_part", bufs=1, name="mean_part")
-                nc.scalar.mul(out=mean_part[k][:], in_=neg_mean[k][:], mul=1.0 / ED)
-                return
             centred = work.tile([P, ED], F32, tag="centred", bufs=LN_DEPTH, name="centred")
             nc.scalar.activation(
                 out=centred[:], in_=u[k][:], func=ACT.Identity, bias=neg_mean[k][:], scale=-float(ED)
@@ -344,15 +343,6 @@ def tile_edgeupdaterwrapper_v01_pb_kernel(
             nc.scalar.activation(
                 out=rstd[k][:], in_=sq_sum[:], func=ACT.Abs_reciprocal_sqrt, bias=eps[:], scale=1.0 / ED
             )
-            if k == ON_VECTOR:
-                nc.scalar.mul(out=rstd[k][:], in_=rstd[k][:], mul=-float(ED))
-
-        def gain(k):
-            scaled[k] = work.tile([P, ED], F32, tag="scaled", bufs=LN_DEPTH, name="scaled")
-            nc.vector.scalar_tensor_tensor(
-                out=scaled[k][:], in0=u[k][:], scalar=mean_part[k][:], in1=gain_all[:],
-                op0=ALU.subtract, op1=ALU.mult,
-            )
 
         def add_shift(k):
             shift[k] = psum.tile([P, ED], F32, tag="s", bufs=BANKS_S, name="shift")
@@ -362,7 +352,7 @@ def tile_edgeupdaterwrapper_v01_pb_kernel(
             nc.tensor.matmul(shift[k][:], lhsT=ones[:], rhs=vec_raw[:, 2, :], start=False, stop=True)
 
         def finish(k):
-            res = work.tile([P, ED], F32, tag="res", bufs=LN_DEPTH, name="res")
+            res = work.tile([P, ED], F32, tag="res", bufs=ROWS // P, name="res")
             for cols in pieces(k):
                 nc.vector.scalar_tensor_tensor(
                     out=res[:, cols], in0=scaled[k][:, cols], scalar=rstd[k][:], in1=shift[k][:, cols],
@@ -377,8 +367,10 @@ def tile_edgeupdaterwrapper_v01_pb_kernel(
             prepare_hid(0, 1)
             group_w2(1, 1)
             prepare_hid(0, 2)
+            keep_clock()
             quantise_w2(1, 1)
             prepare_hid(0, 3)
+            keep_clock()
             prepare_small_inputs()
             prepare_row_vectors()
             for g in range(PASSES):
@@ -393,6 +385,8 @@ def tile_edgeupdaterwrapper_v01_pb_kernel(
             quantise_w2(0, 1)
             for a in range(4):
                 prepare_hid(1, a)
+                if a in (1, 2):
+                    keep_clock()
             add_edges(0)
             for g in range(PASSES):
                 quantise_hid(1, g)
@@ -437,8 +431,6 @@ def tile_edgeupdaterwrapper_v01_pb_kernel(
                 if k == 0:
                     for i in range(4, 8):
                         second_matmul(i)
-                if k == ON_VECTOR:
-                    gain(k)
                 finish(k)
                 if k + 4 < 8:
                     add_shift(k + 4)

from contextlib import ExitStack

import concourse.mybir as mybir
from concourse.masks import make_identity

F32 = mybir.dt.float32
BF16 = mybir.dt.bfloat16
U32 = mybir.dt.uint32
U8 = mybir.dt.uint8
FP8X4 = mybir.dt.float8_e4m3fn_x4
ALU = mybir.AluOpType
ACT = mybir.ActivationFunctionType

P = 128
PACK = 4
K_PASS = P * PACK
NODES = 32
ROWS = NODES * NODES
F = 1024
MD = 1024
ED = 512
PASSES = 2
PLN_LOAD = 512
EPS = 1e-5
FLOPS = 2 * ROWS * F * MD + 2 * ROWS * MD * ED

BLOCKS = ((0, 512), (512, 512))

BANKS_T, BANKS_S, BANKS_B = 2, 4, 2
LN_DEPTH = 4


def tile_edgeupdaterwrapper_v01_pb_kernel(
    tc, hid, x_down, p_ln, W2, b2, Wo, bo, ln_out_g, ln_out_b, out
):
    nc = tc.nc
    hid_rows = hid.rearrange("b i j k -> (b i j) k")
    pln_rows = p_ln.rearrange("b i j f -> (b i j) f")
    out_rows = out.rearrange("b i j f -> (b i j) f")
    xd_rows = x_down.rearrange("b n f -> (b n) f")

    with ExitStack() as ctx:
        keep = ctx.enter_context(tc.tile_pool(name="keep", bufs=1))
        work = ctx.enter_context(tc.tile_pool(name="work", bufs=1))
        psum = ctx.enter_context(tc.psum_pool(name="psum", bufs=1))

        hid_raw = keep.tile([P, ROWS // P, F], BF16)
        w2_raw = keep.tile([P, 2, PASSES, PACK, K_PASS], BF16)
        wo_raw = keep.tile([P, PASSES, PACK, ED], BF16)
        pln_raw = keep.tile([P, ROWS // P, ED], BF16)
        node_raw = keep.tile([P, P], BF16)
        vec_raw = keep.tile([P, 3, ED], BF16)
        w2_grouped = keep.tile([P, 2, PASSES, K_PASS, PACK], BF16, align_bytes=64)
        w2_words = keep.tile([P, 2, PASSES, K_PASS], U32, align_bytes=64)
        w2_scales = keep.tile([P, 2, PASSES, K_PASS], U8, align_bytes=64)
        wo_grouped = keep.tile([P, PASSES, ED, PACK], BF16, align_bytes=64)
        wo_words = keep.tile([P, PASSES, ED], U32, align_bytes=64)
        wo_scales = keep.tile([P, PASSES, ED], U8, align_bytes=64)
        node_add = keep.tile([P, PACK, NODES], F32)
        node_t = keep.tile([P, 72], F32)
        neg_b2 = keep.tile([P, PACK], F32)
        ones = keep.tile([P, P], BF16)
        ident_f32 = keep.tile([P, P], F32)
        ident_bf16 = keep.tile([P, P], BF16)
        eps = keep.tile([P, 1], F32)
        table_warm = keep.tile([P, 1], F32)
        bo_all = keep.tile([P, ED], F32)
        gain_all = keep.tile([P, ED], F32)

        def interleave(copy, dst, src):
            copy(
                out=dst.rearrange("p (c i) t -> p c t i", i=4),
                in_=src.rearrange("p t (c i) -> p c t i", i=4),
            )

        def quantise(words, scales, grouped):
            nc.vector.quantize_mx(out=words.bitcast(FP8X4), scales=scales, in_=grouped)

        nc.vector.memset(node_raw[:], 0.0)
        nc.vector.memset(vec_raw[:], 0.0)
        nc.vector.memset(ones[:], 1.0)
        nc.vector.memset(eps[:], EPS)
        make_identity(nc, ident_f32[:])
        make_identity(nc, ident_bf16[:])
        nc.scalar.activation(out=table_warm[:], in_=eps[:], func=ACT.Abs_reciprocal_sqrt)

        def load_w2(half, g):
            for u in range(2):
                k0 = K_PASS * g + 256 * u
                nc.sync.dma_start(
                    out=w2_raw[:, half, g, 2 * u : 2 * u + 2, :],
                    in_=W2[k0 : k0 + 256, K_PASS * half : K_PASS * (half + 1)].rearrange(
                        "(q e) n -> q e n", e=2
                    ),
                )

        def load_hid(a):
            nc.sync.dma_start(out=hid_raw[:, a, :], in_=hid_rows[P * a : P * (a + 1), :])

        def load_node_inputs():
            nc.sync.dma_start(out=node_raw[0:32, :], in_=xd_rows[:, 0:P])
            nc.sync.dma_start(out=node_raw[32:64, :], in_=xd_rows[:, P : 2 * P])
            nc.sync.dma_start(out=node_raw[64:72, :], in_=b2.rearrange("(m p) -> m p", p=P))

        def load_p_ln(part):
            tiles = PLN_LOAD // P
            nc.sync.dma_start(
                out=pln_raw[:, tiles * part : tiles * (part + 1), :],
                in_=pln_rows[PLN_LOAD * part : PLN_LOAD * (part + 1), :].rearrange(
                    "(a p) f -> p a f", p=P
                ),
            )

        def load_row_vectors():
            for c, vec in enumerate((bo, ln_out_g, ln_out_b)):
                nc.sync.dma_start(out=vec_raw[0:1, c, :], in_=vec.rearrange("(o f) -> o f", o=1))

        def load_wo(g):
            nc.sync.dma_start(
                out=wo_raw[:, g, :, :],
                in_=Wo[K_PASS * g : K_PASS * (g + 1), :].rearrange("(t p) n -> p t n", p=P),
            )

        load_w2(1, 0)
        load_hid(0)
        load_node_inputs()
        load_hid(1)
        load_w2(1, 1)
        load_hid(2)
        load_hid(3)
        load_row_vectors()
        load_p_ln(0)
        load_w2(0, 0)
        load_w2(0, 1)
        load_hid(4)
        load_hid(5)
        load_hid(6)
        load_hid(7)
        load_wo(0)
        load_p_ln(1)
        load_wo(1)

        def group_w2(half, g):
            interleave(nc.vector.tensor_copy, w2_grouped[:, half, g, :, :], w2_raw[:, half, g, :, :])

        def quantise_w2(half, g):
            quantise(
                w2_words[:, half, g, :],
                w2_scales[:, half, g, :],
                w2_grouped[:, half, g, :, :].rearrange("p n t -> p (n t)"),
            )

        def group_wo(g):
            interleave(nc.scalar.copy, wo_grouped[:, g, :, :], wo_raw[:, g, :, :])

        def quantise_wo(g):
            quantise(
                wo_words[:, g, :], wo_scales[:, g, :], wo_grouped[:, g, :, :].rearrange("p n t -> p (n t)")
            )

        def prepare_small_inputs():
            node_ps = psum.tile([P, P], BF16, tag="t", bufs=BANKS_T, name="node_ps")
            nc.tensor.transpose(node_ps[:], node_raw[:], ident_bf16[:])
            nc.scalar.copy(out=node_t[:], in_=node_ps[:, 0:72])
            nc.gpsimd.tensor_scalar_mul(neg_b2[:], node_t[:, 64:68], -1.0)
            for m in range(PACK):
                x0 = NODES * (m % 2)
                nc.gpsimd.tensor_scalar_add(
                    out=node_add[:, m, :],
                    in0=node_t[:, x0 : x0 + NODES],
                    scalar1=node_t[:, 64 + m : 65 + m],
                )
        def prepare_row_vectors():
            for c, dst, factor in ((0, bo_all, -1.0 / ED), (1, gain_all, 1.0)):
                spread = psum.tile([P, ED], F32, tag="t", bufs=BANKS_T, name="spread")
                nc.tensor.matmul(spread[:], lhsT=ones[:], rhs=vec_raw[:, c, :], start=True, stop=True)
                nc.scalar.mul(out=dst[:], in_=spread[:], mul=factor)

        def prepare_edge(b, part):
            pln_t = psum.tile([P, PACK, 256], BF16, tag="b", bufs=BANKS_B, name="pln_t")
            for t in range(PACK):
                for a in range(2):
                    nc.tensor.transpose(
                        pln_t[:, t, P * a : P * (a + 1)],
                        pln_raw[:, BLOCKS[b][0] // P + 2 * part + a, P * t : P * (t + 1)],
                        ident_bf16[:],
                    )
            edge_t[b, part] = pln_t

        hid_grouped, hid_words, hid_scales = {}, {}, {}
        edge_t = {}
        s_planes, relu, s_grouped, s_words, s_scales = {}, {}, {}, {}, {}
        for b, (first, n) in enumerate(BLOCKS):
            s_planes[b] = keep.tile([P, PACK, n], BF16, name="s_planes%d" % b)
            relu[b] = keep.tile([P, n // 4, PACK, 4], F32, name="relu%d" % b)
            s_grouped[b] = keep.tile([P, PASSES, n, PACK], BF16, align_bytes=64, name="s_grouped%d" % b)
            s_words[b] = keep.tile([P, PASSES, n], U32, align_bytes=64, name="s_words%d" % b)
            s_scales[b] = keep.tile([P, PASSES, n], U8, align_bytes=64, name="s_scales%d" % b)

        for b, (first, n) in enumerate(BLOCKS):
            hid_grouped[b] = keep.tile([P, PASSES, n, 2], F32, align_bytes=64, name="hid_grouped%d" % b)
            hid_words[b] = keep.tile([P, PASSES, n], U32, align_bytes=64, name="hid_words%d" % b)
            hid_scales[b] = keep.tile([P, PASSES, n], U8, align_bytes=64, name="hid_scales%d" % b)

        def prepare_hid(b, a):
            hid_t = psum.tile([P, PASSES, 2, P], F32, tag="t", bufs=BANKS_T, name="hid_t")
            pairs_of_k = hid_raw[:, BLOCKS[b][0] // P + a, :].bitcast(F32)
            for g in range(PASSES):
                for u in range(2):
                    w0 = 256 * g + P * u
                    nc.tensor.transpose(hid_t[:, g, u, :], pairs_of_k[:, w0 : w0 + P], ident_f32[:])
            nc.scalar.copy(
                out=hid_grouped[b][:, :, P * a : P * (a + 1), :],
                in_=hid_t[:].rearrange("p g u r -> p g r u"),
            )

        def keep_clock():
            idle = psum.tile([P, P], F32, tag="s", bufs=BANKS_S, name="idle")
            nc.tensor.matmul(idle[:], lhsT=ident_f32[:], rhs=ident_f32[:], start=True, stop=True)

        def quantise_hid(b, g):
            quantise(
                hid_words[b][:, g, :],
                hid_scales[b][:, g, :],
                hid_grouped[b][:, g, :, :].bitcast(BF16).rearrange("p r t -> p (r t)"),
            )

        def first_matmul(b, m):
            n = BLOCKS[b][1]
            half, t = divmod(m, PACK)
            x = psum.tile([P, n], F32, tag="s", bufs=BANKS_S, name="x")
            cols = slice(P * t, P * (t + 1))
            for g in range(PASSES):
                nc.tensor.matmul_mx(
                    out=x[:],
                    lhsT=w2_words[:, half, g, cols].bitcast(FP8X4),
                    lhsT_scale=w2_scales[:, half, g, cols],
                    rhs=hid_words[b][:, g, :].bitcast(FP8X4),
                    rhs_scale=hid_scales[b][:, g, :],
                    start=(g == 0),
                    stop=(g == PASSES - 1),
                )
            return x

        def node_chunk(b, m):
            first, n = BLOCKS[b]
            i0, ni = first // NODES, n // NODES
            x = first_matmul(b, m)
            if m < 2:
                add = node_add[:, m, i0 : i0 + ni].unsqueeze(2).to_broadcast([P, ni, NODES])
            else:
                add = node_add[:, m, :].unsqueeze(1).to_broadcast([P, ni, NODES])
            nc.vector.scalar_tensor_tensor(
                out=s_planes[b][:, m, :].rearrange("p (i j) -> p i j", j=NODES),
                in0=x[:].rearrange("p (i j) -> p i j", j=NODES),
                scalar=neg_b2[:, m : m + 1],
                in1=add,
                op0=ALU.max,
                op1=ALU.add,
            )

        def interleave_nodes(copy, b):
            interleave(copy, s_grouped[b][:, 0, :, :], s_planes[b][:])

        def edge_chunk(b, m):
            t = m - PACK
            x = first_matmul(b, m)
            nc.scalar.activation(
                out=relu[b][:, :, t, :],
                in_=x[:].rearrange("p (c i) -> p c i", i=4),
                func=ACT.Relu,
                bias=node_t[:, 64 + m : 65 + m],
                scale=1.0,
            )

        def add_edges(b):
            for part in range(BLOCKS[b][1] // 256):
                nc.vector.tensor_tensor(
                    out=s_grouped[b][:, 1, 256 * part : 256 * (part + 1), :].rearrange(
                        "p (c i) t -> p c i t", i=4
                    ),
                    in0=edge_t[b, part][:].rearrange("p t (c i) -> p c i t", i=4),
                    in1=relu[b][:, 64 * part : 64 * (part + 1), :, :].rearrange("p c t i -> p c i t"),
                    op=ALU.add,
                )

        def quantise_s(b, half):
            quantise(
                s_words[b][:, half, :],
                s_scales[b][:, half, :],
                s_grouped[b][:, half, :, :].rearrange("p r t -> p (r t)"),
            )

        z, u, neg_mean, scaled, rstd, shift = {}, {}, {}, {}, {}, {}

        def pieces(k):
            width = ED // 2 if k == ROWS // P - 1 else ED
            return [slice(f, f + width) for f in range(0, ED, width)]

        def second_matmul(k):
            b, a = divmod(k, 4)
            rows = slice(P * a, P * (a + 1))
            tag, bufs = ("t", BANKS_T) if k < 6 else ("b", BANKS_B)
            z[k] = psum.tile([P, ED], F32, tag=tag, bufs=bufs, name="z")
            for g in range(PASSES):
                nc.tensor.matmul_mx(
                    out=z[k][:],
                    lhsT=s_words[b][:, g, rows].bitcast(FP8X4),
                    lhsT_scale=s_scales[b][:, g, rows],
                    rhs=wo_words[:, g, :].bitcast(FP8X4),
                    rhs_scale=wo_scales[:, g, :],
                    start=(g == 0),
                    stop=(g == PASSES - 1),
                )

        def add_bo(k):
            u[k] = work.tile([P, ED], F32, tag="u", bufs=LN_DEPTH, name="u")
            neg_mean[k] = work.tile([P, 1], F32, tag="neg_mean", bufs=LN_DEPTH, name="neg_mean")
            nc.vector.scalar_tensor_tensor(
                out=u[k][:], in0=z[k][:], scalar=-1.0 / ED, in1=bo_all[:], op0=ALU.mult, op1=ALU.add,
                accum_out=neg_mean[k][:],
            )

        def centre(k):
            centred = work.tile([P, ED], F32, tag="centred", bufs=LN_DEPTH, name="centred")
            nc.scalar.activation(
                out=centred[:], in_=u[k][:], func=ACT.Identity, bias=neg_mean[k][:], scale=-float(ED)
            )
            scaled[k] = work.tile([P, ED], F32, tag="scaled", bufs=LN_DEPTH, name="scaled")
            for cols in pieces(k):
                nc.gpsimd.tensor_tensor(
                    out=scaled[k][:, cols], in0=centred[:, cols], in1=gain_all[:, cols], op=ALU.mult
                )

        def deviation(k):
            squares = work.tile([P, ED], BF16, tag="squares", bufs=2, name="squares")
            sq_sum = work.tile([P, 1], F32, tag="sq_sum", bufs=LN_DEPTH, name="sq_sum")
            nc.scalar.activation(
                out=squares[:], in_=u[k][:], func=ACT.Square, bias=neg_mean[k][:], scale=-float(ED),
                accum_out=sq_sum[:],
            )
            rstd[k] = work.tile([P, 1], F32, tag="rstd", bufs=LN_DEPTH, name="rstd")
            nc.scalar.activation(
                out=rstd[k][:], in_=sq_sum[:], func=ACT.Abs_reciprocal_sqrt, bias=eps[:], scale=1.0 / ED
            )

        def add_shift(k):
            shift[k] = psum.tile([P, ED], F32, tag="s", bufs=BANKS_S, name="shift")
            nc.tensor.matmul(
                shift[k][:], lhsT=ident_bf16[:], rhs=pln_raw[:, k, :], start=True, stop=False
            )
            nc.tensor.matmul(shift[k][:], lhsT=ones[:], rhs=vec_raw[:, 2, :], start=False, stop=True)

        def finish(k):
            res = work.tile([P, ED], F32, tag="res", bufs=ROWS // P, name="res")
            for cols in pieces(k):
                nc.vector.scalar_tensor_tensor(
                    out=res[:, cols], in0=scaled[k][:, cols], scalar=rstd[k][:], in1=shift[k][:, cols],
                    op0=ALU.mult, op1=ALU.add,
                )
                nc.sync.dma_start(out=out_rows[P * k : P * (k + 1), cols], in_=res[:, cols])

        with tc.manual_schedule():
            group_w2(1, 0)
            quantise_w2(1, 0)
            prepare_hid(0, 0)
            prepare_hid(0, 1)
            group_w2(1, 1)
            prepare_hid(0, 2)
            keep_clock()
            quantise_w2(1, 1)
            prepare_hid(0, 3)
            keep_clock()
            prepare_small_inputs()
            prepare_row_vectors()
            for g in range(PASSES):
                quantise_hid(0, g)
            prepare_edge(0, 0)
            group_w2(0, 0)
            for m in range(4, 8):
                edge_chunk(0, m)
            prepare_edge(0, 1)
            group_w2(0, 1)
            quantise_w2(0, 0)
            quantise_w2(0, 1)
            for a in range(4):
                prepare_hid(1, a)
                if a in (1, 2):
                    keep_clock()
            add_edges(0)
            for g in range(PASSES):
                quantise_hid(1, g)
            for m in range(4):
                node_chunk(0, m)
            group_wo(0)
            group_wo(1)
            quantise_s(0, 1)
            interleave_nodes(nc.scalar.copy, 0)
            for part in range(2):
                prepare_edge(1, part)
            for m in range(8):
                if m < 4:
                    node_chunk(1, m)
                else:
                    edge_chunk(1, m)
            quantise_wo(0)
            quantise_s(0, 0)
            quantise_wo(1)
            for k in range(2):
                second_matmul(k)
            interleave_nodes(nc.vector.tensor_copy, 1)
            for k in range(2):
                add_bo(k)
            for k in range(2):
                centre(k)
            add_edges(1)
            for k in range(2, 4):
                second_matmul(k)
            for k in range(2):
                deviation(k)
            add_bo(2)
            quantise_s(1, 1)
            quantise_s(1, 0)
            add_bo(3)
            for k in range(4):
                add_shift(k)
            for k in range(8):
                if k + 2 < 8:
                    centre(k + 2)
                    deviation(k + 2)
                if k == 0:
                    for i in range(4, 8):
                        second_matmul(i)
                finish(k)
                if k + 4 < 8:
                    add_shift(k + 4)
                    add_bo(k + 4)
